import numpy as np
import ml_dtypes


def mxq(x, axis, fmt="e4m3"):
    dtype, down = {"e4m3": (ml_dtypes.float8_e4m3fn, 7), "e5m2": (ml_dtypes.float8_e5m2, 14)}[fmt]
    v = np.moveaxis(np.asarray(x, np.float32).astype(ml_dtypes.bfloat16).astype(np.float64), axis, -1)
    blocks = v.reshape(v.shape[:-1] + (-1, 32))
    amax = np.abs(blocks).max(-1, keepdims=True)
    byte = np.maximum(np.where(amax > 0, np.frexp(amax)[1] - 1 + 127, 0) - down, 1)
    scale = np.exp2(byte - 127.0)
    codes = (blocks / scale).astype(np.float32).astype(dtype).astype(np.float64)
    return np.moveaxis((codes * scale).reshape(v.shape), -1, axis)


WIDE = False


def mx_kscale(k):
    if not WIDE:
        return np.ones(k)
    levels = np.array([10, -10, 5, -5, 0])
    a = np.random.permutation(np.resize(levels, k // 512 * 4)).reshape(k // 512, 4)
    idx = np.arange(k)
    return np.exp2(a[idx // 512, idx % 128 // 32])


BF16 = ml_dtypes.bfloat16


def bf(x):
    return np.asarray(x, np.float32).astype(BF16)


def f64(x):
    return np.asarray(x).astype(np.float64)


B, N, F, C0, C1, E, G = 2, 512, 2048, 2048, 1024, 2, 4
EPS_BN = 1e-5
SLOPE = 0.01
R = B * N
CG = (E + 1) * F // G
OG = C0 // G


def bn_train(y, gamma, beta):
    mean = y.mean(axis=(0, 1), keepdims=True)
    var = y.var(axis=(0, 1), keepdims=True)
    return (y - mean) / np.sqrt(var + EPS_BN) * gamma + beta


def leaky(v):
    return np.where(v >= 0.0, v, SLOPE * v)


def setup_inputs():
    s = mx_kscale(CG)
    sx = np.tile(s, G)
    t = mx_kscale(C0)
    return {"node_feat": bf(np.random.standard_normal((B, N, F)) * 5.0 * sx[:F]),
            "aggr": bf(np.random.standard_normal((B, N, E * F)) * 6.0 / np.sqrt(N) * sx[F:]),
            "w0": bf(np.random.standard_normal((C0, CG)) / np.sqrt(CG) / s),
            "gamma0": bf((1.0 + 0.1 * np.random.standard_normal(C0)) * t),
            "beta0": bf(0.1 * np.random.standard_normal(C0) * t),
            "w1": bf(np.random.standard_normal((C1, C0)) / np.sqrt(C0) / t),
            "gamma1": bf(1.0 + 0.1 * np.random.standard_normal(C1)),
            "beta1": bf(0.1 * np.random.standard_normal(C1))}


def reference(node_feat, aggr, w0, gamma0, beta0, w1, gamma1, beta1):
    x = np.concatenate([f64(node_feat), f64(aggr)], axis=-1)
    xg = x.reshape(R, G, CG).transpose(1, 0, 2)
    wg = f64(w0).reshape(G, OG, CG).transpose(0, 2, 1)
    y0 = mxq(xg, 2, "e4m3") @ mxq(wg, 1, "e4m3")
    y0 = y0.transpose(1, 0, 2).reshape(B, N, C0)
    h = leaky(bn_train(y0, f64(gamma0), f64(beta0)))
    y1 = (mxq(h.reshape(R, C0), 1, "e4m3") @ mxq(f64(w1).T, 0, "e4m3")).reshape(B, N, C1)
    return leaky(bn_train(y1, f64(gamma1), f64(beta1)))

@@ -1,0 +1,264 @@
+from contextlib import ExitStack
+
+import concourse.mybir as mybir
+from concourse.masks import make_identity
+
+F32 = mybir.dt.float32
+BF16 = mybir.dt.bfloat16
+U32 = mybir.dt.uint32
+U8 = mybir.dt.uint8
+FP8X4 = mybir.dt.float8_e4m3fn_x4
+ALU = mybir.AluOpType
+ACT = mybir.ActivationFunctionType
+
+P = 128
+ROWS = 1024
+NODE_K = 2048
+GROUPS = 4
+GROUP_K = 1536
+GROUP_PASSES = 3
+HIDDEN = 2048
+HIDDEN_PASSES = 4
+OUT_CH = 1024
+TILES_PER_GROUP = 4
+HIDDEN_TILES = 16
+OUT_TILES = 8
+PASS_WORDS = 256
+BANK = 512
+PAIR = 256
+EPS_BN = 1e-5
+SLOPE = 0.01
+
+FLOPS = 2 * ROWS * GROUPS * GROUP_K * 512 + 2 * ROWS * HIDDEN * OUT_CH
+
+
+def tile_nodeupdatenetwork_pb_kernel(
+    tc, node_feat, aggr, w0, gamma0, beta0, w1, gamma1, beta1, out
+):
+    nc = tc.nc
+    node_rows = node_feat.flatten_outer_dims()
+    aggr_rows = aggr.flatten_outer_dims()
+    out_rows = out.flatten_outer_dims()
+
+    with ExitStack() as whole:
+        const = whole.enter_context(tc.tile_pool(name="const", bufs=1))
+        small = whole.enter_context(tc.tile_pool(name="small", bufs=4))
+        kept = whole.enter_context(tc.tile_pool(name="kept", bufs=1))
+        tbanks = whole.enter_context(tc.psum_pool(name="tbanks", bufs=4))
+        sums = whole.enter_context(tc.psum_pool(name="sums", bufs=4))
+
+        vec_rows = const.tile([P, 2 * P], BF16)
+        nc.vector.memset(vec_rows[:], 0.0)
+        nc.scalar.dma_start(out=vec_rows[0:8, :], in_=gamma0.rearrange("(a w) -> a w", w=2 * P))
+        nc.scalar.dma_start(out=vec_rows[8:12, :], in_=gamma1.rearrange("(a w) -> a w", w=2 * P))
+        nc.scalar.dma_start(out=vec_rows[12:20, :], in_=beta0.rearrange("(a w) -> a w", w=2 * P))
+        nc.scalar.dma_start(out=vec_rows[20:24, :], in_=beta1.rearrange("(a w) -> a w", w=2 * P))
+
+        ident = const.tile([P, P], F32)
+        make_identity(nc, ident[:])
+        eps = const.tile([P, 1], F32)
+        nc.vector.memset(eps[:], EPS_BN)
+        warm = const.tile([P, 1], F32)
+        nc.scalar.activation(out=warm[:], in_=eps[:], func=ACT.Sqrt)
+
+        w1_codes = kept.tile([P, HIDDEN_PASSES, OUT_CH], U32, align_bytes=64)
+        w1_scales = kept.tile([P, HIDDEN_PASSES, OUT_CH], U8, align_bytes=64)
+        h_codes = kept.tile([P, HIDDEN_PASSES, ROWS], U32, align_bytes=64)
+        h_scales = kept.tile([P, HIDDEN_PASSES, ROWS], U8, align_bytes=64)
+
+        def scale_and_bias(stats, tile_index):
+            mean_var = small.tile([P, 2], F32)
+            nc.vector.bn_aggr(out=mean_var[:], in_=stats[:].rearrange("p h s -> p (h s)"))
+            std = small.tile([P, 1], F32)
+            nc.scalar.activation(out=std[:], in_=mean_var[:, 1:2], func=ACT.Sqrt, bias=eps[:, 0:1])
+            rstd = small.tile([P, 1], F32)
+            nc.vector.reciprocal(out=rstd[:], in_=std[:])
+            scale_pm = small.tile([P, 2], F32)
+            nc.vector.tensor_scalar(
+                out=scale_pm[:], in0=gain_pm[:, tile_index, :], scalar1=rstd[:, 0:1], scalar2=None,
+                op0=ALU.mult,
+            )
+            bias = small.tile([P, 1], F32)
+            nc.vector.tensor_scalar(
+                out=bias[:], in0=mean_var[:, 0:1], scalar1=scale_pm[:, 1:2],
+                scalar2=shift[:, tile_index : tile_index + 1], op0=ALU.mult, op1=ALU.add,
+            )
+            return scale_pm, bias
+
+        def multiply_and_normalise(w_codes, w_scales, a_codes, a_scales, passes, w_tile, tile_index, dest):
+            w_cols = slice(P * w_tile, P * (w_tile + 1))
+            stats = small.tile([P, 2, 6], F32)
+            banks = []
+            for half in range(2):
+                r_cols = slice(BANK * half, BANK * (half + 1))
+                acc = sums.tile([P, BANK], F32)
+                for c in range(passes):
+                    nc.tensor.matmul_mx(
+                        out=acc[:],
+                        lhsT=w_codes[:, c, w_cols].bitcast(FP8X4),
+                        lhsT_scale=w_scales[:, c, w_cols],
+                        rhs=a_codes[:, c, r_cols].bitcast(FP8X4),
+                        rhs_scale=a_scales[:, c, r_cols],
+                        start=(c == 0),
+                        stop=(c == passes - 1),
+                    )
+                nc.vector.bn_stats(out=stats[:, half, :], in_=acc[:])
+                banks.append(acc)
+            scale_pm, bias = scale_and_bias(stats, tile_index)
+            for half in range(2):
+                nc.scalar.activation(
+                    out=dest[:, BANK * half : BANK * (half + 1)], in_=banks[half][:],
+                    func=ACT.Identity, scale=scale_pm[:, 0:1], bias=bias[:, 0:1],
+                )
+
+        with ExitStack() as first:
+            raw = first.enter_context(tc.tile_pool(name="raw", bufs=9))
+            raw_w1 = first.enter_context(tc.tile_pool(name="raw_w1", bufs=4))
+            staged = first.enter_context(tc.tile_pool(name="staged", bufs=2))
+            regroup = first.enter_context(tc.tile_pool(name="regroup", bufs=6))
+            normed = first.enter_context(tc.tile_pool(name="normed", bufs=1))
+
+            def load_stage(stage):
+                pairs = []
+                if stage == GROUPS:
+                    for a in range(OUT_TILES // 2):
+                        w1_pair = raw_w1.tile([P, 2, HIDDEN], BF16)
+                        nc.sync.dma_start(
+                            out=w1_pair[:],
+                            in_=w1[PAIR * a : PAIR * (a + 1), :].rearrange("(p e) k -> p e k", e=2),
+                        )
+                        pairs.append((w1_pair, w1_codes, w1_scales, PAIR * a))
+                    return pairs, HIDDEN_PASSES, None
+                w0_codes = staged.tile([P, GROUP_PASSES, 512], U32, align_bytes=64)
+                w0_scales = staged.tile([P, GROUP_PASSES, 512], U8, align_bytes=64)
+                x_codes = staged.tile([P, GROUP_PASSES, ROWS], U32, align_bytes=64)
+                x_scales = staged.tile([P, GROUP_PASSES, ROWS], U8, align_bytes=64)
+                for a in range(TILES_PER_GROUP // 2):
+                    first_row = 512 * stage + PAIR * a
+                    w0_pair = raw.tile([P, 2, GROUP_K], BF16, tag="pair")
+                    nc.sync.dma_start(
+                        out=w0_pair[:],
+                        in_=w0[first_row : first_row + PAIR, :].rearrange("(p e) k -> p e k", e=2),
+                    )
+                    pairs.append((w0_pair, w0_codes, w0_scales, PAIR * a))
+                k0 = GROUP_K * stage
+                from_node = max(0, min(NODE_K - k0, GROUP_K))
+                for j in range(ROWS // PAIR):
+                    rows = slice(PAIR * j, PAIR * (j + 1))
+                    x_pair = raw.tile([P, 2, GROUP_K], BF16, tag="pair")
+                    if from_node > 0:
+                        nc.sync.dma_start(
+                            out=x_pair[:, :, 0:from_node],
+                            in_=node_rows[rows, k0 : k0 + from_node].rearrange("(i p) k -> p i k", p=P),
+                        )
+                    if from_node < GROUP_K:
+                        nc.sync.dma_start(
+                            out=x_pair[:, :, from_node:GROUP_K],
+                            in_=aggr_rows[rows, k0 + from_node - NODE_K : k0 + GROUP_K - NODE_K].rearrange(
+                                "(i p) k -> p i k", p=P
+                            ),
+                        )
+                    pairs.append((x_pair, x_codes, x_scales, PAIR * j))
+                return pairs, GROUP_PASSES, (w0_codes, w0_scales, x_codes, x_scales)
+
+            def transpose_and_quantise(pair, c):
+                raw_pair, codes, scales, col0 = pair
+                bank = tbanks.tile([P, 2, PAIR], F32, tag="bank")
+                for j in range(2):
+                    words = raw_pair[:, j, :].bitcast(F32)
+                    for u in range(2):
+                        first_word = PASS_WORDS * c + P * u
+                        nc.tensor.transpose(
+                            bank[:, u, P * j : P * (j + 1)], words[:, first_word : first_word + P], ident[:]
+                        )
+                grouped = regroup.tile([P, 4 * PAIR], BF16, align_bytes=64)
+                nc.scalar.copy(
+                    out=grouped[:].bitcast(F32).rearrange("p (n u) -> p n u", u=2),
+                    in_=bank[:].rearrange("p u n -> p n u"),
+                )
+                nc.vector.quantize_mx(
+                    out=codes[:, c, col0 : col0 + PAIR].bitcast(FP8X4),
+                    scales=scales[:, c, col0 : col0 + PAIR],
+                    in_=grouped[:],
+                )
+
+            pairs, passes, operands = load_stage(0)
+            loaded = load_stage(1)
+            for pair in pairs:
+                for c in range(passes):
+                    transpose_and_quantise(pair, c)
+
+            vec_bank = tbanks.tile([P, BANK], F32, tag="bank")
+            nc.tensor.transpose(vec_bank[:, 0:P], vec_rows[:].bitcast(F32), ident[:])
+            vec_cols = const.tile([P, 2 * P], BF16)
+            nc.vector.tensor_copy(out=vec_cols[:].bitcast(F32), in_=vec_bank[:, 0:P])
+            n_tiles = HIDDEN_TILES + OUT_TILES
+            gain_pm = const.tile([P, n_tiles, 2], F32)
+            nc.vector.tensor_copy(out=gain_pm[:, :, 0], in_=vec_cols[:, 0:n_tiles])
+            nc.vector.tensor_scalar(
+                out=gain_pm[:, :, 1], in0=vec_cols[:, 0:n_tiles], scalar1=-1.0, scalar2=None, op0=ALU.mult
+            )
+            shift = const.tile([P, n_tiles], F32)
+            nc.vector.tensor_copy(out=shift[:], in_=vec_cols[:, n_tiles : 2 * n_tiles])
+
+            for group in range(GROUPS):
+                w0_codes, w0_scales, x_codes, x_scales = operands
+                pairs, passes, operands = loaded
+                if group + 2 <= GROUPS:
+                    loaded = load_stage(group + 2)
+                units = [(pair, c) for pair in pairs for c in range(passes)]
+                v = normed.tile([P, TILES_PER_GROUP, ROWS], F32)
+                for t in range(TILES_PER_GROUP):
+                    quarter = slice(len(units) * t // TILES_PER_GROUP, len(units) * (t + 1) // TILES_PER_GROUP)
+                    for pair, c in units[quarter]:
+                        transpose_and_quantise(pair, c)
+                    multiply_and_normalise(
+                        w0_codes, w0_scales, x_codes, x_scales, GROUP_PASSES, t,
+                        TILES_PER_GROUP * group + t, v[:, t, :],
+                    )
+                for j in range(ROWS // PAIR):
+                    rows = slice(PAIR * j, PAIR * (j + 1))
+                    h_grouped = regroup.tile([P, 4 * PAIR], BF16, align_bytes=64)
+                    v_by_row = v[:, :, rows].rearrange("p t r -> p r t")
+                    nc.vector.scalar_tensor_tensor(
+                        out=h_grouped[:].rearrange("p (r t) -> p r t", t=TILES_PER_GROUP),
+                        in0=v_by_row, scalar=SLOPE, in1=v_by_row, op0=ALU.mult, op1=ALU.max,
+                    )
+                    nc.vector.quantize_mx(
+                        out=h_codes[:, group, rows].bitcast(FP8X4),
+                        scales=h_scales[:, group, rows],
+                        in_=h_grouped[:],
+                    )
+
+        with ExitStack() as second:
+            work = second.enter_context(tc.tile_pool(name="work", bufs=3))
+            done = second.enter_context(tc.tile_pool(name="done", bufs=4))
+            stores = second.enter_context(tc.tile_pool(name="stores", bufs=2))
+            for a in range(OUT_TILES // 2):
+                out_t = []
+                for e in range(2):
+                    v1 = work.tile([P, ROWS], F32)
+                    multiply_and_normalise(
+                        w1_codes, w1_scales, h_codes, h_scales, HIDDEN_PASSES, 2 * a + e,
+                        HIDDEN_TILES + 2 * a + e, v1[:],
+                    )
+                    o1 = done.tile([P, ROWS], F32)
+                    nc.vector.scalar_tensor_tensor(
+                        out=o1[:], in0=v1[:], scalar=SLOPE, in1=v1[:], op0=ALU.mult, op1=ALU.max
+                    )
+                    out_t.append(o1)
+                by_row = stores.tile([P, ROWS // P, PAIR], F32)
+                for j in range(ROWS // PAIR):
+                    bank = tbanks.tile([P, 2, 2, P], F32, tag="bank")
+                    for i in range(2):
+                        r_cols = slice(P * (2 * j + i), P * (2 * j + i + 1))
+                        for e in range(2):
+                            nc.tensor.transpose(bank[:, i, e, :], out_t[e][:, r_cols], ident[:])
+                    nc.scalar.copy(
+                        out=by_row[:, 2 * j : 2 * j + 2, :].rearrange("p i (c e) -> p i c e", e=2),
+                        in_=bank[:].rearrange("p i e c -> p i c e"),
+                    )
+                nc.sync.dma_start(
+                    out=out_rows[:, PAIR * a : PAIR * (a + 1)].rearrange("(i p) c -> p i c", p=P),
+                    in_=by_row[:],
+                )

@@ -28,6 +28,7 @@ BANK = 512
 PAIR = 256
 EPS_BN = 1e-5
 SLOPE = 0.01
+LEAKY_LAG = 5
 
 FLOPS = 2 * ROWS * GROUPS * GROUP_K * 512 + 2 * ROWS * HIDDEN * OUT_CH
 
@@ -41,6 +42,7 @@ def tile_nodeupdatenetwork_pb_kernel(
     out_rows = out.flatten_outer_dims()
 
     with ExitStack() as whole:
+        whole.enter_context(tc.manual_schedule())
         const = whole.enter_context(tc.tile_pool(name="const", bufs=1))
         small = whole.enter_context(tc.tile_pool(name="small", bufs=4))
         kept = whole.enter_context(tc.tile_pool(name="kept", bufs=1))
@@ -66,26 +68,7 @@ def tile_nodeupdatenetwork_pb_kernel(
         h_codes = kept.tile([P, HIDDEN_PASSES, ROWS], U32, align_bytes=64)
         h_scales = kept.tile([P, HIDDEN_PASSES, ROWS], U8, align_bytes=64)
 
-        def scale_and_bias(stats, tile_index):
-            mean_var = small.tile([P, 2], F32)
-            nc.vector.bn_aggr(out=mean_var[:], in_=stats[:].rearrange("p h s -> p (h s)"))
-            std = small.tile([P, 1], F32)
-            nc.scalar.activation(out=std[:], in_=mean_var[:, 1:2], func=ACT.Sqrt, bias=eps[:, 0:1])
-            rstd = small.tile([P, 1], F32)
-            nc.vector.reciprocal(out=rstd[:], in_=std[:])
-            scale_pm = small.tile([P, 2], F32)
-            nc.vector.tensor_scalar(
-                out=scale_pm[:], in0=gain_pm[:, tile_index, :], scalar1=rstd[:, 0:1], scalar2=None,
-                op0=ALU.mult,
-            )
-            bias = small.tile([P, 1], F32)
-            nc.vector.tensor_scalar(
-                out=bias[:], in0=mean_var[:, 0:1], scalar1=scale_pm[:, 1:2],
-                scalar2=shift[:, tile_index : tile_index + 1], op0=ALU.mult, op1=ALU.add,
-            )
-            return scale_pm, bias
-
-        def multiply_and_normalise(w_codes, w_scales, a_codes, a_scales, passes, w_tile, tile_index, dest):
+        def multiply(w_codes, w_scales, a_codes, a_scales, passes, w_tile):
             w_cols = slice(P * w_tile, P * (w_tile + 1))
             stats = small.tile([P, 2, 6], F32)
             banks = []
@@ -104,7 +87,30 @@ def tile_nodeupdatenetwork_pb_kernel(
                     )
                 nc.vector.bn_stats(out=stats[:, half, :], in_=acc[:])
                 banks.append(acc)
-            scale_pm, bias = scale_and_bias(stats, tile_index)
+            mean_var = small.tile([P, 2], F32)
+            nc.vector.bn_aggr(out=mean_var[:], in_=stats[:].rearrange("p h s -> p (h s)"))
+            return banks, mean_var
+
+        def inverse_std(mean_var):
+            std = small.tile([P, 1], F32)
+            nc.scalar.activation(out=std[:], in_=mean_var[:, 1:2], func=ACT.Sqrt, bias=eps[:, 0:1])
+            rstd = small.tile([P, 1], F32)
+            nc.vector.reciprocal(out=rstd[:], in_=std[:])
+            return rstd
+
+        def scale_and_bias(mean_var, rstd, tile_index):
+            scale_pm = small.tile([P, 2], F32)
+            nc.scalar.activation(
+                out=scale_pm[:], in_=gain_pm[:, tile_index, :], func=ACT.Copy, scale=rstd[:, 0:1]
+            )
+            bias = small.tile([P, 1], F32)
+            nc.scalar.activation(
+                out=bias[:], in_=mean_var[:, 0:1], func=ACT.Identity, scale=scale_pm[:, 1:2],
+                bias=shift[:, tile_index : tile_index + 1],
+            )
+            return scale_pm, bias
+
+        def normalise(banks, scale_pm, bias, dest):
             for half in range(2):
                 nc.scalar.activation(
                     out=dest[:, BANK * half : BANK * (half + 1)], in_=banks[half][:],
@@ -112,17 +118,16 @@ def tile_nodeupdatenetwork_pb_kernel(
                 )
 
         with ExitStack() as first:
-            raw = first.enter_context(tc.tile_pool(name="raw", bufs=9))
-            raw_w1 = first.enter_context(tc.tile_pool(name="raw_w1", bufs=4))
+            raw = first.enter_context(tc.tile_pool(name="raw", bufs=10))
             staged = first.enter_context(tc.tile_pool(name="staged", bufs=2))
-            regroup = first.enter_context(tc.tile_pool(name="regroup", bufs=6))
-            normed = first.enter_context(tc.tile_pool(name="normed", bufs=1))
+            regroup = first.enter_context(tc.tile_pool(name="regroup", bufs=4))
+            normed = first.enter_context(tc.tile_pool(name="normed", bufs=2))
 
             def load_stage(stage):
                 pairs = []
                 if stage == GROUPS:
                     for a in range(OUT_TILES // 2):
-                        w1_pair = raw_w1.tile([P, 2, HIDDEN], BF16)
+                        w1_pair = raw.tile([P, 2, HIDDEN], BF16, tag="pair")
                         nc.sync.dma_start(
                             out=w1_pair[:],
                             in_=w1[PAIR * a : PAIR * (a + 1), :].rearrange("(p e) k -> p e k", e=2),
@@ -135,9 +140,9 @@ def tile_nodeupdatenetwork_pb_kernel(
                 x_scales = staged.tile([P, GROUP_PASSES, ROWS], U8, align_bytes=64)
                 for a in range(TILES_PER_GROUP // 2):
                     first_row = 512 * stage + PAIR * a
-                    w0_pair = raw.tile([P, 2, GROUP_K], BF16, tag="pair")
+                    w0_pair = raw.tile([P, 2, HIDDEN], BF16, tag="pair")
                     nc.sync.dma_start(
-                        out=w0_pair[:],
+                        out=w0_pair[:, :, 0:GROUP_K],
                         in_=w0[first_row : first_row + PAIR, :].rearrange("(p e) k -> p e k", e=2),
                     )
                     pairs.append((w0_pair, w0_codes, w0_scales, PAIR * a))
@@ -145,7 +150,7 @@ def tile_nodeupdatenetwork_pb_kernel(
                 from_node = max(0, min(NODE_K - k0, GROUP_K))
                 for j in range(ROWS // PAIR):
                     rows = slice(PAIR * j, PAIR * (j + 1))
-                    x_pair = raw.tile([P, 2, GROUP_K], BF16, tag="pair")
+                    x_pair = raw.tile([P, 2, HIDDEN], BF16, tag="pair")
                     if from_node > 0:
                         nc.sync.dma_start(
                             out=x_pair[:, :, 0:from_node],
@@ -182,6 +187,23 @@ def tile_nodeupdatenetwork_pb_kernel(
                     in_=grouped[:],
                 )
 
+            def leaky_piece(v, j):
+                h_grouped = regroup.tile([P, 4 * PAIR], BF16, align_bytes=64)
+                v_by_row = v[:, :, PAIR * j : PAIR * (j + 1)].rearrange("p t r -> p r t")
+                nc.vector.scalar_tensor_tensor(
+                    out=h_grouped[:].rearrange("p (r t) -> p r t", t=TILES_PER_GROUP),
+                    in0=v_by_row, scalar=SLOPE, in1=v_by_row, op0=ALU.mult, op1=ALU.max,
+                )
+                return h_grouped
+
+            def quantise_piece(h_grouped, group, j):
+                rows = slice(PAIR * j, PAIR * (j + 1))
+                nc.vector.quantize_mx(
+                    out=h_codes[:, group, rows].bitcast(FP8X4),
+                    scales=h_scales[:, group, rows],
+                    in_=h_grouped[:],
+                )
+
             pairs, passes, operands = load_stage(0)
             loaded = load_stage(1)
             for pair in pairs:
@@ -201,52 +223,49 @@ def tile_nodeupdatenetwork_pb_kernel(
             shift = const.tile([P, n_tiles], F32)
             nc.vector.tensor_copy(out=shift[:], in_=vec_cols[:, n_tiles : 2 * n_tiles])
 
-            for group in range(GROUPS):
-                w0_codes, w0_scales, x_codes, x_scales = operands
-                pairs, passes, operands = loaded
-                if group + 2 <= GROUPS:
-                    loaded = load_stage(group + 2)
-                units = [(pair, c) for pair in pairs for c in range(passes)]
-                v = normed.tile([P, TILES_PER_GROUP, ROWS], F32)
-                for t in range(TILES_PER_GROUP):
-                    quarter = slice(len(units) * t // TILES_PER_GROUP, len(units) * (t + 1) // TILES_PER_GROUP)
-                    for pair, c in units[quarter]:
+            tiles = []
+            normed_groups = []
+            pieces = []
+            for q in range(HIDDEN_TILES + LEAKY_LAG + 2):
+                multiplying = q < HIDDEN_TILES
+                normalising = 1 <= q <= HIDDEN_TILES
+                piece = q - LEAKY_LAG
+                if 0 <= piece < HIDDEN_TILES:
+                    pieces.append(leaky_piece(normed_groups[piece // 4], piece % 4))
+                if 1 <= piece <= HIDDEN_TILES:
+                    quantise_piece(pieces[piece - 1], (piece - 1) // 4, (piece - 1) % 4)
+                if normalising:
+                    banks, mean_var = tiles[q - 1]
+                    rstd = inverse_std(mean_var)
+                if multiplying:
+                    group, t = divmod(q, TILES_PER_GROUP)
+                    if t == 0:
+                        w0_codes, w0_scales, x_codes, x_scales = operands
+                        pairs, passes, operands = loaded
+                        if group + 2 <= GROUPS:
+                            loaded = load_stage(group + 2)
+                        units = [(pair, c) for pair in pairs for c in range(passes)]
+                        v = normed.tile([P, TILES_PER_GROUP, ROWS], F32)
+                        normed_groups.append(v)
+                    quarter = units[len(units) * t // TILES_PER_GROUP : len(units) * (t + 1) // TILES_PER_GROUP]
+                    for pair, c in quarter[: len(quarter) // 2]:
                         transpose_and_quantise(pair, c)
-                    multiply_and_normalise(
-                        w0_codes, w0_scales, x_codes, x_scales, GROUP_PASSES, t,
-                        TILES_PER_GROUP * group + t, v[:, t, :],
-                    )
-                for j in range(ROWS // PAIR):
-                    rows = slice(PAIR * j, PAIR * (j + 1))
-                    h_grouped = regroup.tile([P, 4 * PAIR], BF16, align_bytes=64)
-                    v_by_row = v[:, :, rows].rearrange("p t r -> p r t")
-                    nc.vector.scalar_tensor_tensor(
-                        out=h_grouped[:].rearrange("p (r t) -> p r t", t=TILES_PER_GROUP),
-                        in0=v_by_row, scalar=SLOPE, in1=v_by_row, op0=ALU.mult, op1=ALU.max,
-                    )
-                    nc.vector.quantize_mx(
-                        out=h_codes[:, group, rows].bitcast(FP8X4),
-                        scales=h_scales[:, group, rows],
-                        in_=h_grouped[:],
-                    )
+                if normalising:
+                    scale_pm, bias = scale_and_bias(mean_var, rstd, q - 1)
+                if multiplying:
+                    for pair, c in quarter[len(quarter) // 2 :]:
+                        transpose_and_quantise(pair, c)
+                if normalising:
+                    normalise(banks, scale_pm, bias, normed_groups[(q - 1) // 4][:, (q - 1) % 4, :])
+                if multiplying:
+                    tiles.append(multiply(w0_codes, w0_scales, x_codes, x_scales, GROUP_PASSES, t))
 
         with ExitStack() as second:
             work = second.enter_context(tc.tile_pool(name="work", bufs=3))
             done = second.enter_context(tc.tile_pool(name="done", bufs=4))
             stores = second.enter_context(tc.tile_pool(name="stores", bufs=2))
-            for a in range(OUT_TILES // 2):
-                out_t = []
-                for e in range(2):
-                    v1 = work.tile([P, ROWS], F32)
-                    multiply_and_normalise(
-                        w1_codes, w1_scales, h_codes, h_scales, HIDDEN_PASSES, 2 * a + e,
-                        HIDDEN_TILES + 2 * a + e, v1[:],
-                    )
-                    o1 = done.tile([P, ROWS], F32)
-                    nc.vector.scalar_tensor_tensor(
-                        out=o1[:], in0=v1[:], scalar=SLOPE, in1=v1[:], op0=ALU.mult, op1=ALU.max
-                    )
-                    out_t.append(o1)
+
+            def store_pair(a, out_t):
                 by_row = stores.tile([P, ROWS // P, PAIR], F32)
                 for j in range(ROWS // PAIR):
                     bank = tbanks.tile([P, 2, 2, P], F32, tag="bank")
@@ -262,3 +281,27 @@ def tile_nodeupdatenetwork_pb_kernel(
                     out=out_rows[:, PAIR * a : PAIR * (a + 1)].rearrange("(i p) c -> p i c", p=P),
                     in_=by_row[:],
                 )
+
+            tiles = []
+            normed_tiles = []
+            out_tiles = []
+            for j in range(OUT_TILES + 2):
+                if 2 <= j:
+                    o1 = done.tile([P, ROWS], F32)
+                    nc.vector.scalar_tensor_tensor(
+                        out=o1[:], in0=normed_tiles[j - 2][:], scalar=SLOPE, in1=normed_tiles[j - 2][:],
+                        op0=ALU.mult, op1=ALU.max,
+                    )
+                    out_tiles.append(o1)
+                if 1 <= j <= OUT_TILES:
+                    banks, mean_var = tiles[j - 1]
+                    rstd = inverse_std(mean_var)
+                    scale_pm, bias = scale_and_bias(mean_var, rstd, HIDDEN_TILES + j - 1)
+                    v1 = work.tile([P, ROWS], F32)
+                    normalise(banks, scale_pm, bias, v1[:])
+                    normed_tiles.append(v1)
+                if j < OUT_TILES:
+                    tiles.append(multiply(w1_codes, w1_scales, h_codes, h_scales, HIDDEN_PASSES, j))
+                if 2 <= j and j % 2 == 1:
+                    a = (j - 3) // 2
+                    store_pair(a, out_tiles[2 * a : 2 * a + 2])

@@ -46,8 +46,6 @@ def tile_nodeupdatenetwork_pb_kernel(
         const = whole.enter_context(tc.tile_pool(name="const", bufs=1))
         small = whole.enter_context(tc.tile_pool(name="small", bufs=4))
         kept = whole.enter_context(tc.tile_pool(name="kept", bufs=1))
-        tbanks = whole.enter_context(tc.psum_pool(name="tbanks", bufs=4))
-        sums = whole.enter_context(tc.psum_pool(name="sums", bufs=4))
 
         vec_rows = const.tile([P, 2 * P], BF16)
         nc.vector.memset(vec_rows[:], 0.0)
@@ -91,9 +89,12 @@ def tile_nodeupdatenetwork_pb_kernel(
             nc.vector.bn_aggr(out=mean_var[:], in_=stats[:].rearrange("p h s -> p (h s)"))
             return banks, mean_var
 
-        def inverse_std(mean_var):
+        def standard_deviation(mean_var):
             std = small.tile([P, 1], F32)
             nc.scalar.activation(out=std[:], in_=mean_var[:, 1:2], func=ACT.Sqrt, bias=eps[:, 0:1])
+            return std
+
+        def inverse(std):
             rstd = small.tile([P, 1], F32)
             nc.vector.reciprocal(out=rstd[:], in_=std[:])
             return rstd
@@ -122,6 +123,8 @@ def tile_nodeupdatenetwork_pb_kernel(
             staged = first.enter_context(tc.tile_pool(name="staged", bufs=2))
             regroup = first.enter_context(tc.tile_pool(name="regroup", bufs=4))
             normed = first.enter_context(tc.tile_pool(name="normed", bufs=2))
+            tbanks = first.enter_context(tc.psum_pool(name="tbanks", bufs=4))
+            sums = first.enter_context(tc.psum_pool(name="sums", bufs=4))
 
             def load_stage(stage):
                 pairs = []
@@ -230,13 +233,15 @@ def tile_nodeupdatenetwork_pb_kernel(
                 multiplying = q < HIDDEN_TILES
                 normalising = 1 <= q <= HIDDEN_TILES
                 piece = q - LEAKY_LAG
+                if normalising:
+                    banks, mean_var = tiles[q - 1]
+                    std = standard_deviation(mean_var)
                 if 0 <= piece < HIDDEN_TILES:
                     pieces.append(leaky_piece(normed_groups[piece // 4], piece % 4))
                 if 1 <= piece <= HIDDEN_TILES:
                     quantise_piece(pieces[piece - 1], (piece - 1) // 4, (piece - 1) % 4)
                 if normalising:
-                    banks, mean_var = tiles[q - 1]
-                    rstd = inverse_std(mean_var)
+                    rstd = inverse(std)
                 if multiplying:
                     group, t = divmod(q, TILES_PER_GROUP)
                     if t == 0:
@@ -248,14 +253,10 @@ def tile_nodeupdatenetwork_pb_kernel(
                         v = normed.tile([P, TILES_PER_GROUP, ROWS], F32)
                         normed_groups.append(v)
                     quarter = units[len(units) * t // TILES_PER_GROUP : len(units) * (t + 1) // TILES_PER_GROUP]
-                    for pair, c in quarter[: len(quarter) // 2]:
+                    for pair, c in quarter:
                         transpose_and_quantise(pair, c)
                 if normalising:
                     scale_pm, bias = scale_and_bias(mean_var, rstd, q - 1)
-                if multiplying:
-                    for pair, c in quarter[len(quarter) // 2 :]:
-                        transpose_and_quantise(pair, c)
-                if normalising:
                     normalise(banks, scale_pm, bias, normed_groups[(q - 1) // 4][:, (q - 1) % 4, :])
                 if multiplying:
                     tiles.append(multiply(w0_codes, w0_scales, x_codes, x_scales, GROUP_PASSES, t))
@@ -263,45 +264,69 @@ def tile_nodeupdatenetwork_pb_kernel(
         with ExitStack() as second:
             work = second.enter_context(tc.tile_pool(name="work", bufs=3))
             done = second.enter_context(tc.tile_pool(name="done", bufs=4))
-            stores = second.enter_context(tc.tile_pool(name="stores", bufs=2))
+            stores = second.enter_context(tc.tile_pool(name="stores", bufs=3))
+            sums = second.enter_context(tc.psum_pool(name="sums2", bufs=6))
+            tbanks = second.enter_context(tc.psum_pool(name="tbanks2", bufs=2))
 
-            def store_pair(a, out_t):
-                by_row = stores.tile([P, ROWS // P, PAIR], F32)
-                for j in range(ROWS // PAIR):
-                    bank = tbanks.tile([P, 2, 2, P], F32, tag="bank")
+            def transpose_back(piece):
+                a, half = divmod(piece, 2)
+                banks = []
+                for j in range(2):
+                    bank = tbanks.tile([P, 2, 2, P], F32)
                     for i in range(2):
-                        r_cols = slice(P * (2 * j + i), P * (2 * j + i + 1))
+                        row_tile = 4 * half + 2 * j + i
                         for e in range(2):
-                            nc.tensor.transpose(bank[:, i, e, :], out_t[e][:, r_cols], ident[:])
-                    nc.scalar.copy(
-                        out=by_row[:, 2 * j : 2 * j + 2, :].rearrange("p i (c e) -> p i c e", e=2),
-                        in_=bank[:].rearrange("p i e c -> p i c e"),
-                    )
+                            nc.tensor.transpose(
+                                bank[:, i, e, :], out_tiles[2 * a + e][:, P * row_tile : P * (row_tile + 1)], ident[:]
+                            )
+                    banks.append(bank)
+                return banks
+
+            def store_piece(piece, banks):
+                a, half = divmod(piece, 2)
+                by_row = stores.tile([P, 4, PAIR], F32)
+                nc.scalar.copy(
+                    out=by_row[:, 0:2, :].rearrange("p i (c e) -> p i c e", e=2),
+                    in_=banks[0][:].rearrange("p i e c -> p i c e"),
+                )
+                nc.vector.tensor_copy(
+                    out=by_row[:, 2:4, :].rearrange("p i (c e) -> p i c e", e=2),
+                    in_=banks[1][:].rearrange("p i e c -> p i c e"),
+                )
                 nc.sync.dma_start(
-                    out=out_rows[:, PAIR * a : PAIR * (a + 1)].rearrange("(i p) c -> p i c", p=P),
+                    out=out_rows[BANK * half : BANK * (half + 1), PAIR * a : PAIR * (a + 1)].rearrange(
+                        "(i p) c -> p i c", p=P
+                    ),
                     in_=by_row[:],
                 )
 
             tiles = []
             normed_tiles = []
             out_tiles = []
-            for j in range(OUT_TILES + 2):
-                if 2 <= j:
-                    o1 = done.tile([P, ROWS], F32)
-                    nc.vector.scalar_tensor_tensor(
-                        out=o1[:], in0=normed_tiles[j - 2][:], scalar=SLOPE, in1=normed_tiles[j - 2][:],
-                        op0=ALU.mult, op1=ALU.max,
-                    )
-                    out_tiles.append(o1)
+            back = []
+            for j in range(OUT_TILES + 4):
                 if 1 <= j <= OUT_TILES:
                     banks, mean_var = tiles[j - 1]
-                    rstd = inverse_std(mean_var)
+                    std = standard_deviation(mean_var)
+                if 2 <= j <= OUT_TILES + 1:
+                    o1 = done.tile([P, ROWS], F32)
+                    for half in range(2):
+                        r_cols = slice(BANK * half, BANK * (half + 1))
+                        nc.vector.scalar_tensor_tensor(
+                            out=o1[:, r_cols], in0=normed_tiles[j - 2][:, r_cols], scalar=SLOPE,
+                            in1=normed_tiles[j - 2][:, r_cols], op0=ALU.mult, op1=ALU.max,
+                        )
+                    out_tiles.append(o1)
+                if 1 <= j <= OUT_TILES:
+                    rstd = inverse(std)
+                if 4 <= j:
+                    store_piece(j - 4, back[j - 4])
+                if 1 <= j <= OUT_TILES:
                     scale_pm, bias = scale_and_bias(mean_var, rstd, HIDDEN_TILES + j - 1)
                     v1 = work.tile([P, ROWS], F32)
                     normalise(banks, scale_pm, bias, v1[:])
                     normed_tiles.append(v1)
                 if j < OUT_TILES:
                     tiles.append(multiply(w1_codes, w1_scales, h_codes, h_scales, HIDDEN_PASSES, j))
-                if 2 <= j and j % 2 == 1:
-                    a = (j - 3) // 2
-                    store_pair(a, out_tiles[2 * a : 2 * a + 2])
+                if 3 <= j <= OUT_TILES + 2:
+                    back.append(transpose_back(j - 3))

@@ -28,7 +28,7 @@ BANK = 512
 PAIR = 256
 EPS_BN = 1e-5
 SLOPE = 0.01
-LEAKY_LAG = 5
+REGROUP_LAG = 6
 
 FLOPS = 2 * ROWS * GROUPS * GROUP_K * 512 + 2 * ROWS * HIDDEN * OUT_CH
 
@@ -122,7 +122,8 @@ def tile_nodeupdatenetwork_pb_kernel(
             raw = first.enter_context(tc.tile_pool(name="raw", bufs=10))
             staged = first.enter_context(tc.tile_pool(name="staged", bufs=2))
             regroup = first.enter_context(tc.tile_pool(name="regroup", bufs=4))
-            normed = first.enter_context(tc.tile_pool(name="normed", bufs=2))
+            normed = first.enter_context(tc.tile_pool(name="normed", bufs=3))
+            hidden = first.enter_context(tc.tile_pool(name="hidden", bufs=2))
             tbanks = first.enter_context(tc.psum_pool(name="tbanks", bufs=4))
             sums = first.enter_context(tc.psum_pool(name="sums", bufs=4))
 
@@ -190,12 +191,11 @@ def tile_nodeupdatenetwork_pb_kernel(
                     in_=grouped[:],
                 )
 
-            def leaky_piece(v, j):
+            def regroup_piece(h, j):
                 h_grouped = regroup.tile([P, 4 * PAIR], BF16, align_bytes=64)
-                v_by_row = v[:, :, PAIR * j : PAIR * (j + 1)].rearrange("p t r -> p r t")
-                nc.vector.scalar_tensor_tensor(
-                    out=h_grouped[:].rearrange("p (r t) -> p r t", t=TILES_PER_GROUP),
-                    in0=v_by_row, scalar=SLOPE, in1=v_by_row, op0=ALU.mult, op1=ALU.max,
+                nc.vector.tensor_copy(
+                    out=h_grouped[:].rearrange("p (c i t) -> p c t i", i=4, t=TILES_PER_GROUP),
+                    in_=h[:, :, PAIR * j : PAIR * (j + 1)].rearrange("p t (c i) -> p c t i", i=4),
                 )
                 return h_grouped
 
@@ -227,17 +227,26 @@ def tile_nodeupdatenetwork_pb_kernel(
             nc.vector.tensor_copy(out=shift[:], in_=vec_cols[:, n_tiles : 2 * n_tiles])
 
             tiles = []
-            normed_groups = []
+            normed_tiles = []
+            hidden_groups = []
             pieces = []
-            for q in range(HIDDEN_TILES + LEAKY_LAG + 2):
+            for q in range(HIDDEN_TILES + REGROUP_LAG + 2):
                 multiplying = q < HIDDEN_TILES
                 normalising = 1 <= q <= HIDDEN_TILES
-                piece = q - LEAKY_LAG
+                piece = q - REGROUP_LAG
                 if normalising:
                     banks, mean_var = tiles[q - 1]
                     std = standard_deviation(mean_var)
+                if 2 <= q <= HIDDEN_TILES + 1:
+                    if (q - 2) % TILES_PER_GROUP == 0:
+                        h = hidden.tile([P, TILES_PER_GROUP, ROWS], BF16)
+                        hidden_groups.append(h)
+                    nc.vector.scalar_tensor_tensor(
+                        out=hidden_groups[(q - 2) // 4][:, (q - 2) % 4, :], in0=normed_tiles[q - 2][:],
+                        scalar=SLOPE, in1=normed_tiles[q - 2][:], op0=ALU.mult, op1=ALU.max,
+                    )
                 if 0 <= piece < HIDDEN_TILES:
-                    pieces.append(leaky_piece(normed_groups[piece // 4], piece % 4))
+                    pieces.append(regroup_piece(hidden_groups[piece // 4], piece % 4))
                 if 1 <= piece <= HIDDEN_TILES:
                     quantise_piece(pieces[piece - 1], (piece - 1) // 4, (piece - 1) % 4)
                 if normalising:
@@ -250,14 +259,14 @@ def tile_nodeupdatenetwork_pb_kernel(
                         if group + 2 <= GROUPS:
                             loaded = load_stage(group + 2)
                         units = [(pair, c) for pair in pairs for c in range(passes)]
-                        v = normed.tile([P, TILES_PER_GROUP, ROWS], F32)
-                        normed_groups.append(v)
                     quarter = units[len(units) * t // TILES_PER_GROUP : len(units) * (t + 1) // TILES_PER_GROUP]
                     for pair, c in quarter:
                         transpose_and_quantise(pair, c)
                 if normalising:
                     scale_pm, bias = scale_and_bias(mean_var, rstd, q - 1)
-                    normalise(banks, scale_pm, bias, normed_groups[(q - 1) // 4][:, (q - 1) % 4, :])
+                    v = normed.tile([P, ROWS], F32)
+                    normalise(banks, scale_pm, bias, v[:])
+                    normed_tiles.append(v)
                 if multiplying:
                     tiles.append(multiply(w0_codes, w0_scales, x_codes, x_scales, GROUP_PASSES, t))
 

@@ -28,7 +28,7 @@ BANK = 512
 PAIR = 256
 EPS_BN = 1e-5
 SLOPE = 0.01
-REGROUP_LAG = 6
+LEAKY_LAG = 5
 
 FLOPS = 2 * ROWS * GROUPS * GROUP_K * 512 + 2 * ROWS * HIDDEN * OUT_CH
 
@@ -66,28 +66,27 @@ def tile_nodeupdatenetwork_pb_kernel(
         h_codes = kept.tile([P, HIDDEN_PASSES, ROWS], U32, align_bytes=64)
         h_scales = kept.tile([P, HIDDEN_PASSES, ROWS], U8, align_bytes=64)
 
-        def multiply(w_codes, w_scales, a_codes, a_scales, passes, w_tile):
+        def multiply_half(w_codes, w_scales, a_codes, a_scales, passes, w_tile, half, stats):
             w_cols = slice(P * w_tile, P * (w_tile + 1))
-            stats = small.tile([P, 2, 6], F32)
-            banks = []
-            for half in range(2):
-                r_cols = slice(BANK * half, BANK * (half + 1))
-                acc = sums.tile([P, BANK], F32)
-                for c in range(passes):
-                    nc.tensor.matmul_mx(
-                        out=acc[:],
-                        lhsT=w_codes[:, c, w_cols].bitcast(FP8X4),
-                        lhsT_scale=w_scales[:, c, w_cols],
-                        rhs=a_codes[:, c, r_cols].bitcast(FP8X4),
-                        rhs_scale=a_scales[:, c, r_cols],
-                        start=(c == 0),
-                        stop=(c == passes - 1),
-                    )
-                nc.vector.bn_stats(out=stats[:, half, :], in_=acc[:])
-                banks.append(acc)
+            r_cols = slice(BANK * half, BANK * (half + 1))
+            acc = sums.tile([P, BANK], F32)
+            for c in range(passes):
+                nc.tensor.matmul_mx(
+                    out=acc[:],
+                    lhsT=w_codes[:, c, w_cols].bitcast(FP8X4),
+                    lhsT_scale=w_scales[:, c, w_cols],
+                    rhs=a_codes[:, c, r_cols].bitcast(FP8X4),
+                    rhs_scale=a_scales[:, c, r_cols],
+                    start=(c == 0),
+                    stop=(c == passes - 1),
+                )
+            nc.vector.bn_stats(out=stats[:, half, :], in_=acc[:])
+            return acc
+
+        def mean_and_variance(stats):
             mean_var = small.tile([P, 2], F32)
             nc.vector.bn_aggr(out=mean_var[:], in_=stats[:].rearrange("p h s -> p (h s)"))
-            return banks, mean_var
+            return mean_var
 
         def standard_deviation(mean_var):
             std = small.tile([P, 1], F32)
@@ -99,31 +98,32 @@ def tile_nodeupdatenetwork_pb_kernel(
             nc.vector.reciprocal(out=rstd[:], in_=std[:])
             return rstd
 
-        def scale_and_bias(mean_var, rstd, tile_index):
-            scale_pm = small.tile([P, 2], F32)
-            nc.scalar.activation(
-                out=scale_pm[:], in_=gain_pm[:, tile_index, :], func=ACT.Copy, scale=rstd[:, 0:1]
+        def minus_gain_mean(mean_var, tile_index):
+            nc.vector.tensor_scalar(
+                out=gain_mean[:, tile_index, 1:2], in0=mean_var[:, 0:1],
+                scalar1=minus_gain[:, tile_index : tile_index + 1], scalar2=None, op0=ALU.mult,
             )
-            bias = small.tile([P, 1], F32)
-            nc.scalar.activation(
-                out=bias[:], in_=mean_var[:, 0:1], func=ACT.Identity, scale=scale_pm[:, 1:2],
-                bias=shift[:, tile_index : tile_index + 1],
-            )
-            return scale_pm, bias
 
-        def normalise(banks, scale_pm, bias, dest):
+        def scale_and_bias(rstd, tile_index):
+            scale_bias = small.tile([P, 2], F32)
+            nc.vector.scalar_tensor_tensor(
+                out=scale_bias[:], in0=gain_mean[:, tile_index, :], scalar=rstd[:, 0:1],
+                in1=zero_shift[:, tile_index, :], op0=ALU.mult, op1=ALU.add,
+            )
+            return scale_bias
+
+        def normalise(banks, scale_bias, dest):
             for half in range(2):
                 nc.scalar.activation(
                     out=dest[:, BANK * half : BANK * (half + 1)], in_=banks[half][:],
-                    func=ACT.Identity, scale=scale_pm[:, 0:1], bias=bias[:, 0:1],
+                    func=ACT.Identity, scale=scale_bias[:, 0:1], bias=scale_bias[:, 1:2],
                 )
 
         with ExitStack() as first:
             raw = first.enter_context(tc.tile_pool(name="raw", bufs=10))
             staged = first.enter_context(tc.tile_pool(name="staged", bufs=2))
-            regroup = first.enter_context(tc.tile_pool(name="regroup", bufs=4))
-            normed = first.enter_context(tc.tile_pool(name="normed", bufs=3))
-            hidden = first.enter_context(tc.tile_pool(name="hidden", bufs=2))
+            regroup = first.enter_context(tc.tile_pool(name="regroup", bufs=6))
+            normed = first.enter_context(tc.tile_pool(name="normed", bufs=2))
             tbanks = first.enter_context(tc.psum_pool(name="tbanks", bufs=4))
             sums = first.enter_context(tc.psum_pool(name="sums", bufs=4))
 
@@ -142,14 +142,17 @@ def tile_nodeupdatenetwork_pb_kernel(
                 w0_scales = staged.tile([P, GROUP_PASSES, 512], U8, align_bytes=64)
                 x_codes = staged.tile([P, GROUP_PASSES, ROWS], U32, align_bytes=64)
                 x_scales = staged.tile([P, GROUP_PASSES, ROWS], U8, align_bytes=64)
-                for a in range(TILES_PER_GROUP // 2):
+
+                def load_w0(a):
                     first_row = 512 * stage + PAIR * a
                     w0_pair = raw.tile([P, 2, HIDDEN], BF16, tag="pair")
                     nc.sync.dma_start(
                         out=w0_pair[:, :, 0:GROUP_K],
                         in_=w0[first_row : first_row + PAIR, :].rearrange("(p e) k -> p e k", e=2),
                     )
-                    pairs.append((w0_pair, w0_codes, w0_scales, PAIR * a))
+                    return w0_pair, w0_codes, w0_scales, PAIR * a
+
+                pairs.append(load_w0(0))
                 k0 = GROUP_K * stage
                 from_node = max(0, min(NODE_K - k0, GROUP_K))
                 for j in range(ROWS // PAIR):
@@ -168,6 +171,7 @@ def tile_nodeupdatenetwork_pb_kernel(
                             ),
                         )
                     pairs.append((x_pair, x_codes, x_scales, PAIR * j))
+                pairs.append(load_w0(1))
                 return pairs, GROUP_PASSES, (w0_codes, w0_scales, x_codes, x_scales)
 
             def transpose_and_quantise(pair, c):
@@ -191,11 +195,12 @@ def tile_nodeupdatenetwork_pb_kernel(
                     in_=grouped[:],
                 )
 
-            def regroup_piece(h, j):
+            def leaky_piece(v, j):
                 h_grouped = regroup.tile([P, 4 * PAIR], BF16, align_bytes=64)
-                nc.vector.tensor_copy(
-                    out=h_grouped[:].rearrange("p (c i t) -> p c t i", i=4, t=TILES_PER_GROUP),
-                    in_=h[:, :, PAIR * j : PAIR * (j + 1)].rearrange("p t (c i) -> p c t i", i=4),
+                v_by_row = v[:, :, PAIR * j : PAIR * (j + 1)].rearrange("p t r -> p r t")
+                nc.vector.scalar_tensor_tensor(
+                    out=h_grouped[:].rearrange("p (r t) -> p r t", t=TILES_PER_GROUP),
+                    in0=v_by_row, scalar=SLOPE, in1=v_by_row, op0=ALU.mult, op1=ALU.max,
                 )
                 return h_grouped
 
@@ -209,48 +214,45 @@ def tile_nodeupdatenetwork_pb_kernel(
 
             pairs, passes, operands = load_stage(0)
             loaded = load_stage(1)
-            for pair in pairs:
-                for c in range(passes):
-                    transpose_and_quantise(pair, c)
+            units = [(pair, c) for pair in pairs for c in range(passes)]
+            for pair, c in units[:-GROUP_PASSES]:
+                transpose_and_quantise(pair, c)
+            left_over = units[-GROUP_PASSES:]
 
             vec_bank = tbanks.tile([P, BANK], F32, tag="bank")
             nc.tensor.transpose(vec_bank[:, 0:P], vec_rows[:].bitcast(F32), ident[:])
             vec_cols = const.tile([P, 2 * P], BF16)
             nc.vector.tensor_copy(out=vec_cols[:].bitcast(F32), in_=vec_bank[:, 0:P])
             n_tiles = HIDDEN_TILES + OUT_TILES
-            gain_pm = const.tile([P, n_tiles, 2], F32)
-            nc.vector.tensor_copy(out=gain_pm[:, :, 0], in_=vec_cols[:, 0:n_tiles])
+            gain_mean = const.tile([P, n_tiles, 2], F32)
+            nc.vector.tensor_copy(out=gain_mean[:, :, 0], in_=vec_cols[:, 0:n_tiles])
+            minus_gain = const.tile([P, n_tiles], F32)
             nc.vector.tensor_scalar(
-                out=gain_pm[:, :, 1], in0=vec_cols[:, 0:n_tiles], scalar1=-1.0, scalar2=None, op0=ALU.mult
+                out=minus_gain[:], in0=vec_cols[:, 0:n_tiles], scalar1=-1.0, scalar2=None, op0=ALU.mult
             )
-            shift = const.tile([P, n_tiles], F32)
-            nc.vector.tensor_copy(out=shift[:], in_=vec_cols[:, n_tiles : 2 * n_tiles])
+            zero_shift = const.tile([P, n_tiles, 2], F32)
+            nc.vector.memset(zero_shift[:], 0.0)
+            nc.vector.tensor_copy(out=zero_shift[:, :, 1], in_=vec_cols[:, n_tiles : 2 * n_tiles])
 
             tiles = []
-            normed_tiles = []
-            hidden_groups = []
+            normed_groups = []
             pieces = []
-            for q in range(HIDDEN_TILES + REGROUP_LAG + 2):
+            for q in range(HIDDEN_TILES + LEAKY_LAG + 2):
                 multiplying = q < HIDDEN_TILES
                 normalising = 1 <= q <= HIDDEN_TILES
-                piece = q - REGROUP_LAG
+                piece = q - LEAKY_LAG
                 if normalising:
                     banks, mean_var = tiles[q - 1]
                     std = standard_deviation(mean_var)
-                if 2 <= q <= HIDDEN_TILES + 1:
-                    if (q - 2) % TILES_PER_GROUP == 0:
-                        h = hidden.tile([P, TILES_PER_GROUP, ROWS], BF16)
-                        hidden_groups.append(h)
-                    nc.vector.scalar_tensor_tensor(
-                        out=hidden_groups[(q - 2) // 4][:, (q - 2) % 4, :], in0=normed_tiles[q - 2][:],
-                        scalar=SLOPE, in1=normed_tiles[q - 2][:], op0=ALU.mult, op1=ALU.max,
-                    )
                 if 0 <= piece < HIDDEN_TILES:
-                    pieces.append(regroup_piece(hidden_groups[piece // 4], piece % 4))
+                    pieces.append(leaky_piece(normed_groups[piece // 4], piece % 4))
+                if normalising:
+                    minus_gain_mean(mean_var, q - 1)
+                    rstd = inverse(std)
                 if 1 <= piece <= HIDDEN_TILES:
                     quantise_piece(pieces[piece - 1], (piece - 1) // 4, (piece - 1) % 4)
                 if normalising:
-                    rstd = inverse(std)
+                    scale_bias = scale_and_bias(rstd, q - 1)
                 if multiplying:
                     group, t = divmod(q, TILES_PER_GROUP)
                     if t == 0:
@@ -258,22 +260,27 @@ def tile_nodeupdatenetwork_pb_kernel(
                         pairs, passes, operands = loaded
                         if group + 2 <= GROUPS:
                             loaded = load_stage(group + 2)
-                        units = [(pair, c) for pair in pairs for c in range(passes)]
+                        units = left_over + [(pair, c) for pair in pairs for c in range(passes)]
+                        left_over = []
+                        v = normed.tile([P, TILES_PER_GROUP, ROWS], F32)
+                        normed_groups.append(v)
                     quarter = units[len(units) * t // TILES_PER_GROUP : len(units) * (t + 1) // TILES_PER_GROUP]
-                    for pair, c in quarter:
+                    stats = small.tile([P, 2, 6], F32)
+                    for pair, c in quarter[: len(quarter) // 2]:
+                        transpose_and_quantise(pair, c)
+                    acc0 = multiply_half(w0_codes, w0_scales, x_codes, x_scales, GROUP_PASSES, t, 0, stats)
+                    for pair, c in quarter[len(quarter) // 2 :]:
                         transpose_and_quantise(pair, c)
                 if normalising:
-                    scale_pm, bias = scale_and_bias(mean_var, rstd, q - 1)
-                    v = normed.tile([P, ROWS], F32)
-                    normalise(banks, scale_pm, bias, v[:])
-                    normed_tiles.append(v)
+                    normalise(banks, scale_bias, normed_groups[(q - 1) // 4][:, (q - 1) % 4, :])
                 if multiplying:
-                    tiles.append(multiply(w0_codes, w0_scales, x_codes, x_scales, GROUP_PASSES, t))
+                    acc1 = multiply_half(w0_codes, w0_scales, x_codes, x_scales, GROUP_PASSES, t, 1, stats)
+                    tiles.append(([acc0, acc1], mean_and_variance(stats)))
 
         with ExitStack() as second:
             work = second.enter_context(tc.tile_pool(name="work", bufs=3))
             done = second.enter_context(tc.tile_pool(name="done", bufs=4))
-            stores = second.enter_context(tc.tile_pool(name="stores", bufs=3))
+            stores = second.enter_context(tc.tile_pool(name="stores", bufs=4))
             sums = second.enter_context(tc.psum_pool(name="sums2", bufs=6))
             tbanks = second.enter_context(tc.psum_pool(name="tbanks2", bufs=2))
 
@@ -293,20 +300,25 @@ def tile_nodeupdatenetwork_pb_kernel(
 
             def store_piece(piece, banks):
                 a, half = divmod(piece, 2)
-                by_row = stores.tile([P, 4, PAIR], F32)
-                nc.scalar.copy(
-                    out=by_row[:, 0:2, :].rearrange("p i (c e) -> p i c e", e=2),
-                    in_=banks[0][:].rearrange("p i e c -> p i c e"),
-                )
-                nc.vector.tensor_copy(
-                    out=by_row[:, 2:4, :].rearrange("p i (c e) -> p i c e", e=2),
-                    in_=banks[1][:].rearrange("p i e c -> p i c e"),
-                )
-                nc.sync.dma_start(
-                    out=out_rows[BANK * half : BANK * (half + 1), PAIR * a : PAIR * (a + 1)].rearrange(
-                        "(i p) c -> p i c", p=P
-                    ),
-                    in_=by_row[:],
+                for j in range(2):
+                    by_row = stores.tile([P, 2, PAIR], F32)
+                    nc.scalar.copy(
+                        out=by_row[:].rearrange("p i (c e) -> p i c e", e=2),
+                        in_=banks[j][:].rearrange("p i e c -> p i c e"),
+                    )
+                    first_row = BANK * half + PAIR * j
+                    nc.sync.dma_start(
+                        out=out_rows[first_row : first_row + PAIR, PAIR * a : PAIR * (a + 1)].rearrange(
+                            "(i p) c -> p i c", p=P
+                        ),
+                        in_=by_row[:],
+                    )
+
+            def leaky_half(dest, source, half):
+                r_cols = slice(BANK * half, BANK * (half + 1))
+                nc.vector.scalar_tensor_tensor(
+                    out=dest[:, r_cols], in0=source[:, r_cols], scalar=SLOPE, in1=source[:, r_cols],
+                    op0=ALU.mult, op1=ALU.max,
                 )
 
             tiles = []
@@ -314,28 +326,30 @@ def tile_nodeupdatenetwork_pb_kernel(
             out_tiles = []
             back = []
             for j in range(OUT_TILES + 4):
-                if 1 <= j <= OUT_TILES:
+                normalising = 1 <= j <= OUT_TILES
+                if normalising:
                     banks, mean_var = tiles[j - 1]
                     std = standard_deviation(mean_var)
                 if 2 <= j <= OUT_TILES + 1:
                     o1 = done.tile([P, ROWS], F32)
-                    for half in range(2):
-                        r_cols = slice(BANK * half, BANK * (half + 1))
-                        nc.vector.scalar_tensor_tensor(
-                            out=o1[:, r_cols], in0=normed_tiles[j - 2][:, r_cols], scalar=SLOPE,
-                            in1=normed_tiles[j - 2][:, r_cols], op0=ALU.mult, op1=ALU.max,
-                        )
-                    out_tiles.append(o1)
-                if 1 <= j <= OUT_TILES:
+                    leaky_half(o1, normed_tiles[j - 2], 0)
+                if normalising:
+                    minus_gain_mean(mean_var, HIDDEN_TILES + j - 1)
                     rstd = inverse(std)
+                if 2 <= j <= OUT_TILES + 1:
+                    leaky_half(o1, normed_tiles[j - 2], 1)
+                    out_tiles.append(o1)
                 if 4 <= j:
                     store_piece(j - 4, back[j - 4])
-                if 1 <= j <= OUT_TILES:
-                    scale_pm, bias = scale_and_bias(mean_var, rstd, HIDDEN_TILES + j - 1)
+                if normalising:
+                    scale_bias = scale_and_bias(rstd, HIDDEN_TILES + j - 1)
                     v1 = work.tile([P, ROWS], F32)
-                    normalise(banks, scale_pm, bias, v1[:])
+                    normalise(banks, scale_bias, v1[:])
                     normed_tiles.append(v1)
                 if j < OUT_TILES:
-                    tiles.append(multiply(w1_codes, w1_scales, h_codes, h_scales, HIDDEN_PASSES, j))
+                    stats = small.tile([P, 2, 6], F32)
+                    acc0 = multiply_half(w1_codes, w1_scales, h_codes, h_scales, HIDDEN_PASSES, j, 0, stats)
+                    acc1 = multiply_half(w1_codes, w1_scales, h_codes, h_scales, HIDDEN_PASSES, j, 1, stats)
+                    tiles.append(([acc0, acc1], mean_and_variance(stats)))
                 if 3 <= j <= OUT_TILES + 2:
                     back.append(transpose_back(j - 3))

@@ -16,21 +16,23 @@ ROWS = 1024
 NODE_K = 2048
 GROUPS = 4
 GROUP_K = 1536
+GROUP_OUT = 512
 GROUP_PASSES = 3
+GROUP_TILES = 4
 HIDDEN = 2048
 HIDDEN_PASSES = 4
-OUT_CH = 1024
-TILES_PER_GROUP = 4
 HIDDEN_TILES = 16
+OUT_CH = 1024
 OUT_TILES = 8
 PASS_WORDS = 256
 BANK = 512
 PAIR = 256
+STATS = 6
 EPS_BN = 1e-5
 SLOPE = 0.01
 LEAKY_LAG = 5
 
-FLOPS = 2 * ROWS * GROUPS * GROUP_K * 512 + 2 * ROWS * HIDDEN * OUT_CH
+FLOPS = 2 * ROWS * GROUPS * GROUP_K * GROUP_OUT + 2 * ROWS * HIDDEN * OUT_CH
 
 
 def tile_nodeupdatenetwork_pb_kernel(
@@ -128,35 +130,35 @@ def tile_nodeupdatenetwork_pb_kernel(
             sums = first.enter_context(tc.psum_pool(name="sums", bufs=4))
 
             def load_stage(stage):
-                pairs = []
                 if stage == GROUPS:
+                    units = []
                     for a in range(OUT_TILES // 2):
                         w1_pair = raw.tile([P, 2, HIDDEN], BF16, tag="pair")
                         nc.sync.dma_start(
                             out=w1_pair[:],
                             in_=w1[PAIR * a : PAIR * (a + 1), :].rearrange("(p e) k -> p e k", e=2),
                         )
-                        pairs.append((w1_pair, w1_codes, w1_scales, PAIR * a))
-                    return pairs, HIDDEN_PASSES, None
-                w0_codes = staged.tile([P, GROUP_PASSES, 512], U32, align_bytes=64)
-                w0_scales = staged.tile([P, GROUP_PASSES, 512], U8, align_bytes=64)
+                        units.extend([(w1_pair, c, w1_codes, w1_scales, PAIR * a) for c in range(HIDDEN_PASSES)])
+                    return units, None
+                w0_codes = staged.tile([P, GROUP_PASSES, GROUP_OUT], U32, align_bytes=64)
+                w0_scales = staged.tile([P, GROUP_PASSES, GROUP_OUT], U8, align_bytes=64)
                 x_codes = staged.tile([P, GROUP_PASSES, ROWS], U32, align_bytes=64)
                 x_scales = staged.tile([P, GROUP_PASSES, ROWS], U8, align_bytes=64)
 
                 def load_w0(a):
-                    first_row = 512 * stage + PAIR * a
+                    first_row = GROUP_OUT * stage + PAIR * a
                     w0_pair = raw.tile([P, 2, HIDDEN], BF16, tag="pair")
                     nc.sync.dma_start(
                         out=w0_pair[:, :, 0:GROUP_K],
                         in_=w0[first_row : first_row + PAIR, :].rearrange("(p e) k -> p e k", e=2),
                     )
-                    return w0_pair, w0_codes, w0_scales, PAIR * a
+                    return [(w0_pair, c, w0_codes, w0_scales, PAIR * a) for c in range(GROUP_PASSES)]
 
-                pairs.append(load_w0(0))
+                units = load_w0(0)
                 k0 = GROUP_K * stage
                 from_node = max(0, min(NODE_K - k0, GROUP_K))
-                for j in range(ROWS // PAIR):
-                    rows = slice(PAIR * j, PAIR * (j + 1))
+                for r in range(ROWS // PAIR):
+                    rows = slice(PAIR * r, PAIR * (r + 1))
                     x_pair = raw.tile([P, 2, HIDDEN], BF16, tag="pair")
                     if from_node > 0:
                         nc.sync.dma_start(
@@ -170,19 +172,19 @@ def tile_nodeupdatenetwork_pb_kernel(
                                 "(i p) k -> p i k", p=P
                             ),
                         )
-                    pairs.append((x_pair, x_codes, x_scales, PAIR * j))
-                pairs.append(load_w0(1))
-                return pairs, GROUP_PASSES, (w0_codes, w0_scales, x_codes, x_scales)
+                    units.extend([(x_pair, c, x_codes, x_scales, PAIR * r) for c in range(GROUP_PASSES)])
+                units.extend(load_w0(1))
+                return units, (w0_codes, w0_scales, x_codes, x_scales)
 
-            def transpose_and_quantise(pair, c):
-                raw_pair, codes, scales, col0 = pair
+            def transpose_and_quantise(unit):
+                pair, c, codes, scales, col0 = unit
                 bank = tbanks.tile([P, 2, PAIR], F32, tag="bank")
-                for j in range(2):
-                    words = raw_pair[:, j, :].bitcast(F32)
+                for i in range(2):
+                    words = pair[:, i, :].bitcast(F32)
                     for u in range(2):
                         first_word = PASS_WORDS * c + P * u
                         nc.tensor.transpose(
-                            bank[:, u, P * j : P * (j + 1)], words[:, first_word : first_word + P], ident[:]
+                            bank[:, u, P * i : P * (i + 1)], words[:, first_word : first_word + P], ident[:]
                         )
                 grouped = regroup.tile([P, 4 * PAIR], BF16, align_bytes=64)
                 nc.scalar.copy(
@@ -195,28 +197,29 @@ def tile_nodeupdatenetwork_pb_kernel(
                     in_=grouped[:],
                 )
 
-            def leaky_piece(v, j):
+            def leaky_piece(piece):
+                g, r = divmod(piece, ROWS // PAIR)
                 h_grouped = regroup.tile([P, 4 * PAIR], BF16, align_bytes=64)
-                v_by_row = v[:, :, PAIR * j : PAIR * (j + 1)].rearrange("p t r -> p r t")
+                v_by_row = normed_groups[g][:, :, PAIR * r : PAIR * (r + 1)].rearrange("p t n -> p n t")
                 nc.vector.scalar_tensor_tensor(
-                    out=h_grouped[:].rearrange("p (r t) -> p r t", t=TILES_PER_GROUP),
+                    out=h_grouped[:].rearrange("p (n t) -> p n t", t=GROUP_TILES),
                     in0=v_by_row, scalar=SLOPE, in1=v_by_row, op0=ALU.mult, op1=ALU.max,
                 )
                 return h_grouped
 
-            def quantise_piece(h_grouped, group, j):
-                rows = slice(PAIR * j, PAIR * (j + 1))
+            def quantise_piece(piece):
+                g, r = divmod(piece, ROWS // PAIR)
+                rows = slice(PAIR * r, PAIR * (r + 1))
                 nc.vector.quantize_mx(
-                    out=h_codes[:, group, rows].bitcast(FP8X4),
-                    scales=h_scales[:, group, rows],
-                    in_=h_grouped[:],
+                    out=h_codes[:, g, rows].bitcast(FP8X4),
+                    scales=h_scales[:, g, rows],
+                    in_=pieces[piece][:],
                 )
 
-            pairs, passes, operands = load_stage(0)
+            units, operands = load_stage(0)
             loaded = load_stage(1)
-            units = [(pair, c) for pair in pairs for c in range(passes)]
-            for pair, c in units[:-GROUP_PASSES]:
-                transpose_and_quantise(pair, c)
+            for unit in units[:-GROUP_PASSES]:
+                transpose_and_quantise(unit)
             left_over = units[-GROUP_PASSES:]
 
             vec_bank = tbanks.tile([P, BANK], F32, tag="bank")
@@ -245,74 +248,46 @@ def tile_nodeupdatenetwork_pb_kernel(
                     banks, mean_var = tiles[q - 1]
                     std = standard_deviation(mean_var)
                 if 0 <= piece < HIDDEN_TILES:
-                    pieces.append(leaky_piece(normed_groups[piece // 4], piece % 4))
+                    pieces.append(leaky_piece(piece))
                 if normalising:
                     minus_gain_mean(mean_var, q - 1)
                     rstd = inverse(std)
-                if 1 <= piece <= HIDDEN_TILES:
-                    quantise_piece(pieces[piece - 1], (piece - 1) // 4, (piece - 1) % 4)
+                if multiplying:
+                    g, t = divmod(q, GROUP_TILES)
+                    if t == 0:
+                        w0_codes, w0_scales, x_codes, x_scales = operands
+                        units, operands = loaded
+                        units = left_over + units
+                        left_over = []
+                        if g + 2 <= GROUPS:
+                            loaded = load_stage(g + 2)
+                        v = normed.tile([P, GROUP_TILES, ROWS], F32)
+                        normed_groups.append(v)
+                    quarter = units[len(units) * t // GROUP_TILES : len(units) * (t + 1) // GROUP_TILES]
+                    stats = small.tile([P, 2, STATS], F32)
+                    for unit in quarter[: len(quarter) // 2]:
+                        transpose_and_quantise(unit)
                 if normalising:
                     scale_bias = scale_and_bias(rstd, q - 1)
                 if multiplying:
-                    group, t = divmod(q, TILES_PER_GROUP)
-                    if t == 0:
-                        w0_codes, w0_scales, x_codes, x_scales = operands
-                        pairs, passes, operands = loaded
-                        if group + 2 <= GROUPS:
-                            loaded = load_stage(group + 2)
-                        units = left_over + [(pair, c) for pair in pairs for c in range(passes)]
-                        left_over = []
-                        v = normed.tile([P, TILES_PER_GROUP, ROWS], F32)
-                        normed_groups.append(v)
-                    quarter = units[len(units) * t // TILES_PER_GROUP : len(units) * (t + 1) // TILES_PER_GROUP]
-                    stats = small.tile([P, 2, 6], F32)
-                    for pair, c in quarter[: len(quarter) // 2]:
-                        transpose_and_quantise(pair, c)
                     acc0 = multiply_half(w0_codes, w0_scales, x_codes, x_scales, GROUP_PASSES, t, 0, stats)
-                    for pair, c in quarter[len(quarter) // 2 :]:
-                        transpose_and_quantise(pair, c)
+                    for unit in quarter[len(quarter) // 2 :]:
+                        transpose_and_quantise(unit)
                 if normalising:
-                    normalise(banks, scale_bias, normed_groups[(q - 1) // 4][:, (q - 1) % 4, :])
+                    normalise(banks, scale_bias, normed_groups[(q - 1) // GROUP_TILES][:, (q - 1) % GROUP_TILES, :])
                 if multiplying:
                     acc1 = multiply_half(w0_codes, w0_scales, x_codes, x_scales, GROUP_PASSES, t, 1, stats)
+                if 1 <= piece <= HIDDEN_TILES:
+                    quantise_piece(piece - 1)
+                if multiplying:
                     tiles.append(([acc0, acc1], mean_and_variance(stats)))
 
         with ExitStack() as second:
             work = second.enter_context(tc.tile_pool(name="work", bufs=3))
             done = second.enter_context(tc.tile_pool(name="done", bufs=4))
-            stores = second.enter_context(tc.tile_pool(name="stores", bufs=4))
+            stores = second.enter_context(tc.tile_pool(name="stores", bufs=8))
             sums = second.enter_context(tc.psum_pool(name="sums2", bufs=6))
             tbanks = second.enter_context(tc.psum_pool(name="tbanks2", bufs=2))
-
-            def transpose_back(piece):
-                a, half = divmod(piece, 2)
-                banks = []
-                for j in range(2):
-                    bank = tbanks.tile([P, 2, 2, P], F32)
-                    for i in range(2):
-                        row_tile = 4 * half + 2 * j + i
-                        for e in range(2):
-                            nc.tensor.transpose(
-                                bank[:, i, e, :], out_tiles[2 * a + e][:, P * row_tile : P * (row_tile + 1)], ident[:]
-                            )
-                    banks.append(bank)
-                return banks
-
-            def store_piece(piece, banks):
-                a, half = divmod(piece, 2)
-                for j in range(2):
-                    by_row = stores.tile([P, 2, PAIR], F32)
-                    nc.scalar.copy(
-                        out=by_row[:].rearrange("p i (c e) -> p i c e", e=2),
-                        in_=banks[j][:].rearrange("p i e c -> p i c e"),
-                    )
-                    first_row = BANK * half + PAIR * j
-                    nc.sync.dma_start(
-                        out=out_rows[first_row : first_row + PAIR, PAIR * a : PAIR * (a + 1)].rearrange(
-                            "(i p) c -> p i c", p=P
-                        ),
-                        in_=by_row[:],
-                    )
 
             def leaky_half(dest, source, half):
                 r_cols = slice(BANK * half, BANK * (half + 1))
@@ -321,35 +296,69 @@ def tile_nodeupdatenetwork_pb_kernel(
                     op0=ALU.mult, op1=ALU.max,
                 )
 
+            def transpose_back(piece):
+                a, half = divmod(piece, 2)
+                banks = []
+                for b in range(2):
+                    bank = tbanks.tile([P, 2, 2, P], F32)
+                    for i in range(2):
+                        first_row = BANK * half + PAIR * b + P * i
+                        for e in range(2):
+                            nc.tensor.transpose(
+                                bank[:, i, e, :], out_tiles[2 * a + e][:, first_row : first_row + P], ident[:]
+                            )
+                    banks.append(bank)
+                return banks
+
+            def store_piece(piece):
+                a, half = divmod(piece, 2)
+                for b in range(2):
+                    by_row = stores.tile([P, 2, PAIR], F32)
+                    nc.scalar.copy(
+                        out=by_row[:].rearrange("p i (c e) -> p i c e", e=2),
+                        in_=back[piece][b][:].rearrange("p i e c -> p i c e"),
+                    )
+                    first_row = BANK * half + PAIR * b
+                    nc.sync.dma_start(
+                        out=out_rows[first_row : first_row + PAIR, PAIR * a : PAIR * (a + 1)].rearrange(
+                            "(i p) c -> p i c", p=P
+                        ),
+                        in_=by_row[:],
+                    )
+
             tiles = []
             normed_tiles = []
             out_tiles = []
             back = []
-            for j in range(OUT_TILES + 4):
-                normalising = 1 <= j <= OUT_TILES
+            for q in range(OUT_TILES + 4):
+                multiplying = q < OUT_TILES
+                normalising = 1 <= q <= OUT_TILES
+                finishing = 2 <= q <= OUT_TILES + 1
                 if normalising:
-                    banks, mean_var = tiles[j - 1]
+                    banks, mean_var = tiles[q - 1]
                     std = standard_deviation(mean_var)
-                if 2 <= j <= OUT_TILES + 1:
+                if finishing:
                     o1 = done.tile([P, ROWS], F32)
-                    leaky_half(o1, normed_tiles[j - 2], 0)
-                if normalising:
-                    minus_gain_mean(mean_var, HIDDEN_TILES + j - 1)
-                    rstd = inverse(std)
-                if 2 <= j <= OUT_TILES + 1:
-                    leaky_half(o1, normed_tiles[j - 2], 1)
                     out_tiles.append(o1)
-                if 4 <= j:
-                    store_piece(j - 4, back[j - 4])
+                    leaky_half(o1, normed_tiles[q - 2], 0)
                 if normalising:
-                    scale_bias = scale_and_bias(rstd, HIDDEN_TILES + j - 1)
+                    minus_gain_mean(mean_var, HIDDEN_TILES + q - 1)
+                    rstd = inverse(std)
+                if 4 <= q:
+                    store_piece(q - 4)
+                if multiplying:
+                    stats = small.tile([P, 2, STATS], F32)
+                    acc0 = multiply_half(w1_codes, w1_scales, h_codes, h_scales, HIDDEN_PASSES, q, 0, stats)
+                if normalising:
+                    scale_bias = scale_and_bias(rstd, HIDDEN_TILES + q - 1)
                     v1 = work.tile([P, ROWS], F32)
                     normalise(banks, scale_bias, v1[:])
                     normed_tiles.append(v1)
-                if j < OUT_TILES:
-                    stats = small.tile([P, 2, 6], F32)
-                    acc0 = multiply_half(w1_codes, w1_scales, h_codes, h_scales, HIDDEN_PASSES, j, 0, stats)
-                    acc1 = multiply_half(w1_codes, w1_scales, h_codes, h_scales, HIDDEN_PASSES, j, 1, stats)
+                if multiplying:
+                    acc1 = multiply_half(w1_codes, w1_scales, h_codes, h_scales, HIDDEN_PASSES, q, 1, stats)
+                if finishing:
+                    leaky_half(o1, normed_tiles[q - 2], 1)
+                if multiplying:
                     tiles.append(([acc0, acc1], mean_and_variance(stats)))
-                if 3 <= j <= OUT_TILES + 2:
-                    back.append(transpose_back(j - 3))
+                if 3 <= q <= OUT_TILES + 2:
+                    back.append(transpose_back(q - 3))

@@ -31,6 +31,27 @@ STATS = 6
 EPS_BN = 1e-5
 SLOPE = 0.01
 LEAKY_LAG = 5
+T_RING = [0, 1, 2, 3]
+L2_RING = [4, 5, 6, 7, 0, 1]
+OUT_RING = [2, 3]
+RG = 6
+PRO = 15
+E2 = 0
+DEFER = 76
+C_QUANT = [0,0,0,3,2,2,0,0,0]
+
+
+def KA(q):
+    return 2
+
+
+def QUOTA(q):
+    return 5 if q < 6 else 4 if q<14 else 3
+
+
+def VCOPY(q):
+    return 2 if q < 5 else None
+
 
 FLOPS = 2 * ROWS * GROUPS * GROUP_K * GROUP_OUT + 2 * ROWS * HIDDEN * OUT_CH
 
@@ -51,28 +72,53 @@ def tile_nodeupdatenetwork_pb_kernel(
 
         vec_rows = const.tile([P, 2 * P], BF16)
         nc.vector.memset(vec_rows[:], 0.0)
-        nc.scalar.dma_start(out=vec_rows[0:8, :], in_=gamma0.rearrange("(a w) -> a w", w=2 * P))
-        nc.scalar.dma_start(out=vec_rows[8:12, :], in_=gamma1.rearrange("(a w) -> a w", w=2 * P))
-        nc.scalar.dma_start(out=vec_rows[12:20, :], in_=beta0.rearrange("(a w) -> a w", w=2 * P))
-        nc.scalar.dma_start(out=vec_rows[20:24, :], in_=beta1.rearrange("(a w) -> a w", w=2 * P))
+
+        def load_vectors():
+            nc.sync.dma_start(out=vec_rows[0:8, :], in_=gamma0.rearrange("(a w) -> a w", w=2 * P))
+            nc.sync.dma_start(out=vec_rows[8:12, :], in_=gamma1.rearrange("(a w) -> a w", w=2 * P))
+            nc.sync.dma_start(out=vec_rows[12:20, :], in_=beta0.rearrange("(a w) -> a w", w=2 * P))
+            nc.sync.dma_start(out=vec_rows[20:24, :], in_=beta1.rearrange("(a w) -> a w", w=2 * P))
 
         ident = const.tile([P, P], F32)
         make_identity(nc, ident[:])
         eps = const.tile([P, 1], F32)
         nc.vector.memset(eps[:], EPS_BN)
         warm = const.tile([P, 1], F32)
-        nc.scalar.activation(out=warm[:], in_=eps[:], func=ACT.Sqrt)
+        nc.scalar.activation(out=warm[:], in_=eps[:], func=ACT.Abs_reciprocal_sqrt)
+
+        n_tiles = HIDDEN_TILES + OUT_TILES
+        vec_cols = const.tile([P, 2 * P], BF16)
+        gain_mean = const.tile([P, n_tiles, 2], F32)
+        minus_gain = const.tile([P, n_tiles], F32)
+        zero_shift = const.tile([P, n_tiles, 2], F32)
+
+        def spread_vectors():
+            vec_bank = psum_bank(T_RING[counts["t"] % len(T_RING)])
+            counts["t"] += 1
+            nc.tensor.transpose(vec_bank[:, 0:P], vec_rows[:].bitcast(F32), ident[:])
+            nc.vector.tensor_copy(out=vec_cols[:].bitcast(F32), in_=vec_bank[:, 0:P])
+            nc.gpsimd.tensor_copy(out=gain_mean[:, :, 0], in_=vec_cols[:, 0:n_tiles])
+            nc.gpsimd.tensor_scalar(
+                out=minus_gain[:], in0=vec_cols[:, 0:n_tiles], scalar1=-1.0, scalar2=None, op0=ALU.mult
+            )
+            nc.gpsimd.memset(zero_shift[:], 0.0)
+            nc.gpsimd.tensor_copy(out=zero_shift[:, :, 1], in_=vec_cols[:, n_tiles : 2 * n_tiles])
 
         w1_codes = kept.tile([P, HIDDEN_PASSES, OUT_CH], U32, align_bytes=64)
         w1_scales = kept.tile([P, HIDDEN_PASSES, OUT_CH], U8, align_bytes=64)
         h_codes = kept.tile([P, HIDDEN_PASSES, ROWS], U32, align_bytes=64)
         h_scales = kept.tile([P, HIDDEN_PASSES, ROWS], U8, align_bytes=64)
 
-        def multiply_half(w_codes, w_scales, a_codes, a_scales, passes, w_tile, half, stats):
+        banks = whole.enter_context(tc.psum_pool(name="banks", bufs=1))
+
+        def psum_bank(k):
+            bank = banks.tile([P, BANK], F32, tag="bank%d" % k)
+            return bank
+
+        def multiply(acc, w_codes, w_scales, a_codes, a_scales, passes, first, last, w_tile, half):
             w_cols = slice(P * w_tile, P * (w_tile + 1))
             r_cols = slice(BANK * half, BANK * (half + 1))
-            acc = sums.tile([P, BANK], F32)
-            for c in range(passes):
+            for c in range(first, last):
                 nc.tensor.matmul_mx(
                     out=acc[:],
                     lhsT=w_codes[:, c, w_cols].bitcast(FP8X4),
@@ -82,29 +128,25 @@ def tile_nodeupdatenetwork_pb_kernel(
                     start=(c == 0),
                     stop=(c == passes - 1),
                 )
+
+        def half_statistics(stats, half, acc):
             nc.vector.bn_stats(out=stats[:, half, :], in_=acc[:])
-            return acc
 
         def mean_and_variance(stats):
             mean_var = small.tile([P, 2], F32)
             nc.vector.bn_aggr(out=mean_var[:], in_=stats[:].rearrange("p h s -> p (h s)"))
             return mean_var
 
-        def standard_deviation(mean_var):
-            std = small.tile([P, 1], F32)
-            nc.scalar.activation(out=std[:], in_=mean_var[:, 1:2], func=ACT.Sqrt, bias=eps[:, 0:1])
-            return std
-
-        def inverse(std):
-            rstd = small.tile([P, 1], F32)
-            nc.vector.reciprocal(out=rstd[:], in_=std[:])
-            return rstd
-
-        def minus_gain_mean(mean_var, tile_index):
-            nc.vector.tensor_scalar(
+        def inverse_deviation(mean_var, tile_index):
+            nc.gpsimd.tensor_scalar(
                 out=gain_mean[:, tile_index, 1:2], in0=mean_var[:, 0:1],
                 scalar1=minus_gain[:, tile_index : tile_index + 1], scalar2=None, op0=ALU.mult,
             )
+            rstd = small.tile([P, 1], F32)
+            nc.scalar.activation(
+                out=rstd[:], in_=mean_var[:, 1:2], func=ACT.Abs_reciprocal_sqrt, bias=eps[:, 0:1]
+            )
+            return rstd
 
         def scale_and_bias(rstd, tile_index):
             scale_bias = small.tile([P, 2], F32)
@@ -114,52 +156,60 @@ def tile_nodeupdatenetwork_pb_kernel(
             )
             return scale_bias
 
-        def normalise(banks, scale_bias, dest):
-            for half in range(2):
-                nc.scalar.activation(
-                    out=dest[:, BANK * half : BANK * (half + 1)], in_=banks[half][:],
-                    func=ACT.Identity, scale=scale_bias[:, 0:1], bias=scale_bias[:, 1:2],
+        def normalise(acc, scale_bias, dest):
+            nc.scalar.activation(
+                out=dest, in_=acc[:], func=ACT.Identity, scale=scale_bias[:, 0:1], bias=scale_bias[:, 1:2]
+            )
+
+        def normalise_v(acc, scale_bias, dest):
+            nc.vector.tensor_scalar(
+                out=dest, in0=acc[:], scalar1=scale_bias[:, 0:1], scalar2=scale_bias[:, 1:2],
+                op0=ALU.mult, op1=ALU.add,
+            )
+
+        regroup = whole.enter_context(tc.tile_pool(name="regroup", bufs=RG))
+        w1_raw = whole.enter_context(tc.tile_pool(name="w1_raw", bufs=2))
+        w1_grouped = whole.enter_context(tc.tile_pool(name="w1_grouped", bufs=12))
+        h_pool = whole.enter_context(tc.tile_pool(name="h_pool", bufs=4))
+        normed = whole.enter_context(tc.tile_pool(name="normed", bufs=2))
+        with ExitStack() as inner:
+            raw = inner.enter_context(tc.tile_pool(name="raw", bufs=8))
+            staged = inner.enter_context(tc.tile_pool(name="staged", bufs=2))
+
+            def load_rows(pool, source, first_row, first_k, width, dest_col, tile_):
+                nc.sync.dma_start(
+                    out=tile_[:, :, dest_col : dest_col + width],
+                    in_=source[first_row : first_row + PAIR, first_k : first_k + width].rearrange("(p e) k -> p e k", e=2),
                 )
 
-        with ExitStack() as first:
-            raw = first.enter_context(tc.tile_pool(name="raw", bufs=10))
-            staged = first.enter_context(tc.tile_pool(name="staged", bufs=2))
-            regroup = first.enter_context(tc.tile_pool(name="regroup", bufs=6))
-            normed = first.enter_context(tc.tile_pool(name="normed", bufs=2))
-            tbanks = first.enter_context(tc.psum_pool(name="tbanks", bufs=4))
-            sums = first.enter_context(tc.psum_pool(name="sums", bufs=4))
+            stage_tiles = []
+            stream = []
 
             def load_stage(stage):
-                if stage == GROUPS:
-                    units = []
-                    for a in range(OUT_TILES // 2):
-                        w1_pair = raw.tile([P, 2, HIDDEN], BF16, tag="pair")
-                        nc.sync.dma_start(
-                            out=w1_pair[:],
-                            in_=w1[PAIR * a : PAIR * (a + 1), :].rearrange("(p e) k -> p e k", e=2),
-                        )
-                        units.extend([(w1_pair, c, w1_codes, w1_scales, PAIR * a) for c in range(HIDDEN_PASSES)])
-                    return units, None
                 w0_codes = staged.tile([P, GROUP_PASSES, GROUP_OUT], U32, align_bytes=64)
                 w0_scales = staged.tile([P, GROUP_PASSES, GROUP_OUT], U8, align_bytes=64)
                 x_codes = staged.tile([P, GROUP_PASSES, ROWS], U32, align_bytes=64)
                 x_scales = staged.tile([P, GROUP_PASSES, ROWS], U8, align_bytes=64)
+                stage_tiles.append((w0_codes, w0_scales, x_codes, x_scales))
 
                 def load_w0(a):
                     first_row = GROUP_OUT * stage + PAIR * a
-                    w0_pair = raw.tile([P, 2, HIDDEN], BF16, tag="pair")
-                    nc.sync.dma_start(
-                        out=w0_pair[:, :, 0:GROUP_K],
-                        in_=w0[first_row : first_row + PAIR, :].rearrange("(p e) k -> p e k", e=2),
-                    )
-                    return [(w0_pair, c, w0_codes, w0_scales, PAIR * a) for c in range(GROUP_PASSES)]
+                    w0_pair = raw.tile([P, 2, GROUP_K], BF16, tag="pair")
+                    cuts = GROUP_PASSES if (stage == 0 and a == 0) else 1
+                    for j in range(cuts):
+                        ks = slice(GROUP_K // cuts * j, GROUP_K // cuts * (j + 1))
+                        nc.sync.dma_start(
+                            out=w0_pair[:, :, ks],
+                            in_=w0[first_row : first_row + PAIR, ks].rearrange("(p e) k -> p e k", e=2),
+                        )
+                    stream.extend([(w0_pair, c, w0_codes, w0_scales, PAIR * a) for c in range(GROUP_PASSES)])
 
-                units = load_w0(0)
+                load_w0(0)
                 k0 = GROUP_K * stage
                 from_node = max(0, min(NODE_K - k0, GROUP_K))
                 for r in range(ROWS // PAIR):
                     rows = slice(PAIR * r, PAIR * (r + 1))
-                    x_pair = raw.tile([P, 2, HIDDEN], BF16, tag="pair")
+                    x_pair = raw.tile([P, 2, GROUP_K], BF16, tag="pair")
                     if from_node > 0:
                         nc.sync.dma_start(
                             out=x_pair[:, :, 0:from_node],
@@ -172,40 +222,96 @@ def tile_nodeupdatenetwork_pb_kernel(
                                 "(i p) k -> p i k", p=P
                             ),
                         )
-                    units.extend([(x_pair, c, x_codes, x_scales, PAIR * r) for c in range(GROUP_PASSES)])
-                units.extend(load_w0(1))
-                return units, (w0_codes, w0_scales, x_codes, x_scales)
+                    stream.extend([(x_pair, c, x_codes, x_scales, PAIR * r) for c in range(GROUP_PASSES)])
+                load_w0(1)
 
-            def transpose_and_quantise(unit):
+            def load_w1(a):
+                w1_pair = w1_raw.tile([P, 2, HIDDEN], BF16)
+                nc.sync.dma_start(
+                    out=w1_pair[:],
+                    in_=w1[PAIR * a : PAIR * (a + 1), :].rearrange("(p e) k -> p e k", e=2),
+                )
+                stream.extend([(w1_pair, c, w1_codes, w1_scales, PAIR * a) for c in range(HIDDEN_PASSES)])
+
+            counts = {"t": 0}
+
+            def transpose_in(unit):
                 pair, c, codes, scales, col0 = unit
-                bank = tbanks.tile([P, 2, PAIR], F32, tag="bank")
+                bank = psum_bank(T_RING[counts["t"] % len(T_RING)])
+                counts["t"] += 1
+                by_word = bank[:].rearrange("p (u n) -> p u n", u=2)
                 for i in range(2):
                     words = pair[:, i, :].bitcast(F32)
                     for u in range(2):
                         first_word = PASS_WORDS * c + P * u
                         nc.tensor.transpose(
-                            bank[:, u, P * i : P * (i + 1)], words[:, first_word : first_word + P], ident[:]
+                            by_word[:, u, P * i : P * (i + 1)], words[:, first_word : first_word + P], ident[:]
                         )
-                grouped = regroup.tile([P, 4 * PAIR], BF16, align_bytes=64)
-                nc.scalar.copy(
-                    out=grouped[:].bitcast(F32).rearrange("p (n u) -> p n u", u=2),
-                    in_=bank[:].rearrange("p u n -> p n u"),
-                )
+                return bank
+
+            def group_words(bank, on_vector, later=False):
+                if later:
+                    grouped = w1_grouped.tile([P, 4 * PAIR], BF16, align_bytes=64, tag="later")
+                else:
+                    grouped = regroup.tile([P, 4 * PAIR], BF16, align_bytes=64, tag="now")
+                dest = grouped[:].bitcast(F32).rearrange("p (n u) -> p n u", u=2)
+                src = bank[:].rearrange("p (u n) -> p n u", u=2)
+                if on_vector:
+                    nc.vector.tensor_copy(out=dest, in_=src)
+                else:
+                    nc.scalar.copy(out=dest, in_=src)
+                return grouped
+
+            def quantise(unit, grouped):
+                pair, c, codes, scales, col0 = unit
                 nc.vector.quantize_mx(
                     out=codes[:, c, col0 : col0 + PAIR].bitcast(FP8X4),
                     scales=scales[:, c, col0 : col0 + PAIR],
                     in_=grouped[:],
                 )
 
+            normed_groups = []
+            pieces = []
+            deferred = []
+
+            def quant_or_defer(unit, grouped, later):
+                if later:
+                    deferred.append((unit, grouped))
+                else:
+                    quantise(unit, grouped)
+
+            def quant_deferred(n):
+                for unit, grouped in deferred[:n]:
+                    quantise(unit, grouped)
+                del_n = deferred[n:]
+                deferred.clear()
+                deferred.extend(del_n)
+
+            def leaky_scalar(piece, pool):
+                g, r = divmod(piece, ROWS // PAIR)
+                v_by_row = normed_groups[g][:, :, PAIR * r : PAIR * (r + 1)].rearrange("p t n -> p n t")
+                up = pool.tile([P, 4 * PAIR], BF16, align_bytes=64)
+                down = pool.tile([P, 4 * PAIR], BF16, align_bytes=64)
+                nc.scalar.activation(out=up[:].rearrange("p (n t) -> p n t", t=GROUP_TILES), in_=v_by_row, func=ACT.Copy)
+                nc.scalar.activation(
+                    out=down[:].rearrange("p (n t) -> p n t", t=GROUP_TILES), in_=v_by_row, func=ACT.Copy, scale=SLOPE
+                )
+                return up, down
+
+            def leaky_max(up, down):
+                h_grouped = h_pool.tile([P, 4 * PAIR], BF16, align_bytes=64)
+                nc.vector.tensor_tensor(out=h_grouped[:], in0=up[:], in1=down[:], op=ALU.max)
+                pieces.append(h_grouped)
+
             def leaky_piece(piece):
                 g, r = divmod(piece, ROWS // PAIR)
-                h_grouped = regroup.tile([P, 4 * PAIR], BF16, align_bytes=64)
+                h_grouped = h_pool.tile([P, 4 * PAIR], BF16, align_bytes=64)
                 v_by_row = normed_groups[g][:, :, PAIR * r : PAIR * (r + 1)].rearrange("p t n -> p n t")
                 nc.vector.scalar_tensor_tensor(
                     out=h_grouped[:].rearrange("p (n t) -> p n t", t=GROUP_TILES),
                     in0=v_by_row, scalar=SLOPE, in1=v_by_row, op0=ALU.mult, op1=ALU.max,
                 )
-                return h_grouped
+                pieces.append(h_grouped)
 
             def quantise_piece(piece):
                 g, r = divmod(piece, ROWS // PAIR)
@@ -216,149 +322,259 @@ def tile_nodeupdatenetwork_pb_kernel(
                     in_=pieces[piece][:],
                 )
 
-            units, operands = load_stage(0)
-            loaded = load_stage(1)
-            for unit in units[:-GROUP_PASSES]:
-                transpose_and_quantise(unit)
-            left_over = units[-GROUP_PASSES:]
+            load_stage(0)
+            load_vectors()
+            load_stage(1)
 
-            vec_bank = tbanks.tile([P, BANK], F32, tag="bank")
-            nc.tensor.transpose(vec_bank[:, 0:P], vec_rows[:].bitcast(F32), ident[:])
-            vec_cols = const.tile([P, 2 * P], BF16)
-            nc.vector.tensor_copy(out=vec_cols[:].bitcast(F32), in_=vec_bank[:, 0:P])
-            n_tiles = HIDDEN_TILES + OUT_TILES
-            gain_mean = const.tile([P, n_tiles, 2], F32)
-            nc.vector.tensor_copy(out=gain_mean[:, :, 0], in_=vec_cols[:, 0:n_tiles])
-            minus_gain = const.tile([P, n_tiles], F32)
-            nc.vector.tensor_scalar(
-                out=minus_gain[:], in0=vec_cols[:, 0:n_tiles], scalar1=-1.0, scalar2=None, op0=ALU.mult
-            )
-            zero_shift = const.tile([P, n_tiles, 2], F32)
-            nc.vector.memset(zero_shift[:], 0.0)
-            nc.vector.tensor_copy(out=zero_shift[:, :, 1], in_=vec_cols[:, n_tiles : 2 * n_tiles])
+            def step(unit, v=False):
+                b = transpose_in(unit)
+                g = group_words(b, v)
+                quantise(unit, g)
 
-            tiles = []
-            normed_groups = []
-            pieces = []
-            for q in range(HIDDEN_TILES + LEAKY_LAG + 2):
-                multiplying = q < HIDDEN_TILES
-                normalising = 1 <= q <= HIDDEN_TILES
-                piece = q - LEAKY_LAG
-                if normalising:
-                    banks, mean_var = tiles[q - 1]
-                    std = standard_deviation(mean_var)
-                if 0 <= piece < HIDDEN_TILES:
-                    pieces.append(leaky_piece(piece))
-                if normalising:
-                    minus_gain_mean(mean_var, q - 1)
-                    rstd = inverse(std)
-                if multiplying:
-                    g, t = divmod(q, GROUP_TILES)
-                    if t == 0:
-                        w0_codes, w0_scales, x_codes, x_scales = operands
-                        units, operands = loaded
-                        units = left_over + units
-                        left_over = []
-                        if g + 2 <= GROUPS:
-                            loaded = load_stage(g + 2)
-                        v = normed.tile([P, GROUP_TILES, ROWS], F32)
-                        normed_groups.append(v)
-                    quarter = units[len(units) * t // GROUP_TILES : len(units) * (t + 1) // GROUP_TILES]
+            pos = 0
+            for n, unit in enumerate(stream[0:PRO]):
+                step(unit, False)
+            pos = PRO
+            spread_vectors()
+
+            accs = {}
+            stats_of = {}
+            mv = {}
+            rs = {}
+            sb = {}
+
+            def matmul_half(q, half):
+                g, t = divmod(q, GROUP_TILES)
+                w0_codes, w0_scales, x_codes, x_scales = stage_tiles[g]
+                acc = psum_bank(4 + (2 * q + half) % 4)
+                multiply(acc, w0_codes, w0_scales, x_codes, x_scales, GROUP_PASSES, 0, GROUP_PASSES, t, half)
+                accs[q, half] = acc
+
+            def bn_half(q, half):
+                if half == 0:
                     stats = small.tile([P, 2, STATS], F32)
-                    for unit in quarter[: len(quarter) // 2]:
-                        transpose_and_quantise(unit)
-                if normalising:
-                    scale_bias = scale_and_bias(rstd, q - 1)
-                if multiplying:
-                    acc0 = multiply_half(w0_codes, w0_scales, x_codes, x_scales, GROUP_PASSES, t, 0, stats)
-                    for unit in quarter[len(quarter) // 2 :]:
-                        transpose_and_quantise(unit)
-                if normalising:
-                    normalise(banks, scale_bias, normed_groups[(q - 1) // GROUP_TILES][:, (q - 1) % GROUP_TILES, :])
-                if multiplying:
-                    acc1 = multiply_half(w0_codes, w0_scales, x_codes, x_scales, GROUP_PASSES, t, 1, stats)
-                if 1 <= piece <= HIDDEN_TILES:
-                    quantise_piece(piece - 1)
-                if multiplying:
-                    tiles.append(([acc0, acc1], mean_and_variance(stats)))
+                    stats_of[q] = stats
+                half_statistics(stats_of[q], half, accs[q, half])
 
+            def norm_half(q, half):
+                normalise(accs[q, half], sb[q], normed_groups[q // 4][:, q % 4, BANK * half : BANK * (half + 1)])
+
+            accs2 = {}
+
+            def l2(q, half, first, last):
+                if first == 0:
+                    accs2[q, half] = psum_bank(L2_RING[(2 * q + half) % len(L2_RING)])
+                multiply(accs2[q, half], w1_codes, w1_scales, h_codes, h_scales, HIDDEN_PASSES, first, last, q, half)
+
+            for q in range(HIDDEN_TILES):
+                g, t = divmod(q, GROUP_TILES)
+                if t == 0:
+                    if g + 2 < GROUPS:
+                        load_stage(g + 2)
+                    elif g + 2 == GROUPS:
+                        for a in range(4):
+                            load_w1(a)
+                    v = normed.tile([P, GROUP_TILES, ROWS], F32)
+                    normed_groups.append(v)
+                piece = q - LEAKY_LAG
+                n_units = QUOTA(q)
+                us = stream[pos : pos + n_units]
+                first = pos
+                pos += n_units
+                vec = VCOPY(q)
+                k = KA(q)
+
+                def isl(j):
+                    return first + j >= DEFER
+
+                tb = [transpose_in(u) for u in us[:k]]
+                if piece >= 0:
+                    leaky_piece(piece)
+                gs = [group_words(tb[0], 0 == vec, isl(0))]
+                if q >= 1:
+                    rs[q - 1] = inverse_deviation(mv[q - 1], q - 1)
+                for j in range(1, k):
+                    gs.append(group_words(tb[j], j == vec, isl(j)))
+                if q >= 1:
+                    sb[q - 1] = scale_and_bias(rs[q - 1], q - 1)
+                for j in range(k):
+                    quant_or_defer(us[j], gs[j], isl(j))
+                matmul_half(q, 0)
+                tb += [transpose_in(u) for u in us[k:]]
+                for j in range(k, len(us) - 1):
+                    gs.append(group_words(tb[j], j == vec, isl(j)))
+                bn_half(q, 0)
+                for j in range(k, len(us) - 1):
+                    quant_or_defer(us[j], gs[j], isl(j))
+                if q >= 1:
+                    norm_half(q - 1, 0)
+                    norm_half(q - 1, 1)
+                gs.append(group_words(tb[-1], False, isl(len(us) - 1)))
+                matmul_half(q, 1)
+                if piece >= 1:
+                    quantise_piece(piece - 1)
+                bn_half(q, 1)
+                if q == 15:
+                    quantise_piece(10)
+                quant_or_defer(us[-1], gs[-1], isl(len(us) - 1))
+                mv[q] = mean_and_variance(stats_of[q])
+            rest = stream[pos:]
+
+            def prepare(us):
+                for u in us:
+                    b = transpose_in(u)
+                    quant_or_defer(u, group_words(b, False, True), True)
+
+            rs[15] = inverse_deviation(mv[15], 15)
+            leaky_piece(11)
+            prepare(rest[:2])
+            sb[15] = scale_and_bias(rs[15], 15)
+            norm_half(15, 0)
+            norm_half(15, 1)
+            quantise_piece(11)
+            quant_deferred(4)
+            l2(0, 0, 0, 3)
+            l2(0, 1, 0, 3)
         with ExitStack() as second:
             work = second.enter_context(tc.tile_pool(name="work", bufs=3))
             done = second.enter_context(tc.tile_pool(name="done", bufs=4))
             stores = second.enter_context(tc.tile_pool(name="stores", bufs=8))
-            sums = second.enter_context(tc.psum_pool(name="sums2", bufs=6))
-            tbanks = second.enter_context(tc.psum_pool(name="tbanks2", bufs=2))
+            v1s = {}
+            o1s = {}
 
-            def leaky_half(dest, source, half):
+            def lh(q, half, dest=None):
+                if half == 0:
+                    o1 = done.tile([P, ROWS], F32)
+                    o1s[q] = o1
                 r_cols = slice(BANK * half, BANK * (half + 1))
                 nc.vector.scalar_tensor_tensor(
-                    out=dest[:, r_cols], in0=source[:, r_cols], scalar=SLOPE, in1=source[:, r_cols],
+                    out=o1s[q][:, r_cols], in0=v1s[q][:, r_cols], scalar=SLOPE, in1=v1s[q][:, r_cols],
                     op0=ALU.mult, op1=ALU.max,
                 )
 
-            def transpose_back(piece):
+            back = {}
+
+            def tback(piece, ring):
                 a, half = divmod(piece, 2)
-                banks = []
+                bs = []
                 for b in range(2):
-                    bank = tbanks.tile([P, 2, 2, P], F32)
+                    bank = psum_bank(ring[b])
+                    view = bank[:].rearrange("p (i e c) -> p i e c", i=2, e=2)
                     for i in range(2):
                         first_row = BANK * half + PAIR * b + P * i
                         for e in range(2):
                             nc.tensor.transpose(
-                                bank[:, i, e, :], out_tiles[2 * a + e][:, first_row : first_row + P], ident[:]
+                                view[:, i, e, :], o1s[2 * a + e][:, first_row : first_row + P], ident[:]
                             )
-                    banks.append(bank)
-                return banks
+                    bs.append(bank)
+                back[piece] = bs
 
-            def store_piece(piece):
+            def store(piece, b, on_vector=False):
                 a, half = divmod(piece, 2)
-                for b in range(2):
-                    by_row = stores.tile([P, 2, PAIR], F32)
-                    nc.scalar.copy(
-                        out=by_row[:].rearrange("p i (c e) -> p i c e", e=2),
-                        in_=back[piece][b][:].rearrange("p i e c -> p i c e"),
-                    )
-                    first_row = BANK * half + PAIR * b
-                    nc.sync.dma_start(
-                        out=out_rows[first_row : first_row + PAIR, PAIR * a : PAIR * (a + 1)].rearrange(
-                            "(i p) c -> p i c", p=P
-                        ),
-                        in_=by_row[:],
-                    )
+                by_row = stores.tile([P, 2, PAIR], F32)
+                dest = by_row[:].rearrange("p i (c e) -> p i c e", e=2)
+                src = back[piece][b][:].rearrange("p (i e c) -> p i c e", i=2, e=2)
+                if on_vector:
+                    nc.vector.tensor_copy(out=dest, in_=src)
+                else:
+                    nc.scalar.copy(out=dest, in_=src)
+                first_row = BANK * half + PAIR * b
+                nc.sync.dma_start(
+                    out=out_rows[first_row : first_row + PAIR, PAIR * a : PAIR * (a + 1)].rearrange(
+                        "(i p) c -> p i c", p=P
+                    ),
+                    in_=by_row[:],
+                )
 
-            tiles = []
-            normed_tiles = []
-            out_tiles = []
-            back = []
-            for q in range(OUT_TILES + 4):
-                multiplying = q < OUT_TILES
-                normalising = 1 <= q <= OUT_TILES
-                finishing = 2 <= q <= OUT_TILES + 1
-                if normalising:
-                    banks, mean_var = tiles[q - 1]
-                    std = standard_deviation(mean_var)
-                if finishing:
-                    o1 = done.tile([P, ROWS], F32)
-                    out_tiles.append(o1)
-                    leaky_half(o1, normed_tiles[q - 2], 0)
-                if normalising:
-                    minus_gain_mean(mean_var, HIDDEN_TILES + q - 1)
-                    rstd = inverse(std)
-                if 4 <= q:
-                    store_piece(q - 4)
-                if multiplying:
-                    stats = small.tile([P, 2, STATS], F32)
-                    acc0 = multiply_half(w1_codes, w1_scales, h_codes, h_scales, HIDDEN_PASSES, q, 0, stats)
-                if normalising:
-                    scale_bias = scale_and_bias(rstd, HIDDEN_TILES + q - 1)
+            mv2 = {}
+            rs2 = {}
+            sb2 = {}
+
+            def norm2(q, half):
+                if half == 0:
                     v1 = work.tile([P, ROWS], F32)
-                    normalise(banks, scale_bias, v1[:])
-                    normed_tiles.append(v1)
-                if multiplying:
-                    acc1 = multiply_half(w1_codes, w1_scales, h_codes, h_scales, HIDDEN_PASSES, q, 1, stats)
-                if finishing:
-                    leaky_half(o1, normed_tiles[q - 2], 1)
-                if multiplying:
-                    tiles.append(([acc0, acc1], mean_and_variance(stats)))
-                if 3 <= q <= OUT_TILES + 2:
-                    back.append(transpose_back(q - 3))
+                    v1s[q] = v1
+                normalise(accs2[q, half], sb2[q], v1s[q][:, BANK * half : BANK * (half + 1)])
+
+            acc2_stats = {}
+
+            def bn2(q, half):
+                if half == 0:
+                    stats = small.tile([P, 2, STATS], F32)
+                    acc2_stats[q] = stats
+                half_statistics(acc2_stats[q], half, accs2[q, half])
+
+            tb = [transpose_in(u) for u in rest[2:5]]
+            l2(1, 0, 0, 3)
+            l2(1, 1, 0, 3)
+            leaky_piece(12)
+            leaky_piece(13)
+            up, down = leaky_scalar(14, stores)
+            quantise_piece(12)
+            quantise_piece(13)
+            l2(0, 0, 3, 4)
+            l2(1, 0, 3, 4)
+            for j, u in enumerate(rest[2:5]):
+                quant_or_defer(u, group_words(tb[j], False, True), True)
+            leaky_max(up, down)
+            leaky_piece(15)
+            prepare(rest[5:])
+            bn2(0, 0)
+            quantise_piece(14)
+            quantise_piece(15)
+            l2(0, 1, 3, 4)
+            l2(1, 1, 3, 4)
+            bn2(1, 0)
+            quant_deferred(1)
+            bn2(0, 1)
+            quant_deferred(1)
+            mv2[0] = mean_and_variance(acc2_stats[0])
+            rs2[0] = inverse_deviation(mv2[0], HIDDEN_TILES)
+            bn2(1, 1)
+            sb2[0] = scale_and_bias(rs2[0], HIDDEN_TILES)
+            norm2(0, 0)
+            norm2(0, 1)
+            quant_deferred(1)
+            mv2[1] = mean_and_variance(acc2_stats[1])
+            rs2[1] = inverse_deviation(mv2[1], HIDDEN_TILES + 1)
+            quant_deferred(1)
+            sb2[1] = scale_and_bias(rs2[1], HIDDEN_TILES + 1)
+            norm2(1, 0)
+            norm2(1, 1)
+
+            for q in range(2, OUT_TILES + 1):
+                mul = q < OUT_TILES
+                if q >= 4:
+                    store(q - 4, 0)
+                lh(q - 2, 0)
+                if q >= 3:
+                    mv2[q - 1] = mean_and_variance(acc2_stats[q - 1])
+                    rs2[q - 1] = inverse_deviation(mv2[q - 1], HIDDEN_TILES + q - 1)
+                if mul:
+                    l2(q, 0, E2 if q == 2 else 0, 4)
+                    bn2(q, 0)
+                if q >= 3:
+                    sb2[q - 1] = scale_and_bias(rs2[q - 1], HIDDEN_TILES + q - 1)
+                quant_deferred(C_QUANT[q])
+                if q >= 4:
+                    store(q - 4, 1)
+                if q >= 3:
+                    norm2(q - 1, 0)
+                    norm2(q - 1, 1)
+                if mul:
+                    l2(q, 1, E2 if q == 2 else 0, 4)
+                lh(q - 2, 1)
+                if mul:
+                    bn2(q, 1)
+                if q >= 3:
+                    tback(q - 3, OUT_RING)
+            lh(7, 0)
+            tback(6, [4, 5])
+            store(5, 0)
+            store(5, 1)
+            lh(7, 1)
+            tback(7, [6, 7])
+            store(6, 0)
+            store(6, 1, True)
+            store(7, 0)
+            store(7, 1, True)

@@ -97,12 +97,12 @@ def tile_nodeupdatenetwork_pb_kernel(
             counts["t"] += 1
             nc.tensor.transpose(vec_bank[:, 0:P], vec_rows[:].bitcast(F32), ident[:])
             nc.vector.tensor_copy(out=vec_cols[:].bitcast(F32), in_=vec_bank[:, 0:P])
-            nc.gpsimd.tensor_copy(out=gain_mean[:, :, 0], in_=vec_cols[:, 0:n_tiles])
-            nc.gpsimd.tensor_scalar(
+            nc.vector.tensor_copy(out=gain_mean[:, :, 0], in_=vec_cols[:, 0:n_tiles])
+            nc.vector.tensor_scalar(
                 out=minus_gain[:], in0=vec_cols[:, 0:n_tiles], scalar1=-1.0, scalar2=None, op0=ALU.mult
             )
-            nc.gpsimd.memset(zero_shift[:], 0.0)
-            nc.gpsimd.tensor_copy(out=zero_shift[:, :, 1], in_=vec_cols[:, n_tiles : 2 * n_tiles])
+            nc.vector.memset(zero_shift[:], 0.0)
+            nc.vector.tensor_copy(out=zero_shift[:, :, 1], in_=vec_cols[:, n_tiles : 2 * n_tiles])
 
         w1_codes = kept.tile([P, HIDDEN_PASSES, OUT_CH], U32, align_bytes=64)
         w1_scales = kept.tile([P, HIDDEN_PASSES, OUT_CH], U8, align_bytes=64)
@@ -138,13 +138,13 @@ def tile_nodeupdatenetwork_pb_kernel(
             return mean_var
 
         def inverse_deviation(mean_var, tile_index):
-            nc.gpsimd.tensor_scalar(
-                out=gain_mean[:, tile_index, 1:2], in0=mean_var[:, 0:1],
-                scalar1=minus_gain[:, tile_index : tile_index + 1], scalar2=None, op0=ALU.mult,
-            )
             rstd = small.tile([P, 1], F32)
             nc.scalar.activation(
                 out=rstd[:], in_=mean_var[:, 1:2], func=ACT.Abs_reciprocal_sqrt, bias=eps[:, 0:1]
+            )
+            nc.scalar.activation(
+                out=gain_mean[:, tile_index, 1:2], in_=mean_var[:, 0:1], func=ACT.Identity,
+                scale=minus_gain[:, tile_index : tile_index + 1],
             )
             return rstd
 

@@ -30,28 +30,30 @@ PAIR = 256
 STATS = 6
 EPS_BN = 1e-5
 SLOPE = 0.01
-LEAKY_LAG = 5
-T_RING = [0, 1, 2, 3]
-L2_RING = [4, 5, 6, 7, 0, 1]
-OUT_RING = [2, 3]
+
 RG = 6
-PRO = 15
-E2 = 0
-DEFER = 76
-C_QUANT = [0,0,0,3,2,2,0,0,0]
-
-
-def KA(q):
-    return 2
-
-
-def QUOTA(q):
-    return 5 if q < 6 else 4 if q<14 else 3
-
-
-def VCOPY(q):
-    return 2 if q < 5 else None
-
+LAGB = 3
+HEAD_UNITS = 15
+LATER = 76
+DEF0 = 4
+LATE_Q = [0, 0, 0, 3, 2, 2, 0, 0, 0]
+RINGS = {"in": [0, 1, 2, 3], "sum": [4, 5, 6, 7], "sum2": [4, 5, 6, 7, 0, 1], "out": [2, 3], "tail": [4, 5, 6, 7]}
+ROUNDS = [([(0, 0), (0, 1)], 5, None, [2], 5),
+          ([(1, 0), (1, 1)], 5, None, [2], 5),
+          ([(2, 0), (2, 1)], 5, None, [2], 5),
+          ([(3, 0), (3, 1)], 5, None, [2], 5),
+          ([(4, 0), (4, 1)], 5, None, [2], 5),
+          ([(5, 0), (5, 1)], 5, 0, [], 2),
+          ([(6, 0), (6, 1)], 4, 1, [], 2),
+          ([(7, 0), (7, 1)], 4, 2, [], 2),
+          ([(8, 0), (8, 1)], 4, 3, [], 2),
+          ([(9, 0), (9, 1)], 4, 4, [], 2),
+          ([(10, 0), (10, 1)], 4, 5, [], 2),
+          ([(11, 0), (11, 1)], 4, 6, [], 2),
+          ([(12, 0), (12, 1)], 4, 7, [], 2),
+          ([(13, 0), (13, 1)], 4, 8, [], 2),
+          ([(14, 0), (14, 1)], 3, 9, [], 2),
+          ([(15, 0), (15, 1)], 3, 10, [], 2)]
 
 FLOPS = 2 * ROWS * GROUPS * GROUP_K * GROUP_OUT + 2 * ROWS * HIDDEN * OUT_CH
 
@@ -69,15 +71,11 @@ def tile_nodeupdatenetwork_pb_kernel(
         const = whole.enter_context(tc.tile_pool(name="const", bufs=1))
         small = whole.enter_context(tc.tile_pool(name="small", bufs=4))
         kept = whole.enter_context(tc.tile_pool(name="kept", bufs=1))
+        psum = whole.enter_context(tc.psum_pool(name="psum", bufs=1))
 
-        vec_rows = const.tile([P, 2 * P], BF16)
-        nc.vector.memset(vec_rows[:], 0.0)
-
-        def load_vectors():
-            nc.sync.dma_start(out=vec_rows[0:8, :], in_=gamma0.rearrange("(a w) -> a w", w=2 * P))
-            nc.sync.dma_start(out=vec_rows[8:12, :], in_=gamma1.rearrange("(a w) -> a w", w=2 * P))
-            nc.sync.dma_start(out=vec_rows[12:20, :], in_=beta0.rearrange("(a w) -> a w", w=2 * P))
-            nc.sync.dma_start(out=vec_rows[20:24, :], in_=beta1.rearrange("(a w) -> a w", w=2 * P))
+        def psum_bank(k):
+            bank = psum.tile([P, BANK], F32, tag="bank%d" % k)
+            return bank
 
         ident = const.tile([P, P], F32)
         make_identity(nc, ident[:])
@@ -85,35 +83,70 @@ def tile_nodeupdatenetwork_pb_kernel(
         nc.vector.memset(eps[:], EPS_BN)
         warm = const.tile([P, 1], F32)
         nc.scalar.activation(out=warm[:], in_=eps[:], func=ACT.Abs_reciprocal_sqrt)
-
+        vec_rows = const.tile([P, 2 * P], BF16)
+        nc.vector.memset(vec_rows[:], 0.0)
         n_tiles = HIDDEN_TILES + OUT_TILES
         vec_cols = const.tile([P, 2 * P], BF16)
         gain_mean = const.tile([P, n_tiles, 2], F32)
         minus_gain = const.tile([P, n_tiles], F32)
         zero_shift = const.tile([P, n_tiles, 2], F32)
 
-        def spread_vectors():
-            vec_bank = psum_bank(T_RING[counts["t"] % len(T_RING)])
-            counts["t"] += 1
-            nc.tensor.transpose(vec_bank[:, 0:P], vec_rows[:].bitcast(F32), ident[:])
-            nc.vector.tensor_copy(out=vec_cols[:].bitcast(F32), in_=vec_bank[:, 0:P])
-            nc.vector.tensor_copy(out=gain_mean[:, :, 0], in_=vec_cols[:, 0:n_tiles])
-            nc.vector.tensor_scalar(
-                out=minus_gain[:], in0=vec_cols[:, 0:n_tiles], scalar1=-1.0, scalar2=None, op0=ALU.mult
-            )
-            nc.vector.memset(zero_shift[:], 0.0)
-            nc.vector.tensor_copy(out=zero_shift[:, :, 1], in_=vec_cols[:, n_tiles : 2 * n_tiles])
-
         w1_codes = kept.tile([P, HIDDEN_PASSES, OUT_CH], U32, align_bytes=64)
         w1_scales = kept.tile([P, HIDDEN_PASSES, OUT_CH], U8, align_bytes=64)
         h_codes = kept.tile([P, HIDDEN_PASSES, ROWS], U32, align_bytes=64)
         h_scales = kept.tile([P, HIDDEN_PASSES, ROWS], U8, align_bytes=64)
 
-        banks = whole.enter_context(tc.psum_pool(name="banks", bufs=1))
+        state = {}
 
-        def psum_bank(k):
-            bank = banks.tile([P, BANK], F32, tag="bank%d" % k)
-            return bank
+        def take_bank(ring):
+            n = state.get(ring, 0)
+            state[ring] = n + 1
+            return psum_bank(RINGS[ring][n % len(RINGS[ring])])
+
+        class_stats = {}
+        mean_var_of = {}
+        rstd_of = {}
+        scale_bias_of = {}
+        acc_of = {}
+
+        def half_statistics(tile, half):
+            if half == 0:
+                stats = small.tile([P, 2, STATS], F32)
+                class_stats[tile] = stats
+            nc.vector.bn_stats(out=class_stats[tile][:, half, :], in_=acc_of[tile, half][:])
+
+        def mean_and_variance(tile):
+            mean_var = small.tile([P, 2], F32)
+            nc.vector.bn_aggr(out=mean_var[:], in_=class_stats[tile][:].rearrange("p h s -> p (h s)"))
+            mean_var_of[tile] = mean_var
+
+        def inverse_deviation(tile):
+            rstd = small.tile([P, 1], F32)
+            nc.scalar.activation(
+                out=rstd[:], in_=mean_var_of[tile][:, 1:2], func=ACT.Abs_reciprocal_sqrt, bias=eps[:, 0:1]
+            )
+            nc.scalar.activation(
+                out=gain_mean[:, tile, 1:2], in_=mean_var_of[tile][:, 0:1], func=ACT.Identity,
+                scale=minus_gain[:, tile : tile + 1],
+            )
+            rstd_of[tile] = rstd
+
+        def scale_and_bias(tile):
+            scale_bias = small.tile([P, 2], F32)
+            nc.scalar.activation(
+                out=scale_bias[:, 0:1], in_=gain_mean[:, tile, 0:1], func=ACT.Identity, scale=rstd_of[tile][:, 0:1]
+            )
+            nc.scalar.activation(
+                out=scale_bias[:, 1:2], in_=gain_mean[:, tile, 1:2], func=ACT.Identity, scale=rstd_of[tile][:, 0:1],
+                bias=zero_shift[:, tile, 1:2],
+            )
+            scale_bias_of[tile] = scale_bias
+
+        def normalise(tile, half, dest):
+            nc.scalar.activation(
+                out=dest, in_=acc_of[tile, half][:], func=ACT.Identity,
+                scale=scale_bias_of[tile][:, 0:1], bias=scale_bias_of[tile][:, 1:2],
+            )
 
         def multiply(acc, w_codes, w_scales, a_codes, a_scales, passes, first, last, w_tile, half):
             w_cols = slice(P * w_tile, P * (w_tile + 1))
@@ -129,61 +162,126 @@ def tile_nodeupdatenetwork_pb_kernel(
                     stop=(c == passes - 1),
                 )
 
-        def half_statistics(stats, half, acc):
-            nc.vector.bn_stats(out=stats[:, half, :], in_=acc[:])
-
-        def mean_and_variance(stats):
-            mean_var = small.tile([P, 2], F32)
-            nc.vector.bn_aggr(out=mean_var[:], in_=stats[:].rearrange("p h s -> p (h s)"))
-            return mean_var
-
-        def inverse_deviation(mean_var, tile_index):
-            rstd = small.tile([P, 1], F32)
-            nc.scalar.activation(
-                out=rstd[:], in_=mean_var[:, 1:2], func=ACT.Abs_reciprocal_sqrt, bias=eps[:, 0:1]
-            )
-            nc.scalar.activation(
-                out=gain_mean[:, tile_index, 1:2], in_=mean_var[:, 0:1], func=ACT.Identity,
-                scale=minus_gain[:, tile_index : tile_index + 1],
-            )
-            return rstd
-
-        def scale_and_bias(rstd, tile_index):
-            scale_bias = small.tile([P, 2], F32)
-            nc.vector.scalar_tensor_tensor(
-                out=scale_bias[:], in0=gain_mean[:, tile_index, :], scalar=rstd[:, 0:1],
-                in1=zero_shift[:, tile_index, :], op0=ALU.mult, op1=ALU.add,
-            )
-            return scale_bias
-
-        def normalise(acc, scale_bias, dest):
-            nc.scalar.activation(
-                out=dest, in_=acc[:], func=ACT.Identity, scale=scale_bias[:, 0:1], bias=scale_bias[:, 1:2]
-            )
-
-        def normalise_v(acc, scale_bias, dest):
-            nc.vector.tensor_scalar(
-                out=dest, in0=acc[:], scalar1=scale_bias[:, 0:1], scalar2=scale_bias[:, 1:2],
-                op0=ALU.mult, op1=ALU.add,
-            )
-
         regroup = whole.enter_context(tc.tile_pool(name="regroup", bufs=RG))
+        h_pool = whole.enter_context(tc.tile_pool(name="h_pool", bufs=4))
         w1_raw = whole.enter_context(tc.tile_pool(name="w1_raw", bufs=2))
         w1_grouped = whole.enter_context(tc.tile_pool(name="w1_grouped", bufs=12))
-        h_pool = whole.enter_context(tc.tile_pool(name="h_pool", bufs=4))
         normed = whole.enter_context(tc.tile_pool(name="normed", bufs=2))
-        with ExitStack() as inner:
-            raw = inner.enter_context(tc.tile_pool(name="raw", bufs=8))
-            staged = inner.enter_context(tc.tile_pool(name="staged", bufs=2))
+        stream = []
+        stage_tiles = []
+        deferred = []
+        pieces = {}
+        normed_groups = []
 
-            def load_rows(pool, source, first_row, first_k, width, dest_col, tile_):
-                nc.sync.dma_start(
-                    out=tile_[:, :, dest_col : dest_col + width],
-                    in_=source[first_row : first_row + PAIR, first_k : first_k + width].rearrange("(p e) k -> p e k", e=2),
-                )
+        def transpose_in(n):
+            pair, c, codes, scales, col0 = stream[n]
+            bank = take_bank("in")
+            by_word = bank[:].rearrange("p (u n) -> p u n", u=2)
+            for i in range(2):
+                words = pair[:, i, :].bitcast(F32)
+                for u in range(2):
+                    first_word = PASS_WORDS * c + P * u
+                    nc.tensor.transpose(
+                        by_word[:, u, P * i : P * (i + 1)], words[:, first_word : first_word + P], ident[:]
+                    )
+            return bank
 
-            stage_tiles = []
-            stream = []
+        def group_words(n, bank, on_vector=False):
+            if n >= LATER:
+                grouped = w1_grouped.tile([P, 4 * PAIR], BF16, align_bytes=64, tag="later")
+            else:
+                grouped = regroup.tile([P, 4 * PAIR], BF16, align_bytes=64, tag="now")
+            dest = grouped[:].bitcast(F32).rearrange("p (n u) -> p n u", u=2)
+            src = bank[:].rearrange("p (u n) -> p n u", u=2)
+            if on_vector:
+                nc.vector.tensor_copy(out=dest, in_=src)
+            else:
+                nc.scalar.copy(out=dest, in_=src)
+            return grouped
+
+        def quantise_now(n, grouped):
+            pair, c, codes, scales, col0 = stream[n]
+            nc.vector.quantize_mx(
+                out=codes[:, c, col0 : col0 + PAIR].bitcast(FP8X4),
+                scales=scales[:, c, col0 : col0 + PAIR],
+                in_=grouped[:],
+            )
+
+        def quantise(n, grouped):
+            if n >= LATER:
+                deferred.append((n, grouped))
+            else:
+                quantise_now(n, grouped)
+
+        def quantise_deferred(count):
+            for n, grouped in deferred[:count]:
+                quantise_now(n, grouped)
+            rest = deferred[count:]
+            deferred.clear()
+            deferred.extend(rest)
+
+        def matmul_half(tile, half):
+            g, t = divmod(tile, GROUP_TILES)
+            w0_codes, w0_scales, x_codes, x_scales = stage_tiles[g]
+            acc_of[tile, half] = take_bank("sum")
+            multiply(acc_of[tile, half], w0_codes, w0_scales, x_codes, x_scales, GROUP_PASSES, 0, GROUP_PASSES, t, half)
+
+        def second_half(q, half, first, last):
+            if first == 0:
+                acc_of[HIDDEN_TILES + q, half] = take_bank("sum2")
+            multiply(
+                acc_of[HIDDEN_TILES + q, half], w1_codes, w1_scales, h_codes, h_scales, HIDDEN_PASSES,
+                first, last, q, half,
+            )
+
+        def normalise_hidden(tile, half):
+            g, t = divmod(tile, GROUP_TILES)
+            normalise(tile, half, normed_groups[g][:, t, BANK * half : BANK * (half + 1)])
+
+        def by_row(piece):
+            g, r = divmod(piece, ROWS // PAIR)
+            return normed_groups[g][:, :, PAIR * r : PAIR * (r + 1)].rearrange("p t n -> p n t")
+
+        def leaky_piece(piece):
+            h_grouped = h_pool.tile([P, 4 * PAIR], BF16, align_bytes=64)
+            nc.vector.scalar_tensor_tensor(
+                out=h_grouped[:].rearrange("p (n t) -> p n t", t=GROUP_TILES),
+                in0=by_row(piece), scalar=SLOPE, in1=by_row(piece), op0=ALU.mult, op1=ALU.max,
+            )
+            pieces[piece] = h_grouped
+
+        def leaky_terms(piece, pool):
+            up = pool.tile([P, 4 * PAIR], BF16, align_bytes=64)
+            down = pool.tile([P, 4 * PAIR], BF16, align_bytes=64)
+            nc.scalar.activation(
+                out=up[:].rearrange("p (n t) -> p n t", t=GROUP_TILES), in_=by_row(piece), func=ACT.Copy
+            )
+            nc.scalar.activation(
+                out=down[:].rearrange("p (n t) -> p n t", t=GROUP_TILES), in_=by_row(piece), func=ACT.Copy, scale=SLOPE
+            )
+            return up, down
+
+        def leaky_max(piece, terms):
+            h_grouped = h_pool.tile([P, 4 * PAIR], BF16, align_bytes=64)
+            nc.vector.tensor_tensor(out=h_grouped[:], in0=terms[0][:], in1=terms[1][:], op=ALU.max)
+            pieces[piece] = h_grouped
+
+        def quantise_piece(piece):
+            g, r = divmod(piece, ROWS // PAIR)
+            rows = slice(PAIR * r, PAIR * (r + 1))
+            nc.vector.quantize_mx(
+                out=h_codes[:, g, rows].bitcast(FP8X4), scales=h_scales[:, g, rows], in_=pieces[piece][:]
+            )
+
+        with ExitStack() as first:
+            raw = first.enter_context(tc.tile_pool(name="raw", bufs=8))
+            staged = first.enter_context(tc.tile_pool(name="staged", bufs=2))
+
+            def load_vectors():
+                nc.sync.dma_start(out=vec_rows[0:8, :], in_=gamma0.rearrange("(a w) -> a w", w=2 * P))
+                nc.sync.dma_start(out=vec_rows[8:12, :], in_=gamma1.rearrange("(a w) -> a w", w=2 * P))
+                nc.sync.dma_start(out=vec_rows[12:20, :], in_=beta0.rearrange("(a w) -> a w", w=2 * P))
+                nc.sync.dma_start(out=vec_rows[20:24, :], in_=beta1.rearrange("(a w) -> a w", w=2 * P))
 
             def load_stage(stage):
                 w0_codes = staged.tile([P, GROUP_PASSES, GROUP_OUT], U32, align_bytes=64)
@@ -205,6 +303,8 @@ def tile_nodeupdatenetwork_pb_kernel(
                     stream.extend([(w0_pair, c, w0_codes, w0_scales, PAIR * a) for c in range(GROUP_PASSES)])
 
                 load_w0(0)
+                if stage == 0:
+                    load_vectors()
                 k0 = GROUP_K * stage
                 from_node = max(0, min(NODE_K - k0, GROUP_K))
                 for r in range(ROWS // PAIR):
@@ -225,224 +325,105 @@ def tile_nodeupdatenetwork_pb_kernel(
                     stream.extend([(x_pair, c, x_codes, x_scales, PAIR * r) for c in range(GROUP_PASSES)])
                 load_w0(1)
 
-            def load_w1(a):
+            load_stage(0)
+            for stage in range(1, GROUPS):
+                load_stage(stage)
+            for a in range(OUT_TILES // 2):
                 w1_pair = w1_raw.tile([P, 2, HIDDEN], BF16)
                 nc.sync.dma_start(
-                    out=w1_pair[:],
-                    in_=w1[PAIR * a : PAIR * (a + 1), :].rearrange("(p e) k -> p e k", e=2),
+                    out=w1_pair[:], in_=w1[PAIR * a : PAIR * (a + 1), :].rearrange("(p e) k -> p e k", e=2)
                 )
                 stream.extend([(w1_pair, c, w1_codes, w1_scales, PAIR * a) for c in range(HIDDEN_PASSES)])
+            for g in range(GROUPS):
+                v = normed.tile([P, GROUP_TILES, ROWS], F32)
+                normed_groups.append(v)
 
-            counts = {"t": 0}
-
-            def transpose_in(unit):
-                pair, c, codes, scales, col0 = unit
-                bank = psum_bank(T_RING[counts["t"] % len(T_RING)])
-                counts["t"] += 1
-                by_word = bank[:].rearrange("p (u n) -> p u n", u=2)
-                for i in range(2):
-                    words = pair[:, i, :].bitcast(F32)
-                    for u in range(2):
-                        first_word = PASS_WORDS * c + P * u
-                        nc.tensor.transpose(
-                            by_word[:, u, P * i : P * (i + 1)], words[:, first_word : first_word + P], ident[:]
-                        )
-                return bank
-
-            def group_words(bank, on_vector, later=False):
-                if later:
-                    grouped = w1_grouped.tile([P, 4 * PAIR], BF16, align_bytes=64, tag="later")
-                else:
-                    grouped = regroup.tile([P, 4 * PAIR], BF16, align_bytes=64, tag="now")
-                dest = grouped[:].bitcast(F32).rearrange("p (n u) -> p n u", u=2)
-                src = bank[:].rearrange("p (u n) -> p n u", u=2)
-                if on_vector:
-                    nc.vector.tensor_copy(out=dest, in_=src)
-                else:
-                    nc.scalar.copy(out=dest, in_=src)
-                return grouped
-
-            def quantise(unit, grouped):
-                pair, c, codes, scales, col0 = unit
-                nc.vector.quantize_mx(
-                    out=codes[:, c, col0 : col0 + PAIR].bitcast(FP8X4),
-                    scales=scales[:, c, col0 : col0 + PAIR],
-                    in_=grouped[:],
+            def spread_vectors():
+                vec_bank = take_bank("in")
+                nc.tensor.transpose(vec_bank[:, 0:P], vec_rows[:].bitcast(F32), ident[:])
+                nc.vector.tensor_copy(out=vec_cols[:].bitcast(F32), in_=vec_bank[:, 0:P])
+                nc.vector.tensor_copy(out=gain_mean[:, :, 0], in_=vec_cols[:, 0:n_tiles])
+                nc.vector.tensor_scalar(
+                    out=minus_gain[:], in0=vec_cols[:, 0:n_tiles], scalar1=-1.0, scalar2=None, op0=ALU.mult
                 )
+                nc.vector.memset(zero_shift[:], 0.0)
+                nc.vector.tensor_copy(out=zero_shift[:, :, 1], in_=vec_cols[:, n_tiles : 2 * n_tiles])
 
-            normed_groups = []
-            pieces = []
-            deferred = []
-
-            def quant_or_defer(unit, grouped, later):
-                if later:
-                    deferred.append((unit, grouped))
-                else:
-                    quantise(unit, grouped)
-
-            def quant_deferred(n):
-                for unit, grouped in deferred[:n]:
-                    quantise(unit, grouped)
-                del_n = deferred[n:]
-                deferred.clear()
-                deferred.extend(del_n)
-
-            def leaky_scalar(piece, pool):
-                g, r = divmod(piece, ROWS // PAIR)
-                v_by_row = normed_groups[g][:, :, PAIR * r : PAIR * (r + 1)].rearrange("p t n -> p n t")
-                up = pool.tile([P, 4 * PAIR], BF16, align_bytes=64)
-                down = pool.tile([P, 4 * PAIR], BF16, align_bytes=64)
-                nc.scalar.activation(out=up[:].rearrange("p (n t) -> p n t", t=GROUP_TILES), in_=v_by_row, func=ACT.Copy)
-                nc.scalar.activation(
-                    out=down[:].rearrange("p (n t) -> p n t", t=GROUP_TILES), in_=v_by_row, func=ACT.Copy, scale=SLOPE
-                )
-                return up, down
-
-            def leaky_max(up, down):
-                h_grouped = h_pool.tile([P, 4 * PAIR], BF16, align_bytes=64)
-                nc.vector.tensor_tensor(out=h_grouped[:], in0=up[:], in1=down[:], op=ALU.max)
-                pieces.append(h_grouped)
-
-            def leaky_piece(piece):
-                g, r = divmod(piece, ROWS // PAIR)
-                h_grouped = h_pool.tile([P, 4 * PAIR], BF16, align_bytes=64)
-                v_by_row = normed_groups[g][:, :, PAIR * r : PAIR * (r + 1)].rearrange("p t n -> p n t")
-                nc.vector.scalar_tensor_tensor(
-                    out=h_grouped[:].rearrange("p (n t) -> p n t", t=GROUP_TILES),
-                    in0=v_by_row, scalar=SLOPE, in1=v_by_row, op0=ALU.mult, op1=ALU.max,
-                )
-                pieces.append(h_grouped)
-
-            def quantise_piece(piece):
-                g, r = divmod(piece, ROWS // PAIR)
-                rows = slice(PAIR * r, PAIR * (r + 1))
-                nc.vector.quantize_mx(
-                    out=h_codes[:, g, rows].bitcast(FP8X4),
-                    scales=h_scales[:, g, rows],
-                    in_=pieces[piece][:],
-                )
-
-            load_stage(0)
-            load_vectors()
-            load_stage(1)
-
-            def step(unit, v=False):
-                b = transpose_in(unit)
-                g = group_words(b, v)
-                quantise(unit, g)
-
-            pos = 0
-            for n, unit in enumerate(stream[0:PRO]):
-                step(unit, False)
-            pos = PRO
+            done_units = 0
+            for n in range(HEAD_UNITS):
+                quantise(n, group_words(n, transpose_in(n)))
+            done_units = HEAD_UNITS
             spread_vectors()
-
-            accs = {}
-            stats_of = {}
-            mv = {}
-            rs = {}
-            sb = {}
-
-            def matmul_half(q, half):
-                g, t = divmod(q, GROUP_TILES)
-                w0_codes, w0_scales, x_codes, x_scales = stage_tiles[g]
-                acc = psum_bank(4 + (2 * q + half) % 4)
-                multiply(acc, w0_codes, w0_scales, x_codes, x_scales, GROUP_PASSES, 0, GROUP_PASSES, t, half)
-                accs[q, half] = acc
-
-            def bn_half(q, half):
-                if half == 0:
-                    stats = small.tile([P, 2, STATS], F32)
-                    stats_of[q] = stats
-                half_statistics(stats_of[q], half, accs[q, half])
-
-            def norm_half(q, half):
-                normalise(accs[q, half], sb[q], normed_groups[q // 4][:, q % 4, BANK * half : BANK * (half + 1)])
-
-            accs2 = {}
-
-            def l2(q, half, first, last):
-                if first == 0:
-                    accs2[q, half] = psum_bank(L2_RING[(2 * q + half) % len(L2_RING)])
-                multiply(accs2[q, half], w1_codes, w1_scales, h_codes, h_scales, HIDDEN_PASSES, first, last, q, half)
-
-            for q in range(HIDDEN_TILES):
-                g, t = divmod(q, GROUP_TILES)
-                if t == 0:
-                    if g + 2 < GROUPS:
-                        load_stage(g + 2)
-                    elif g + 2 == GROUPS:
-                        for a in range(4):
-                            load_w1(a)
-                    v = normed.tile([P, GROUP_TILES, ROWS], F32)
-                    normed_groups.append(v)
-                piece = q - LEAKY_LAG
-                n_units = QUOTA(q)
-                us = stream[pos : pos + n_units]
-                first = pos
-                pos += n_units
-                vec = VCOPY(q)
-                k = KA(q)
-
-                def isl(j):
-                    return first + j >= DEFER
-
-                tb = [transpose_in(u) for u in us[:k]]
-                if piece >= 0:
+            pending = []
+            unquantised = []
+            for halves, n_units, piece, on_vector, k in ROUNDS:
+                ns = list(range(done_units, done_units + n_units))
+                done_units += n_units
+                banks = [transpose_in(n) for n in ns[:k]]
+                groups = []
+                if piece is not None:
                     leaky_piece(piece)
-                gs = [group_words(tb[0], 0 == vec, isl(0))]
-                if q >= 1:
-                    rs[q - 1] = inverse_deviation(mv[q - 1], q - 1)
-                for j in range(1, k):
-                    gs.append(group_words(tb[j], j == vec, isl(j)))
-                if q >= 1:
-                    sb[q - 1] = scale_and_bias(rs[q - 1], q - 1)
-                for j in range(k):
-                    quant_or_defer(us[j], gs[j], isl(j))
-                matmul_half(q, 0)
-                tb += [transpose_in(u) for u in us[k:]]
-                for j in range(k, len(us) - 1):
-                    gs.append(group_words(tb[j], j == vec, isl(j)))
-                bn_half(q, 0)
-                for j in range(k, len(us) - 1):
-                    quant_or_defer(us[j], gs[j], isl(j))
-                if q >= 1:
-                    norm_half(q - 1, 0)
-                    norm_half(q - 1, 1)
-                gs.append(group_words(tb[-1], False, isl(len(us) - 1)))
-                matmul_half(q, 1)
-                if piece >= 1:
-                    quantise_piece(piece - 1)
-                bn_half(q, 1)
-                if q == 15:
-                    quantise_piece(10)
-                quant_or_defer(us[-1], gs[-1], isl(len(us) - 1))
-                mv[q] = mean_and_variance(stats_of[q])
-            rest = stream[pos:]
+                for j, n in enumerate(ns[:k]):
+                    groups.append(group_words(n, banks[j], j in on_vector))
+                    if j == 0:
+                        for tile in pending:
+                            inverse_deviation(tile)
+                for tile in pending:
+                    scale_and_bias(tile)
+                for j, n in enumerate(ns[:k]):
+                    quantise(n, groups[j])
+                for tile in pending[:-1]:
+                    normalise_hidden(tile, 0)
+                    normalise_hidden(tile, 1)
+                matmul_half(halves[0][0], halves[0][1])
+                banks += [transpose_in(n) for n in ns[k:]]
+                for j in range(k, n_units - 1):
+                    groups.append(group_words(ns[j], banks[j], j in on_vector))
+                half_statistics(halves[0][0], halves[0][1])
+                for j in range(k, n_units - 1):
+                    quantise(ns[j], groups[j])
+                for tile in pending[-1:]:
+                    normalise_hidden(tile, 0)
+                    normalise_hidden(tile, 1)
+                if n_units > k:
+                    groups.append(group_words(ns[-1], banks[-1], n_units - 1 in on_vector))
+                matmul_half(halves[1][0], halves[1][1])
+                for p in unquantised:
+                    quantise_piece(p)
+                half_statistics(halves[1][0], halves[1][1])
+                if n_units > k:
+                    quantise(ns[-1], groups[-1])
+                pending = [tile for tile, half in halves if half == 1]
+                pending = [tile for n, tile in enumerate(pending) if tile not in pending[:n]]
+                unquantised = [] if piece is None else [piece]
+                if halves[1][0] == 15:
+                    quantise_piece(piece)
+                for tile in pending:
+                    mean_and_variance(tile)
 
-            def prepare(us):
-                for u in us:
-                    b = transpose_in(u)
-                    quant_or_defer(u, group_words(b, False, True), True)
+            rest = list(range(done_units, len(stream)))
 
-            rs[15] = inverse_deviation(mv[15], 15)
+            inverse_deviation(15)
             leaky_piece(11)
-            prepare(rest[:2])
-            sb[15] = scale_and_bias(rs[15], 15)
-            norm_half(15, 0)
-            norm_half(15, 1)
+            for n in rest[:2]:
+                quantise(n, group_words(n, transpose_in(n)))
+            scale_and_bias(15)
+            normalise_hidden(15, 0)
+            normalise_hidden(15, 1)
             quantise_piece(11)
-            quant_deferred(4)
-            l2(0, 0, 0, 3)
-            l2(0, 1, 0, 3)
+            quantise_deferred(DEF0)
+            second_half(0, 0, 0, 3)
+            second_half(0, 1, 0, 3)
+
         with ExitStack() as second:
             work = second.enter_context(tc.tile_pool(name="work", bufs=3))
             done = second.enter_context(tc.tile_pool(name="done", bufs=4))
             stores = second.enter_context(tc.tile_pool(name="stores", bufs=8))
             v1s = {}
             o1s = {}
+            back = {}
 
-            def lh(q, half, dest=None):
+            def leaky_out(q, half):
                 if half == 0:
                     o1 = done.tile([P, ROWS], F32)
                     o1s[q] = o1
@@ -452,13 +433,10 @@ def tile_nodeupdatenetwork_pb_kernel(
                     op0=ALU.mult, op1=ALU.max,
                 )
 
-            back = {}
-
-            def tback(piece, ring):
+            def transpose_back(piece, ring):
                 a, half = divmod(piece, 2)
-                bs = []
                 for b in range(2):
-                    bank = psum_bank(ring[b])
+                    bank = take_bank(ring)
                     view = bank[:].rearrange("p (i e c) -> p i e c", i=2, e=2)
                     for i in range(2):
                         first_row = BANK * half + PAIR * b + P * i
@@ -466,14 +444,13 @@ def tile_nodeupdatenetwork_pb_kernel(
                             nc.tensor.transpose(
                                 view[:, i, e, :], o1s[2 * a + e][:, first_row : first_row + P], ident[:]
                             )
-                    bs.append(bank)
-                back[piece] = bs
+                    back[piece, b] = bank
 
             def store(piece, b, on_vector=False):
                 a, half = divmod(piece, 2)
-                by_row = stores.tile([P, 2, PAIR], F32)
-                dest = by_row[:].rearrange("p i (c e) -> p i c e", e=2)
-                src = back[piece][b][:].rearrange("p (i e c) -> p i c e", i=2, e=2)
+                rows_out = stores.tile([P, 2, PAIR], F32)
+                dest = rows_out[:].rearrange("p i (c e) -> p i c e", e=2)
+                src = back[piece, b][:].rearrange("p (i e c) -> p i c e", i=2, e=2)
                 if on_vector:
                     nc.vector.tensor_copy(out=dest, in_=src)
                 else:
@@ -483,97 +460,86 @@ def tile_nodeupdatenetwork_pb_kernel(
                     out=out_rows[first_row : first_row + PAIR, PAIR * a : PAIR * (a + 1)].rearrange(
                         "(i p) c -> p i c", p=P
                     ),
-                    in_=by_row[:],
+                    in_=rows_out[:],
                 )
 
-            mv2 = {}
-            rs2 = {}
-            sb2 = {}
-
-            def norm2(q, half):
+            def normalise_out(q, half):
                 if half == 0:
                     v1 = work.tile([P, ROWS], F32)
                     v1s[q] = v1
-                normalise(accs2[q, half], sb2[q], v1s[q][:, BANK * half : BANK * (half + 1)])
+                normalise(HIDDEN_TILES + q, half, v1s[q][:, BANK * half : BANK * (half + 1)])
 
-            acc2_stats = {}
-
-            def bn2(q, half):
-                if half == 0:
-                    stats = small.tile([P, 2, STATS], F32)
-                    acc2_stats[q] = stats
-                half_statistics(acc2_stats[q], half, accs2[q, half])
-
-            tb = [transpose_in(u) for u in rest[2:5]]
-            l2(1, 0, 0, 3)
-            l2(1, 1, 0, 3)
+            T1 = HIDDEN_TILES
+            banks = [transpose_in(n) for n in rest[2:5]]
+            second_half(1, 0, 0, 3)
+            second_half(1, 1, 0, 3)
             leaky_piece(12)
             leaky_piece(13)
-            up, down = leaky_scalar(14, stores)
+            terms = leaky_terms(14, stores)
             quantise_piece(12)
             quantise_piece(13)
-            l2(0, 0, 3, 4)
-            l2(1, 0, 3, 4)
-            for j, u in enumerate(rest[2:5]):
-                quant_or_defer(u, group_words(tb[j], False, True), True)
-            leaky_max(up, down)
+            second_half(0, 0, 3, 4)
+            second_half(1, 0, 3, 4)
+            for j, n in enumerate(rest[2:5]):
+                quantise(n, group_words(n, banks[j]))
+            leaky_max(14, terms)
             leaky_piece(15)
-            prepare(rest[5:])
-            bn2(0, 0)
+            for n in rest[5:]:
+                quantise(n, group_words(n, transpose_in(n)))
+            half_statistics(T1, 0)
             quantise_piece(14)
             quantise_piece(15)
-            l2(0, 1, 3, 4)
-            l2(1, 1, 3, 4)
-            bn2(1, 0)
-            quant_deferred(1)
-            bn2(0, 1)
-            quant_deferred(1)
-            mv2[0] = mean_and_variance(acc2_stats[0])
-            rs2[0] = inverse_deviation(mv2[0], HIDDEN_TILES)
-            bn2(1, 1)
-            sb2[0] = scale_and_bias(rs2[0], HIDDEN_TILES)
-            norm2(0, 0)
-            norm2(0, 1)
-            quant_deferred(1)
-            mv2[1] = mean_and_variance(acc2_stats[1])
-            rs2[1] = inverse_deviation(mv2[1], HIDDEN_TILES + 1)
-            quant_deferred(1)
-            sb2[1] = scale_and_bias(rs2[1], HIDDEN_TILES + 1)
-            norm2(1, 0)
-            norm2(1, 1)
-
+            second_half(0, 1, 3, 4)
+            second_half(1, 1, 3, 4)
+            half_statistics(T1 + 1, 0)
+            quantise_deferred(1)
+            half_statistics(T1, 1)
+            quantise_deferred(1)
+            mean_and_variance(T1)
+            inverse_deviation(T1)
+            half_statistics(T1 + 1, 1)
+            scale_and_bias(T1)
+            normalise_out(0, 0)
+            normalise_out(0, 1)
+            quantise_deferred(1)
+            mean_and_variance(T1 + 1)
+            inverse_deviation(T1 + 1)
+            quantise_deferred(1)
+            scale_and_bias(T1 + 1)
+            normalise_out(1, 0)
+            normalise_out(1, 1)
             for q in range(2, OUT_TILES + 1):
                 mul = q < OUT_TILES
-                if q >= 4:
-                    store(q - 4, 0)
-                lh(q - 2, 0)
+                if q >= LAGB + 1:
+                    store(q - LAGB - 1, 0)
+                leaky_out(q - 2, 0)
                 if q >= 3:
-                    mv2[q - 1] = mean_and_variance(acc2_stats[q - 1])
-                    rs2[q - 1] = inverse_deviation(mv2[q - 1], HIDDEN_TILES + q - 1)
+                    mean_and_variance(T1 + q - 1)
+                    inverse_deviation(T1 + q - 1)
                 if mul:
-                    l2(q, 0, E2 if q == 2 else 0, 4)
-                    bn2(q, 0)
+                    second_half(q, 0, 0, 4)
+                    half_statistics(T1 + q, 0)
                 if q >= 3:
-                    sb2[q - 1] = scale_and_bias(rs2[q - 1], HIDDEN_TILES + q - 1)
-                quant_deferred(C_QUANT[q])
-                if q >= 4:
-                    store(q - 4, 1)
+                    scale_and_bias(T1 + q - 1)
+                quantise_deferred(LATE_Q[q])
+                if q >= LAGB + 1:
+                    store(q - LAGB - 1, 1)
                 if q >= 3:
-                    norm2(q - 1, 0)
-                    norm2(q - 1, 1)
+                    normalise_out(q - 1, 0)
+                    normalise_out(q - 1, 1)
                 if mul:
-                    l2(q, 1, E2 if q == 2 else 0, 4)
-                lh(q - 2, 1)
+                    second_half(q, 1, 0, 4)
+                leaky_out(q - 2, 1)
                 if mul:
-                    bn2(q, 1)
-                if q >= 3:
-                    tback(q - 3, OUT_RING)
-            lh(7, 0)
-            tback(6, [4, 5])
+                    half_statistics(T1 + q, 1)
+                if q >= LAGB:
+                    transpose_back(q - LAGB, "out")
+            leaky_out(7, 0)
+            transpose_back(6, "tail")
             store(5, 0)
             store(5, 1)
-            lh(7, 1)
-            tback(7, [6, 7])
+            leaky_out(7, 1)
+            transpose_back(7, "tail")
             store(6, 0)
             store(6, 1, True)
             store(7, 0)

@@ -38,22 +38,22 @@ LATER = 76
 DEF0 = 4
 LATE_Q = [0, 0, 0, 3, 2, 2, 0, 0, 0]
 RINGS = {"in": [0, 1, 2, 3], "sum": [4, 5, 6, 7], "sum2": [4, 5, 6, 7, 0, 1], "out": [2, 3], "tail": [4, 5, 6, 7]}
-ROUNDS = [([(0, 0), (0, 1)], 5, None, [2], 5),
-          ([(1, 0), (1, 1)], 5, None, [2], 5),
-          ([(2, 0), (2, 1)], 5, None, [2], 5),
-          ([(3, 0), (3, 1)], 5, None, [2], 5),
-          ([(4, 0), (4, 1)], 5, None, [2], 5),
-          ([(5, 0), (5, 1)], 5, 0, [], 2),
-          ([(6, 0), (6, 1)], 4, 1, [], 2),
-          ([(7, 0), (7, 1)], 4, 2, [], 2),
-          ([(8, 0), (8, 1)], 4, 3, [], 2),
-          ([(9, 0), (9, 1)], 4, 4, [], 2),
-          ([(10, 0), (10, 1)], 4, 5, [], 2),
-          ([(11, 0), (11, 1)], 4, 6, [], 2),
-          ([(12, 0), (12, 1)], 4, 7, [], 2),
-          ([(13, 0), (13, 1)], 4, 8, [], 2),
-          ([(14, 0), (14, 1)], 3, 9, [], 2),
-          ([(15, 0), (15, 1)], 3, 10, [], 2)]
+ROUNDS = [([(0, 0), (0, 1)], 5, [], [2], 5),
+          ([(1, 0), (1, 1)], 5, [], [2], 5),
+          ([(2, 0), (2, 1)], 5, [], [2], 5),
+          ([(3, 0), (3, 1)], 4, [], [2], 5),
+          ([(4, 0), (4, 1)], 4, [], [2], 5),
+          ([(5, 0), (5, 1)], 4, [0], [], 2),
+          ([(6, 0), (6, 1)], 4, [1], [], 2),
+          ([(7, 0), (7, 1)], 4, [2], [], 2),
+          ([(8, 0), (8, 1)], 4, [3], [], 2),
+          ([(9, 0), (9, 1)], 4, [4], [], 2),
+          ([(10, 0), (10, 1)], 4, [5], [], 2),
+          ([(11, 0), (11, 1)], 5, [6], [], 2),
+          ([(12, 0), (12, 1)], 4, [7], [], 2),
+          ([(13, 0), (13, 1)], 4, [8], [], 2),
+          ([(14, 0), (14, 1)], 3, [9], [], 2),
+          ([(15, 0), (15, 1)], 3, [10], [], 2)]
 
 FLOPS = 2 * ROWS * GROUPS * GROUP_K * GROUP_OUT + 2 * ROWS * HIDDEN * OUT_CH
 
@@ -133,12 +133,9 @@ def tile_nodeupdatenetwork_pb_kernel(
 
         def scale_and_bias(tile):
             scale_bias = small.tile([P, 2], F32)
-            nc.scalar.activation(
-                out=scale_bias[:, 0:1], in_=gain_mean[:, tile, 0:1], func=ACT.Identity, scale=rstd_of[tile][:, 0:1]
-            )
-            nc.scalar.activation(
-                out=scale_bias[:, 1:2], in_=gain_mean[:, tile, 1:2], func=ACT.Identity, scale=rstd_of[tile][:, 0:1],
-                bias=zero_shift[:, tile, 1:2],
+            nc.vector.scalar_tensor_tensor(
+                out=scale_bias[:], in0=gain_mean[:, tile, :], scalar=rstd_of[tile][:, 0:1],
+                in1=zero_shift[:, tile, :], op0=ALU.mult, op1=ALU.add,
             )
             scale_bias_of[tile] = scale_bias
 
@@ -164,7 +161,7 @@ def tile_nodeupdatenetwork_pb_kernel(
 
         regroup = whole.enter_context(tc.tile_pool(name="regroup", bufs=RG))
         h_pool = whole.enter_context(tc.tile_pool(name="h_pool", bufs=4))
-        w1_raw = whole.enter_context(tc.tile_pool(name="w1_raw", bufs=2))
+        w1_raw = whole.enter_context(tc.tile_pool(name="w1_raw", bufs=3))
         w1_grouped = whole.enter_context(tc.tile_pool(name="w1_grouped", bufs=12))
         normed = whole.enter_context(tc.tile_pool(name="normed", bufs=2))
         stream = []
@@ -173,9 +170,9 @@ def tile_nodeupdatenetwork_pb_kernel(
         pieces = {}
         normed_groups = []
 
-        def transpose_in(n):
+        def transpose_in(n, ring="in"):
             pair, c, codes, scales, col0 = stream[n]
-            bank = take_bank("in")
+            bank = take_bank(ring)
             by_word = bank[:].rearrange("p (u n) -> p u n", u=2)
             for i in range(2):
                 words = pair[:, i, :].bitcast(F32)
@@ -356,18 +353,21 @@ def tile_nodeupdatenetwork_pb_kernel(
             spread_vectors()
             pending = []
             unquantised = []
-            for halves, n_units, piece, on_vector, k in ROUNDS:
+            for halves, n_units, todo, on_vector, k in ROUNDS:
                 ns = list(range(done_units, done_units + n_units))
                 done_units += n_units
                 banks = [transpose_in(n) for n in ns[:k]]
                 groups = []
-                if piece is not None:
-                    leaky_piece(piece)
+                for p in todo[:1]:
+                    leaky_piece(p)
                 for j, n in enumerate(ns[:k]):
                     groups.append(group_words(n, banks[j], j in on_vector))
                     if j == 0:
                         for tile in pending:
                             inverse_deviation(tile)
+                if not ns[:k]:
+                    for tile in pending:
+                        inverse_deviation(tile)
                 for tile in pending:
                     scale_and_bias(tile)
                 for j, n in enumerate(ns[:k]):
@@ -375,11 +375,13 @@ def tile_nodeupdatenetwork_pb_kernel(
                 for tile in pending[:-1]:
                     normalise_hidden(tile, 0)
                     normalise_hidden(tile, 1)
-                matmul_half(halves[0][0], halves[0][1])
+                for tile, half in halves[:1]:
+                    matmul_half(tile, half)
                 banks += [transpose_in(n) for n in ns[k:]]
                 for j in range(k, n_units - 1):
                     groups.append(group_words(ns[j], banks[j], j in on_vector))
-                half_statistics(halves[0][0], halves[0][1])
+                for tile, half in halves[:1]:
+                    half_statistics(tile, half)
                 for j in range(k, n_units - 1):
                     quantise(ns[j], groups[j])
                 for tile in pending[-1:]:
@@ -387,17 +389,23 @@ def tile_nodeupdatenetwork_pb_kernel(
                     normalise_hidden(tile, 1)
                 if n_units > k:
                     groups.append(group_words(ns[-1], banks[-1], n_units - 1 in on_vector))
-                matmul_half(halves[1][0], halves[1][1])
+                for tile, half in halves[1:]:
+                    matmul_half(tile, half)
                 for p in unquantised:
                     quantise_piece(p)
-                half_statistics(halves[1][0], halves[1][1])
+                unquantised = todo[:1]
+                for p in todo[1:]:
+                    leaky_piece(p)
+                for tile, half in halves[1:]:
+                    half_statistics(tile, half)
                 if n_units > k:
                     quantise(ns[-1], groups[-1])
+                for p in todo[1:]:
+                    quantise_piece(p)
                 pending = [tile for tile, half in halves if half == 1]
-                pending = [tile for n, tile in enumerate(pending) if tile not in pending[:n]]
-                unquantised = [] if piece is None else [piece]
-                if halves[1][0] == 15:
-                    quantise_piece(piece)
+                if (15, 1) in halves:
+                    for p in unquantised:
+                        quantise_piece(p)
                 for tile in pending:
                     mean_and_variance(tile)
 
@@ -512,10 +520,10 @@ def tile_nodeupdatenetwork_pb_kernel(
                 mul = q < OUT_TILES
                 if q >= LAGB + 1:
                     store(q - LAGB - 1, 0)
-                leaky_out(q - 2, 0)
                 if q >= 3:
                     mean_and_variance(T1 + q - 1)
                     inverse_deviation(T1 + q - 1)
+                leaky_out(q - 2, 0)
                 if mul:
                     second_half(q, 0, 0, 4)
                     half_statistics(T1 + q, 0)

@@ -85,6 +85,9 @@ def tile_nodeupdatenetwork_pb_kernel(
         nc.scalar.activation(out=warm[:], in_=eps[:], func=ACT.Abs_reciprocal_sqrt)
         vec_rows = const.tile([P, 2 * P], BF16)
         nc.vector.memset(vec_rows[:], 0.0)
+        vec_rows1 = const.tile([P, P], BF16)
+        nc.vector.memset(vec_rows1[:], 0.0)
+        vec_words1 = const.tile([P, P], F32)
         n_tiles = HIDDEN_TILES + OUT_TILES
         vec_cols = const.tile([P, 2 * P], BF16)
         gain_mean = const.tile([P, n_tiles, 2], F32)
@@ -276,9 +279,9 @@ def tile_nodeupdatenetwork_pb_kernel(
 
             def load_vectors():
                 nc.sync.dma_start(out=vec_rows[0:8, :], in_=gamma0.rearrange("(a w) -> a w", w=2 * P))
-                nc.sync.dma_start(out=vec_rows[8:12, :], in_=gamma1.rearrange("(a w) -> a w", w=2 * P))
-                nc.sync.dma_start(out=vec_rows[12:20, :], in_=beta0.rearrange("(a w) -> a w", w=2 * P))
-                nc.sync.dma_start(out=vec_rows[20:24, :], in_=beta1.rearrange("(a w) -> a w", w=2 * P))
+                nc.sync.dma_start(out=vec_rows[8:16, :], in_=beta0.rearrange("(a w) -> a w", w=2 * P))
+                nc.sync.dma_start(out=vec_rows1[0:8, :], in_=gamma1.rearrange("(a w) -> a w", w=P))
+                nc.sync.dma_start(out=vec_rows1[8:16, :], in_=beta1.rearrange("(a w) -> a w", w=P))
 
             def load_stage(stage):
                 w0_codes = staged.tile([P, GROUP_PASSES, GROUP_OUT], U32, align_bytes=64)
@@ -328,7 +331,7 @@ def tile_nodeupdatenetwork_pb_kernel(
             for a in range(OUT_TILES // 2):
                 w1_pair = w1_raw.tile([P, 2, HIDDEN], BF16)
                 nc.sync.dma_start(
-                    out=w1_pair[:], in_=w1[PAIR * a : PAIR * (a + 1), :].rearrange("(p e) k -> p e k", e=2)
+                    out=w1_pair[:], in_=w1[PAIR * a : PAIR * (a + 1), :].rearrange("(i p) k -> p i k", p=P)
                 )
                 stream.extend([(w1_pair, c, w1_codes, w1_scales, PAIR * a) for c in range(HIDDEN_PASSES)])
             for g in range(GROUPS):
@@ -338,19 +341,29 @@ def tile_nodeupdatenetwork_pb_kernel(
             def spread_vectors():
                 vec_bank = take_bank("in")
                 nc.tensor.transpose(vec_bank[:, 0:P], vec_rows[:].bitcast(F32), ident[:])
+                nc.tensor.transpose(vec_bank[:, P : 2 * P], vec_words1[:], ident[:])
                 nc.vector.tensor_copy(out=vec_cols[:].bitcast(F32), in_=vec_bank[:, 0:P])
-                nc.vector.tensor_copy(out=gain_mean[:, :, 0], in_=vec_cols[:, 0:n_tiles])
-                nc.vector.tensor_scalar(
-                    out=minus_gain[:], in0=vec_cols[:, 0:n_tiles], scalar1=-1.0, scalar2=None, op0=ALU.mult
-                )
                 nc.vector.memset(zero_shift[:], 0.0)
-                nc.vector.tensor_copy(out=zero_shift[:, :, 1], in_=vec_cols[:, n_tiles : 2 * n_tiles])
+                nc.vector.tensor_copy(out=gain_mean[:, HIDDEN_TILES:n_tiles, 0], in_=vec_bank[:, P : P + OUT_TILES])
+                nc.vector.tensor_copy(
+                    out=zero_shift[:, HIDDEN_TILES:n_tiles, 1], in_=vec_bank[:, P + OUT_TILES : P + 2 * OUT_TILES]
+                )
+                nc.vector.tensor_copy(out=gain_mean[:, 0:HIDDEN_TILES, 0], in_=vec_cols[:, 0:HIDDEN_TILES])
+                nc.vector.tensor_copy(
+                    out=zero_shift[:, 0:HIDDEN_TILES, 1], in_=vec_cols[:, HIDDEN_TILES : 2 * HIDDEN_TILES]
+                )
+                nc.vector.tensor_scalar(
+                    out=minus_gain[:], in0=gain_mean[:, :, 0], scalar1=-1.0, scalar2=None, op0=ALU.mult
+                )
 
             done_units = 0
             for n in range(HEAD_UNITS):
                 quantise(n, group_words(n, transpose_in(n)))
+                if n == 3:
+                    nc.vector.tensor_copy(out=vec_words1[:], in_=vec_rows1[:])
+                if n == 7:
+                    spread_vectors()
             done_units = HEAD_UNITS
-            spread_vectors()
             pending = []
             unquantised = []
             for halves, n_units, todo, on_vector, k in ROUNDS:
@@ -441,34 +454,23 @@ def tile_nodeupdatenetwork_pb_kernel(
                     op0=ALU.mult, op1=ALU.max,
                 )
 
-            def transpose_back(piece, ring):
-                a, half = divmod(piece, 2)
-                for b in range(2):
-                    bank = take_bank(ring)
-                    view = bank[:].rearrange("p (i e c) -> p i e c", i=2, e=2)
-                    for i in range(2):
-                        first_row = BANK * half + PAIR * b + P * i
-                        for e in range(2):
-                            nc.tensor.transpose(
-                                view[:, i, e, :], o1s[2 * a + e][:, first_row : first_row + P], ident[:]
-                            )
-                    back[piece, b] = bank
+            def transpose_back(q, half, ring):
+                bank = take_bank(ring)
+                view = bank[:].rearrange("p (i c) -> p i c", c=P)
+                for i in range(BANK // P):
+                    first_row = BANK * half + P * i
+                    nc.tensor.transpose(view[:, i, :], o1s[q][:, first_row : first_row + P], ident[:])
+                back[q, half] = bank
 
-            def store(piece, b, on_vector=False):
-                a, half = divmod(piece, 2)
-                rows_out = stores.tile([P, 2, PAIR], F32)
-                dest = rows_out[:].rearrange("p i (c e) -> p i c e", e=2)
-                src = back[piece, b][:].rearrange("p (i e c) -> p i c e", i=2, e=2)
+            def store(q, half, on_vector=False):
+                rows_out = stores.tile([P, BANK], F32)
                 if on_vector:
-                    nc.vector.tensor_copy(out=dest, in_=src)
+                    nc.vector.tensor_copy(out=rows_out[:], in_=back[q, half][:])
                 else:
-                    nc.scalar.copy(out=dest, in_=src)
-                first_row = BANK * half + PAIR * b
+                    nc.scalar.copy(out=rows_out[:], in_=back[q, half][:])
                 nc.sync.dma_start(
-                    out=out_rows[first_row : first_row + PAIR, PAIR * a : PAIR * (a + 1)].rearrange(
-                        "(i p) c -> p i c", p=P
-                    ),
-                    in_=rows_out[:],
+                    out=out_rows[BANK * half : BANK * (half + 1), P * q : P * (q + 1)].rearrange("(i p) c -> p i c", p=P),
+                    in_=rows_out[:].rearrange("p (i c) -> p i c", c=P),
                 )
 
             def normalise_out(q, half):
@@ -516,10 +518,10 @@ def tile_nodeupdatenetwork_pb_kernel(
             scale_and_bias(T1 + 1)
             normalise_out(1, 0)
             normalise_out(1, 1)
-            for q in range(2, OUT_TILES + 1):
+            for q in range(2, OUT_TILES):
                 mul = q < OUT_TILES
-                if q >= LAGB + 1:
-                    store(q - LAGB - 1, 0)
+                if q >= 4:
+                    store(q - 4, 1)
                 if q >= 3:
                     mean_and_variance(T1 + q - 1)
                     inverse_deviation(T1 + q - 1)
@@ -530,9 +532,8 @@ def tile_nodeupdatenetwork_pb_kernel(
                 if q >= 3:
                     scale_and_bias(T1 + q - 1)
                 quantise_deferred(LATE_Q[q])
-                if q >= LAGB + 1:
-                    store(q - LAGB - 1, 1)
                 if q >= 3:
+                    store(q - 3, 0)
                     normalise_out(q - 1, 0)
                     normalise_out(q - 1, 1)
                 if mul:
@@ -540,14 +541,26 @@ def tile_nodeupdatenetwork_pb_kernel(
                 leaky_out(q - 2, 1)
                 if mul:
                     half_statistics(T1 + q, 1)
-                if q >= LAGB:
-                    transpose_back(q - LAGB, "out")
+                if q >= 3:
+                    transpose_back(q - 3, 1, "out")
+                transpose_back(q - 2, 0, "out")
+            mean_and_variance(T1 + 7)
+            inverse_deviation(T1 + 7)
+            transpose_back(5, 1, "out")
+            leaky_out(6, 0)
+            store(4, 1)
+            scale_and_bias(T1 + 7)
+            normalise_out(7, 0)
+            normalise_out(7, 1)
+            leaky_out(6, 1)
+            transpose_back(6, 0, "tail")
+            store(5, 0, True)
+            transpose_back(6, 1, "tail")
             leaky_out(7, 0)
-            transpose_back(6, "tail")
-            store(5, 0)
-            store(5, 1)
+            transpose_back(7, 0, "tail")
             leaky_out(7, 1)
-            transpose_back(7, "tail")
+            transpose_back(7, 1, "tail")
+            store(5, 1)
             store(6, 0)
             store(6, 1, True)
             store(7, 0)

@@ -37,23 +37,23 @@ HEAD_UNITS = 15
 LATER = 76
 DEF0 = 4
 LATE_Q = [0, 0, 0, 3, 2, 2, 0, 0, 0]
-RINGS = {"in": [0, 1, 2, 3], "sum": [4, 5, 6, 7], "sum2": [4, 5, 6, 7, 0, 1], "out": [2, 3], "tail": [4, 5, 6, 7]}
-ROUNDS = [([(0, 0), (0, 1)], 5, [], [2], 5),
-          ([(1, 0), (1, 1)], 5, [], [2], 5),
-          ([(2, 0), (2, 1)], 5, [], [2], 5),
-          ([(3, 0), (3, 1)], 4, [], [2], 5),
-          ([(4, 0), (4, 1)], 4, [], [2], 5),
-          ([(5, 0), (5, 1)], 4, [0], [], 2),
-          ([(6, 0), (6, 1)], 4, [1], [], 2),
-          ([(7, 0), (7, 1)], 4, [2], [], 2),
-          ([(8, 0), (8, 1)], 4, [3], [], 2),
-          ([(9, 0), (9, 1)], 4, [4], [], 2),
-          ([(10, 0), (10, 1)], 4, [5], [], 2),
-          ([(11, 0), (11, 1)], 5, [6], [], 2),
-          ([(12, 0), (12, 1)], 4, [7], [], 2),
-          ([(13, 0), (13, 1)], 4, [8], [], 2),
-          ([(14, 0), (14, 1)], 3, [9], [], 2),
-          ([(15, 0), (15, 1)], 3, [10], [], 2)]
+RINGS = {"in": [0, 1, 2, 3], "sum": [4, 5, 6, 7], "sum2": [4, 5, 6, 7, 0, 1], "out": [2, 3], "tail": [0, 1, 4, 5, 6, 7]}
+ROUNDS = [([(0, 0), (0, 1)], 5, [], [2], 3),
+          ([(1, 0), (1, 1)], 5, [], [2], 3),
+          ([(2, 0), (2, 1)], 5, [], [2], 3),
+          ([(3, 0), (3, 1)], 4, [], [2], 3),
+          ([(4, 0), (4, 1)], 4, [], [2], 3),
+          ([(5, 0), (5, 1)], 4, [0], [], 3),
+          ([(6, 0), (6, 1)], 4, [1], [], 3),
+          ([(7, 0), (7, 1)], 4, [2], [], 3),
+          ([(8, 0), (8, 1)], 4, [3], [], 3),
+          ([(9, 0), (9, 1)], 4, [4], [], 3),
+          ([(10, 0), (10, 1)], 4, [5], [], 3),
+          ([(11, 0), (11, 1)], 5, [6], [], 3),
+          ([(12, 0), (12, 1)], 4, [7], [], 3),
+          ([(13, 0), (13, 1)], 4, [8], [], 3),
+          ([(14, 0), (14, 1)], 3, [9], [], 3),
+          ([(15, 0), (15, 1)], 3, [10], [], 3)]
 
 FLOPS = 2 * ROWS * GROUPS * GROUP_K * GROUP_OUT + 2 * ROWS * HIDDEN * OUT_CH
 
@@ -388,9 +388,9 @@ def tile_nodeupdatenetwork_pb_kernel(
                 for tile in pending[:-1]:
                     normalise_hidden(tile, 0)
                     normalise_hidden(tile, 1)
-                for tile, half in halves[:1]:
-                    matmul_half(tile, half)
                 banks += [transpose_in(n) for n in ns[k:]]
+                for tile, half in halves:
+                    matmul_half(tile, half)
                 for j in range(k, n_units - 1):
                     groups.append(group_words(ns[j], banks[j], j in on_vector))
                 for tile, half in halves[:1]:
@@ -402,8 +402,6 @@ def tile_nodeupdatenetwork_pb_kernel(
                     normalise_hidden(tile, 1)
                 if n_units > k:
                     groups.append(group_words(ns[-1], banks[-1], n_units - 1 in on_vector))
-                for tile, half in halves[1:]:
-                    matmul_half(tile, half)
                 for p in unquantised:
                     quantise_piece(p)
                 unquantised = todo[:1]
@@ -546,7 +544,7 @@ def tile_nodeupdatenetwork_pb_kernel(
                 transpose_back(q - 2, 0, "out")
             mean_and_variance(T1 + 7)
             inverse_deviation(T1 + 7)
-            transpose_back(5, 1, "out")
+            transpose_back(5, 1, "tail")
             leaky_out(6, 0)
             store(4, 1)
             scale_and_bias(T1 + 7)

@@ -33,6 +33,9 @@ SLOPE = 0.01
 
 RG = 6
 LAGB = 3
+ARS_AFTER = 1
+N_LAST = True
+STT_AFTER = 0
 HEAD_UNITS = 15
 LATER = 76
 DEF0 = 4
@@ -375,15 +378,16 @@ def tile_nodeupdatenetwork_pb_kernel(
                     leaky_piece(p)
                 for j, n in enumerate(ns[:k]):
                     groups.append(group_words(n, banks[j], j in on_vector))
-                    if j == 0:
+                    if j == min(ARS_AFTER, k - 1):
                         for tile in pending:
                             inverse_deviation(tile)
                 if not ns[:k]:
                     for tile in pending:
                         inverse_deviation(tile)
-                for tile in pending:
-                    scale_and_bias(tile)
                 for j, n in enumerate(ns[:k]):
+                    if j == min(STT_AFTER, k - 1):
+                        for tile in pending:
+                            scale_and_bias(tile)
                     quantise(n, groups[j])
                 for tile in pending[:-1]:
                     normalise_hidden(tile, 0)
@@ -397,10 +401,12 @@ def tile_nodeupdatenetwork_pb_kernel(
                     half_statistics(tile, half)
                 for j in range(k, n_units - 1):
                     quantise(ns[j], groups[j])
+                if n_units > k and N_LAST:
+                    groups.append(group_words(ns[-1], banks[-1], n_units - 1 in on_vector))
                 for tile in pending[-1:]:
                     normalise_hidden(tile, 0)
                     normalise_hidden(tile, 1)
-                if n_units > k:
+                if n_units > k and not N_LAST:
                     groups.append(group_words(ns[-1], banks[-1], n_units - 1 in on_vector))
                 for p in unquantised:
                     quantise_piece(p)
@@ -437,7 +443,7 @@ def tile_nodeupdatenetwork_pb_kernel(
         with ExitStack() as second:
             work = second.enter_context(tc.tile_pool(name="work", bufs=3))
             done = second.enter_context(tc.tile_pool(name="done", bufs=4))
-            stores = second.enter_context(tc.tile_pool(name="stores", bufs=8))
+            stores = second.enter_context(tc.tile_pool(name="stores", bufs=10))
             v1s = {}
             o1s = {}
             back = {}
@@ -517,49 +523,43 @@ def tile_nodeupdatenetwork_pb_kernel(
             normalise_out(1, 0)
             normalise_out(1, 1)
             for q in range(2, OUT_TILES):
-                mul = q < OUT_TILES
-                if q >= 4:
-                    store(q - 4, 1)
                 if q >= 3:
                     mean_and_variance(T1 + q - 1)
                     inverse_deviation(T1 + q - 1)
                 leaky_out(q - 2, 0)
-                if mul:
-                    second_half(q, 0, 0, 4)
-                    half_statistics(T1 + q, 0)
+                second_half(q, 0, 0, 4)
+                half_statistics(T1 + q, 0)
                 if q >= 3:
                     scale_and_bias(T1 + q - 1)
                 quantise_deferred(LATE_Q[q])
                 if q >= 3:
-                    store(q - 3, 0)
                     normalise_out(q - 1, 0)
                     normalise_out(q - 1, 1)
-                if mul:
-                    second_half(q, 1, 0, 4)
-                leaky_out(q - 2, 1)
-                if mul:
-                    half_statistics(T1 + q, 1)
+                second_half(q, 1, 0, 4)
                 if q >= 3:
                     transpose_back(q - 3, 1, "out")
                 transpose_back(q - 2, 0, "out")
+                if q >= 3:
+                    store(q - 3, 1)
+                store(q - 2, 0)
+                leaky_out(q - 2, 1)
+                half_statistics(T1 + q, 1)
             mean_and_variance(T1 + 7)
             inverse_deviation(T1 + 7)
             transpose_back(5, 1, "tail")
             leaky_out(6, 0)
-            store(4, 1)
+            store(5, 1)
             scale_and_bias(T1 + 7)
+            transpose_back(6, 0, "tail")
             normalise_out(7, 0)
             normalise_out(7, 1)
             leaky_out(6, 1)
-            transpose_back(6, 0, "tail")
-            store(5, 0, True)
             transpose_back(6, 1, "tail")
+            store(6, 0, True)
             leaky_out(7, 0)
             transpose_back(7, 0, "tail")
             leaky_out(7, 1)
             transpose_back(7, 1, "tail")
-            store(5, 1)
-            store(6, 0)
-            store(6, 1, True)
+            store(6, 1)
             store(7, 0)
             store(7, 1, True)

@@ -41,22 +41,11 @@ LATER = 76
 DEF0 = 4
 LATE_Q = [0, 0, 0, 3, 2, 2, 0, 0, 0]
 RINGS = {"in": [0, 1, 2, 3], "sum": [4, 5, 6, 7], "sum2": [4, 5, 6, 7, 0, 1], "out": [2, 3], "tail": [0, 1, 4, 5, 6, 7]}
-ROUNDS = [([(0, 0), (0, 1)], 5, [], [2], 3),
-          ([(1, 0), (1, 1)], 5, [], [2], 3),
-          ([(2, 0), (2, 1)], 5, [], [2], 3),
-          ([(3, 0), (3, 1)], 4, [], [2], 3),
-          ([(4, 0), (4, 1)], 4, [], [2], 3),
-          ([(5, 0), (5, 1)], 4, [0], [], 3),
-          ([(6, 0), (6, 1)], 4, [1], [], 3),
-          ([(7, 0), (7, 1)], 4, [2], [], 3),
-          ([(8, 0), (8, 1)], 4, [3], [], 3),
-          ([(9, 0), (9, 1)], 4, [4], [], 3),
-          ([(10, 0), (10, 1)], 4, [5], [], 3),
-          ([(11, 0), (11, 1)], 5, [6], [], 3),
-          ([(12, 0), (12, 1)], 4, [7], [], 3),
-          ([(13, 0), (13, 1)], 4, [8], [], 3),
-          ([(14, 0), (14, 1)], 3, [9], [], 3),
-          ([(15, 0), (15, 1)], 3, [10], [], 3)]
+UNITS = [5, 5, 5, 4, 4, 4, 4, 4, 4, 4, 4, 5, 4, 4, 3, 3]
+FIRST_UNITS = 3
+VECTOR_COPIES = {0: [2], 1: [2], 2: [2]}
+LEAKY = {2 * m + 3 + half: [(m, half)] for m in range(7) for half in range(2)}
+PIECES = {4 * g + 5 + r: [4 * g + r] for g in range(3) for r in range(4)}
 
 FLOPS = 2 * ROWS * GROUPS * GROUP_K * GROUP_OUT + 2 * ROWS * HIDDEN * OUT_CH
 
@@ -170,11 +159,13 @@ def tile_nodeupdatenetwork_pb_kernel(
         w1_raw = whole.enter_context(tc.tile_pool(name="w1_raw", bufs=3))
         w1_grouped = whole.enter_context(tc.tile_pool(name="w1_grouped", bufs=12))
         normed = whole.enter_context(tc.tile_pool(name="normed", bufs=2))
+        leaky = whole.enter_context(tc.tile_pool(name="leaky", bufs=2))
         stream = []
         stage_tiles = []
         deferred = []
         pieces = {}
-        normed_groups = []
+        normed_pairs = []
+        leaky_groups = []
 
         def transpose_in(n, ring="in"):
             pair, c, codes, scales, col0 = stream[n]
@@ -238,35 +229,29 @@ def tile_nodeupdatenetwork_pb_kernel(
             )
 
         def normalise_hidden(tile, half):
-            g, t = divmod(tile, GROUP_TILES)
-            normalise(tile, half, normed_groups[g][:, t, BANK * half : BANK * (half + 1)])
+            m, e = divmod(tile, 2)
+            normalise(tile, half, normed_pairs[m][:, e, BANK * half : BANK * (half + 1)])
 
-        def by_row(piece):
-            g, r = divmod(piece, ROWS // PAIR)
-            return normed_groups[g][:, :, PAIR * r : PAIR * (r + 1)].rearrange("p t n -> p n t")
-
-        def leaky_piece(piece):
-            h_grouped = h_pool.tile([P, 4 * PAIR], BF16, align_bytes=64)
+        def leaky_pair(m, rows):
+            g, u = divmod(m, 2)
+            v = normed_pairs[m][:, :, rows].rearrange("p t n -> p n t")
             nc.vector.scalar_tensor_tensor(
-                out=h_grouped[:].rearrange("p (n t) -> p n t", t=GROUP_TILES),
-                in0=by_row(piece), scalar=SLOPE, in1=by_row(piece), op0=ALU.mult, op1=ALU.max,
+                out=leaky_groups[g][:, u, rows, :], in0=v, scalar=SLOPE, in1=v, op0=ALU.mult, op1=ALU.max,
             )
-            pieces[piece] = h_grouped
 
-        def leaky_terms(piece, pool):
-            up = pool.tile([P, 4 * PAIR], BF16, align_bytes=64)
-            down = pool.tile([P, 4 * PAIR], BF16, align_bytes=64)
-            nc.scalar.activation(
-                out=up[:].rearrange("p (n t) -> p n t", t=GROUP_TILES), in_=by_row(piece), func=ACT.Copy
-            )
-            nc.scalar.activation(
-                out=down[:].rearrange("p (n t) -> p n t", t=GROUP_TILES), in_=by_row(piece), func=ACT.Copy, scale=SLOPE
-            )
-            return up, down
+        def leaky_half(m, half):
+            leaky_pair(m, slice(BANK * half, BANK * (half + 1)))
 
-        def leaky_max(piece, terms):
+        def regroup_piece(piece, on_scalar=False):
+            g, r = divmod(piece, ROWS // PAIR)
             h_grouped = h_pool.tile([P, 4 * PAIR], BF16, align_bytes=64)
-            nc.vector.tensor_tensor(out=h_grouped[:], in0=terms[0][:], in1=terms[1][:], op=ALU.max)
+            pairs = leaky_groups[g][:].rearrange("p u n e -> p u (n e)").bitcast(F32)
+            dest = h_grouped[:].bitcast(F32).rearrange("p (n u) -> p n u", u=2)
+            src = pairs[:, :, PAIR * r : PAIR * (r + 1)].rearrange("p u n -> p n u")
+            if on_scalar:
+                nc.scalar.copy(out=dest, in_=src)
+            else:
+                nc.vector.tensor_copy(out=dest, in_=src)
             pieces[piece] = h_grouped
 
         def quantise_piece(piece):
@@ -337,9 +322,12 @@ def tile_nodeupdatenetwork_pb_kernel(
                     out=w1_pair[:], in_=w1[PAIR * a : PAIR * (a + 1), :].rearrange("(i p) k -> p i k", p=P)
                 )
                 stream.extend([(w1_pair, c, w1_codes, w1_scales, PAIR * a) for c in range(HIDDEN_PASSES)])
+            for m in range(HIDDEN_TILES // 2):
+                v = normed.tile([P, 2, ROWS], F32)
+                normed_pairs.append(v)
             for g in range(GROUPS):
-                v = normed.tile([P, GROUP_TILES, ROWS], F32)
-                normed_groups.append(v)
+                w = leaky.tile([P, 2, ROWS, 2], BF16, align_bytes=64)
+                leaky_groups.append(w)
 
             def spread_vectors():
                 vec_bank = take_bank("in")
@@ -368,77 +356,63 @@ def tile_nodeupdatenetwork_pb_kernel(
                     spread_vectors()
             done_units = HEAD_UNITS
             pending = []
-            unquantised = []
-            for halves, n_units, todo, on_vector, k in ROUNDS:
+            for r in range(HIDDEN_TILES):
+                n_units = UNITS[r]
                 ns = list(range(done_units, done_units + n_units))
                 done_units += n_units
+                k = FIRST_UNITS
+                on_vector = VECTOR_COPIES.get(r, [])
+                todo = PIECES.get(r, [])
                 banks = [transpose_in(n) for n in ns[:k]]
+                for m, half in LEAKY.get(r, []):
+                    leaky_half(m, half)
                 groups = []
-                for p in todo[:1]:
-                    leaky_piece(p)
                 for j, n in enumerate(ns[:k]):
                     groups.append(group_words(n, banks[j], j in on_vector))
-                    if j == min(ARS_AFTER, k - 1):
+                    if j == ARS_AFTER:
                         for tile in pending:
                             inverse_deviation(tile)
-                if not ns[:k]:
-                    for tile in pending:
-                        inverse_deviation(tile)
                 for j, n in enumerate(ns[:k]):
-                    if j == min(STT_AFTER, k - 1):
+                    if j == STT_AFTER:
                         for tile in pending:
                             scale_and_bias(tile)
                     quantise(n, groups[j])
-                for tile in pending[:-1]:
-                    normalise_hidden(tile, 0)
-                    normalise_hidden(tile, 1)
                 banks += [transpose_in(n) for n in ns[k:]]
-                for tile, half in halves:
-                    matmul_half(tile, half)
-                for j in range(k, n_units - 1):
+                matmul_half(r, 0)
+                matmul_half(r, 1)
+                for j in range(k, n_units):
                     groups.append(group_words(ns[j], banks[j], j in on_vector))
-                for tile, half in halves[:1]:
-                    half_statistics(tile, half)
+                for p in todo:
+                    regroup_piece(p)
+                half_statistics(r, 0)
                 for j in range(k, n_units - 1):
                     quantise(ns[j], groups[j])
-                if n_units > k and N_LAST:
-                    groups.append(group_words(ns[-1], banks[-1], n_units - 1 in on_vector))
-                for tile in pending[-1:]:
+                for tile in pending:
                     normalise_hidden(tile, 0)
                     normalise_hidden(tile, 1)
-                if n_units > k and not N_LAST:
-                    groups.append(group_words(ns[-1], banks[-1], n_units - 1 in on_vector))
-                for p in unquantised:
+                for p in todo:
                     quantise_piece(p)
-                unquantised = todo[:1]
-                for p in todo[1:]:
-                    leaky_piece(p)
-                for tile, half in halves[1:]:
-                    half_statistics(tile, half)
+                half_statistics(r, 1)
                 if n_units > k:
                     quantise(ns[-1], groups[-1])
-                for p in todo[1:]:
-                    quantise_piece(p)
-                pending = [tile for tile, half in halves if half == 1]
-                if (15, 1) in halves:
-                    for p in unquantised:
-                        quantise_piece(p)
-                for tile in pending:
-                    mean_and_variance(tile)
+                pending = [r]
+                mean_and_variance(r)
 
             rest = list(range(done_units, len(stream)))
 
             inverse_deviation(15)
-            leaky_piece(11)
+            regroup_piece(11)
             for n in rest[:2]:
                 quantise(n, group_words(n, transpose_in(n)))
             scale_and_bias(15)
             normalise_hidden(15, 0)
             normalise_hidden(15, 1)
             quantise_piece(11)
-            quantise_deferred(DEF0)
+            leaky_half(6, 1)
             second_half(0, 0, 0, 3)
             second_half(0, 1, 0, 3)
+            second_half(1, 0, 0, 3)
+            second_half(1, 1, 0, 3)
 
         with ExitStack() as second:
             work = second.enter_context(tc.tile_pool(name="work", bufs=3))
@@ -485,30 +459,31 @@ def tile_nodeupdatenetwork_pb_kernel(
 
             T1 = HIDDEN_TILES
             banks = [transpose_in(n) for n in rest[2:5]]
-            second_half(1, 0, 0, 3)
-            second_half(1, 1, 0, 3)
-            leaky_piece(12)
-            leaky_piece(13)
-            terms = leaky_terms(14, stores)
+            leaky_pair(7, slice(0, PAIR))
+            leaky_pair(7, slice(PAIR, 2 * PAIR))
+            regroup_piece(12)
+            regroup_piece(13, True)
+            leaky_pair(7, slice(2 * PAIR, 3 * PAIR))
             quantise_piece(12)
+            regroup_piece(14, True)
             quantise_piece(13)
+            leaky_pair(7, slice(3 * PAIR, 4 * PAIR))
+            regroup_piece(15, True)
+            quantise_piece(14)
             second_half(0, 0, 3, 4)
             second_half(1, 0, 3, 4)
             for j, n in enumerate(rest[2:5]):
                 quantise(n, group_words(n, banks[j]))
-            leaky_max(14, terms)
-            leaky_piece(15)
             for n in rest[5:]:
                 quantise(n, group_words(n, transpose_in(n)))
             half_statistics(T1, 0)
-            quantise_piece(14)
             quantise_piece(15)
             second_half(0, 1, 3, 4)
             second_half(1, 1, 3, 4)
             half_statistics(T1 + 1, 0)
-            quantise_deferred(1)
+            quantise_deferred(2)
             half_statistics(T1, 1)
-            quantise_deferred(1)
+            quantise_deferred(2)
             mean_and_variance(T1)
             inverse_deviation(T1)
             half_statistics(T1 + 1, 1)

@@ -32,20 +32,28 @@ EPS_BN = 1e-5
 SLOPE = 0.01
 
 RG = 6
+HEAD_MM = 11
+HEAD_ST = 12
+HEAD_D = 2
+HEAD_VECTOR = []
+SCALAR_PIECES = list(range(12))
 LAGB = 3
 ARS_AFTER = 1
 N_LAST = True
 STT_AFTER = 0
 HEAD_UNITS = 15
-LATER = 76
+LATER = 80
 DEF0 = 4
-LATE_Q = [0, 0, 0, 3, 2, 2, 0, 0, 0]
-RINGS = {"in": [0, 1, 2, 3], "sum": [4, 5, 6, 7], "sum2": [4, 5, 6, 7, 0, 1], "out": [2, 3], "tail": [0, 1, 4, 5, 6, 7]}
+LATE_Q = [0, 0, 0, 1, 1, 2, 0, 0, 0]
+RINGS = {"in": [0, 1, 2, 3], "late": [2, 3], "out": [2, 3, 0, 1], "tail": [6, 7, 2, 3, 0, 1]}
+OUT_BANKS = [4, 0, 6, 4, 6, 4, 6, 4]
+BACK = {3: [(0, 0), (0, 1)], 4: [(1, 0), (1, 1)], 5: [(2, 0), (2, 1), (3, 0)], 6: [(3, 1), (4, 0), (4, 1)], 7: [(5, 0), (5, 1)], 8: [(6, 0), (6, 1), (7, 0), (7, 1)]}
 UNITS = [5, 5, 5, 4, 4, 4, 4, 4, 4, 4, 4, 5, 4, 4, 3, 3]
 FIRST_UNITS = 3
 VECTOR_COPIES = {0: [2], 1: [2], 2: [2]}
 LEAKY = {2 * m + 3 + half: [(m, half)] for m in range(7) for half in range(2)}
 PIECES = {4 * g + 5 + r: [4 * g + r] for g in range(3) for r in range(4)}
+PIECES[15] = [10, 11]
 
 FLOPS = 2 * ROWS * GROUPS * GROUP_K * GROUP_OUT + 2 * ROWS * HIDDEN * OUT_CH
 
@@ -217,12 +225,12 @@ def tile_nodeupdatenetwork_pb_kernel(
         def matmul_half(tile, half):
             g, t = divmod(tile, GROUP_TILES)
             w0_codes, w0_scales, x_codes, x_scales = stage_tiles[g]
-            acc_of[tile, half] = take_bank("sum")
+            acc_of[tile, half] = psum_bank(4 + 2 * (tile % 2) + half)
             multiply(acc_of[tile, half], w0_codes, w0_scales, x_codes, x_scales, GROUP_PASSES, 0, GROUP_PASSES, t, half)
 
         def second_half(q, half, first, last):
             if first == 0:
-                acc_of[HIDDEN_TILES + q, half] = take_bank("sum2")
+                acc_of[HIDDEN_TILES + q, half] = psum_bank(OUT_BANKS[q] + half)
             multiply(
                 acc_of[HIDDEN_TILES + q, half], w1_codes, w1_scales, h_codes, h_scales, HIDDEN_PASSES,
                 first, last, q, half,
@@ -349,7 +357,16 @@ def tile_nodeupdatenetwork_pb_kernel(
 
             done_units = 0
             for n in range(HEAD_UNITS):
-                quantise(n, group_words(n, transpose_in(n)))
+                bank = transpose_in(n)
+                if n == HEAD_MM:
+                    matmul_half(0, 0)
+                if n == HEAD_MM + HEAD_D:
+                    matmul_half(1, 0)
+                quantise(n, group_words(n, bank, n in HEAD_VECTOR))
+                if n == HEAD_ST:
+                    half_statistics(0, 0)
+                if n == HEAD_ST + HEAD_D:
+                    half_statistics(1, 0)
                 if n == 3:
                     nc.vector.tensor_copy(out=vec_words1[:], in_=vec_rows1[:])
                 if n == 7:
@@ -378,21 +395,26 @@ def tile_nodeupdatenetwork_pb_kernel(
                             scale_and_bias(tile)
                     quantise(n, groups[j])
                 banks += [transpose_in(n) for n in ns[k:]]
-                matmul_half(r, 0)
+                if r >= 2:
+                    matmul_half(r, 0)
                 matmul_half(r, 1)
                 for j in range(k, n_units):
                     groups.append(group_words(ns[j], banks[j], j in on_vector))
                 for p in todo:
-                    regroup_piece(p)
-                half_statistics(r, 0)
+                    regroup_piece(p, p in SCALAR_PIECES)
+                if r >= 2:
+                    half_statistics(r, 0)
                 for j in range(k, n_units - 1):
                     quantise(ns[j], groups[j])
                 for tile in pending:
                     normalise_hidden(tile, 0)
                     normalise_hidden(tile, 1)
-                for p in todo:
-                    quantise_piece(p)
+                if r < 15:
+                    for p in todo:
+                        quantise_piece(p)
                 half_statistics(r, 1)
+                if r == 15:
+                    quantise_piece(10)
                 if n_units > k:
                     quantise(ns[-1], groups[-1])
                 pending = [r]
@@ -401,18 +423,16 @@ def tile_nodeupdatenetwork_pb_kernel(
             rest = list(range(done_units, len(stream)))
 
             inverse_deviation(15)
-            regroup_piece(11)
-            for n in rest[:2]:
-                quantise(n, group_words(n, transpose_in(n)))
+            quantise_piece(11)
             scale_and_bias(15)
+            second_half(1, 0, 0, 3)
+            second_half(0, 0, 0, 3)
+            second_half(1, 1, 0, 3)
+            second_half(0, 1, 0, 3)
             normalise_hidden(15, 0)
             normalise_hidden(15, 1)
-            quantise_piece(11)
             leaky_half(6, 1)
-            second_half(0, 0, 0, 3)
-            second_half(0, 1, 0, 3)
-            second_half(1, 0, 0, 3)
-            second_half(1, 1, 0, 3)
+            banks = [transpose_in(n, "late") for n in rest[:2]]
 
         with ExitStack() as second:
             work = second.enter_context(tc.tile_pool(name="work", bufs=3))
@@ -451,90 +471,97 @@ def tile_nodeupdatenetwork_pb_kernel(
                     in_=rows_out[:].rearrange("p (i c) -> p i c", c=P),
                 )
 
-            def normalise_out(q, half):
+            def normalise_out(q, half, on_vector=False):
                 if half == 0:
                     v1 = work.tile([P, ROWS], F32)
                     v1s[q] = v1
-                normalise(HIDDEN_TILES + q, half, v1s[q][:, BANK * half : BANK * (half + 1)])
+                dest = v1s[q][:, BANK * half : BANK * (half + 1)]
+                if on_vector:
+                    scale_bias = scale_bias_of[HIDDEN_TILES + q]
+                    nc.vector.tensor_scalar(
+                        out=dest, in0=acc_of[HIDDEN_TILES + q, half][:], scalar1=scale_bias[:, 0:1],
+                        scalar2=scale_bias[:, 1:2], op0=ALU.mult, op1=ALU.add,
+                    )
+                else:
+                    normalise(HIDDEN_TILES + q, half, dest)
 
             T1 = HIDDEN_TILES
-            banks = [transpose_in(n) for n in rest[2:5]]
-            leaky_pair(7, slice(0, PAIR))
-            leaky_pair(7, slice(PAIR, 2 * PAIR))
-            regroup_piece(12)
-            regroup_piece(13, True)
-            leaky_pair(7, slice(2 * PAIR, 3 * PAIR))
-            quantise_piece(12)
-            regroup_piece(14, True)
-            quantise_piece(13)
-            leaky_pair(7, slice(3 * PAIR, 4 * PAIR))
-            regroup_piece(15, True)
-            quantise_piece(14)
-            second_half(0, 0, 3, 4)
-            second_half(1, 0, 3, 4)
-            for j, n in enumerate(rest[2:5]):
-                quantise(n, group_words(n, banks[j]))
-            for n in rest[5:]:
-                quantise(n, group_words(n, transpose_in(n)))
-            half_statistics(T1, 0)
+            second_half(2, 0, 0, 3)
+            second_half(2, 1, 0, 3)
+            for r in range(4):
+                leaky_pair(7, slice(PAIR * r, PAIR * (r + 1)))
+                regroup_piece(12 + r, True)
+                if r == 1:
+                    for j, n in enumerate(rest[:2]):
+                        quantise(n, group_words(n, banks[j]))
+            for r in range(3):
+                quantise_piece(12 + r)
+            for q in range(3):
+                second_half(q, 0, 3, 4)
             quantise_piece(15)
-            second_half(0, 1, 3, 4)
-            second_half(1, 1, 3, 4)
+            half_statistics(T1, 0)
+            for q in range(3):
+                second_half(q, 1, 3, 4)
+            banks = [transpose_in(n, "late") for n in rest[2:4]]
+            for j, n in enumerate(rest[2:4]):
+                quantise(n, group_words(n, banks[j]))
             half_statistics(T1 + 1, 0)
-            quantise_deferred(2)
             half_statistics(T1, 1)
-            quantise_deferred(2)
-            mean_and_variance(T1)
-            inverse_deviation(T1)
             half_statistics(T1 + 1, 1)
-            scale_and_bias(T1)
-            normalise_out(0, 0)
-            normalise_out(0, 1)
-            quantise_deferred(1)
+            mean_and_variance(T1)
             mean_and_variance(T1 + 1)
+            inverse_deviation(T1)
             inverse_deviation(T1 + 1)
-            quantise_deferred(1)
+            half_statistics(T1 + 2, 0)
+            scale_and_bias(T1)
             scale_and_bias(T1 + 1)
-            normalise_out(1, 0)
-            normalise_out(1, 1)
-            for q in range(2, OUT_TILES):
-                if q >= 3:
-                    mean_and_variance(T1 + q - 1)
-                    inverse_deviation(T1 + q - 1)
-                leaky_out(q - 2, 0)
+            for q in range(2):
+                normalise_out(q, 0)
+                normalise_out(q, 1)
+            banks = [transpose_in(n, "late") for n in rest[4:6]]
+            half_statistics(T1 + 2, 1)
+            quantise_deferred(1)
+            for j, n in enumerate(rest[4:6]):
+                quantise(n, group_words(n, banks[j]))
+            for q in range(3, OUT_TILES):
+                mean_and_variance(T1 + q - 1)
+                inverse_deviation(T1 + q - 1)
+                leaky_out(*BACK[q][0])
                 second_half(q, 0, 0, 4)
+                if q == 3:
+                    quantise_deferred(3)
+                scale_and_bias(T1 + q - 1)
                 half_statistics(T1 + q, 0)
-                if q >= 3:
-                    scale_and_bias(T1 + q - 1)
-                quantise_deferred(LATE_Q[q])
-                if q >= 3:
-                    normalise_out(q - 1, 0)
-                    normalise_out(q - 1, 1)
+                normalise_out(q - 1, 0)
+                normalise_out(q - 1, 1)
                 second_half(q, 1, 0, 4)
-                if q >= 3:
-                    transpose_back(q - 3, 1, "out")
-                transpose_back(q - 2, 0, "out")
-                if q >= 3:
-                    store(q - 3, 1)
-                store(q - 2, 0)
-                leaky_out(q - 2, 1)
+                for piece in BACK[q][1:]:
+                    leaky_out(*piece)
+                quantise_deferred({3: 1, 4: 1, 5: 3, 6: 0, 7: 0}[q])
                 half_statistics(T1 + q, 1)
-            mean_and_variance(T1 + 7)
-            inverse_deviation(T1 + 7)
-            transpose_back(5, 1, "tail")
+                for piece in BACK[q]:
+                    transpose_back(*piece, "out")
+                for piece in BACK[q][:-1]:
+                    store(*piece)
+                if q == 7:
+                    mean_and_variance(T1 + 7)
+                    inverse_deviation(T1 + 7)
+                store(*BACK[q][-1])
+                if q == 4:
+                    for n in rest[6:]:
+                        quantise(n, group_words(n, transpose_in(n, "out")))
             leaky_out(6, 0)
-            store(5, 1)
             scale_and_bias(T1 + 7)
-            transpose_back(6, 0, "tail")
-            normalise_out(7, 0)
-            normalise_out(7, 1)
             leaky_out(6, 1)
+            transpose_back(6, 0, "tail")
             transpose_back(6, 1, "tail")
-            store(6, 0, True)
+            normalise_out(7, 0)
+            normalise_out(7, 1, True)
             leaky_out(7, 0)
             transpose_back(7, 0, "tail")
             leaky_out(7, 1)
             transpose_back(7, 1, "tail")
+            store(6, 0)
             store(6, 1)
             store(7, 0)
             store(7, 1, True)

@@ -36,20 +36,20 @@ HEAD_MM = 11
 HEAD_ST = 12
 HEAD_D = 2
 HEAD_VECTOR = []
-SCALAR_PIECES = list(range(12))
+SCALAR_PIECES = [0, 1, 3, 4, 6, 7, 8, 9, 10, 11]
 LAGB = 3
 ARS_AFTER = 1
 N_LAST = True
 STT_AFTER = 0
 HEAD_UNITS = 15
-LATER = 80
+LATER = 51
 DEF0 = 4
 LATE_Q = [0, 0, 0, 1, 1, 2, 0, 0, 0]
 RINGS = {"in": [0, 1, 2, 3], "late": [2, 3], "out": [2, 3, 0, 1], "tail": [6, 7, 2, 3, 0, 1]}
 OUT_BANKS = [4, 0, 6, 4, 6, 4, 6, 4]
 BACK = {3: [(0, 0), (0, 1)], 4: [(1, 0), (1, 1)], 5: [(2, 0), (2, 1), (3, 0)], 6: [(3, 1), (4, 0), (4, 1)], 7: [(5, 0), (5, 1)], 8: [(6, 0), (6, 1), (7, 0), (7, 1)]}
-UNITS = [5, 5, 5, 4, 4, 4, 4, 4, 4, 4, 4, 5, 4, 4, 3, 3]
-FIRST_UNITS = 3
+ITEMS = [3, 3, 2, 2, 3, 3, 2, 2, 3, 3, 2, 2, 3, 2, 1, 1]
+COPIES_FIRST = 3
 VECTOR_COPIES = {0: [2], 1: [2], 2: [2]}
 LEAKY = {2 * m + 3 + half: [(m, half)] for m in range(7) for half in range(2)}
 PIECES = {4 * g + 5 + r: [4 * g + r] for g in range(3) for r in range(4)}
@@ -94,8 +94,8 @@ def tile_nodeupdatenetwork_pb_kernel(
         minus_gain = const.tile([P, n_tiles], F32)
         zero_shift = const.tile([P, n_tiles, 2], F32)
 
-        w1_codes = kept.tile([P, HIDDEN_PASSES, OUT_CH], U32, align_bytes=64)
-        w1_scales = kept.tile([P, HIDDEN_PASSES, OUT_CH], U8, align_bytes=64)
+        w1_codes = kept.tile([P, OUT_TILES // 2, HIDDEN_PASSES, PAIR], U32, align_bytes=64)
+        w1_scales = kept.tile([P, OUT_TILES // 2, HIDDEN_PASSES, PAIR], U8, align_bytes=64)
         h_codes = kept.tile([P, HIDDEN_PASSES, ROWS], U32, align_bytes=64)
         h_scales = kept.tile([P, HIDDEN_PASSES, ROWS], U8, align_bytes=64)
 
@@ -149,13 +149,14 @@ def tile_nodeupdatenetwork_pb_kernel(
             )
 
         def multiply(acc, w_codes, w_scales, a_codes, a_scales, passes, first, last, w_tile, half):
-            w_cols = slice(P * w_tile, P * (w_tile + 1))
+            a = w_tile // 2
+            w_cols = slice(P * (w_tile % 2), P * (w_tile % 2 + 1))
             r_cols = slice(BANK * half, BANK * (half + 1))
             for c in range(first, last):
                 nc.tensor.matmul_mx(
                     out=acc[:],
-                    lhsT=w_codes[:, c, w_cols].bitcast(FP8X4),
-                    lhsT_scale=w_scales[:, c, w_cols],
+                    lhsT=w_codes[:, a, c, w_cols].bitcast(FP8X4),
+                    lhsT_scale=w_scales[:, a, c, w_cols],
                     rhs=a_codes[:, c, r_cols].bitcast(FP8X4),
                     rhs_scale=a_scales[:, c, r_cols],
                     start=(c == 0),
@@ -165,7 +166,7 @@ def tile_nodeupdatenetwork_pb_kernel(
         regroup = whole.enter_context(tc.tile_pool(name="regroup", bufs=RG))
         h_pool = whole.enter_context(tc.tile_pool(name="h_pool", bufs=4))
         w1_raw = whole.enter_context(tc.tile_pool(name="w1_raw", bufs=3))
-        w1_grouped = whole.enter_context(tc.tile_pool(name="w1_grouped", bufs=12))
+        w1_grouped = whole.enter_context(tc.tile_pool(name="w1_grouped", bufs=3))
         normed = whole.enter_context(tc.tile_pool(name="normed", bufs=2))
         leaky = whole.enter_context(tc.tile_pool(name="leaky", bufs=2))
         stream = []
@@ -175,8 +176,8 @@ def tile_nodeupdatenetwork_pb_kernel(
         normed_pairs = []
         leaky_groups = []
 
-        def transpose_in(n, ring="in"):
-            pair, c, codes, scales, col0 = stream[n]
+        def transpose_unit(unit, ring="in"):
+            pair, c = unit
             bank = take_bank(ring)
             by_word = bank[:].rearrange("p (u n) -> p u n", u=2)
             for i in range(2):
@@ -188,32 +189,37 @@ def tile_nodeupdatenetwork_pb_kernel(
                     )
             return bank
 
-        def group_words(n, bank, on_vector=False):
+        def new_grouped(n):
+            units = len(stream[n][0])
             if n >= LATER:
-                grouped = w1_grouped.tile([P, 4 * PAIR], BF16, align_bytes=64, tag="later")
+                grouped = w1_grouped.tile([P, 4 * PAIR * units], BF16, align_bytes=64, tag="later")
             else:
-                grouped = regroup.tile([P, 4 * PAIR], BF16, align_bytes=64, tag="now")
-            dest = grouped[:].bitcast(F32).rearrange("p (n u) -> p n u", u=2)
+                grouped = regroup.tile([P, 4 * PAIR * units], BF16, align_bytes=64, tag="now%d" % units, bufs=2 + units)
+            return grouped
+
+        def group_words(grouped, j, bank, on_vector=False):
+            dest = grouped[:, 4 * PAIR * j : 4 * PAIR * (j + 1)].bitcast(F32).rearrange("p (n u) -> p n u", u=2)
             src = bank[:].rearrange("p (u n) -> p n u", u=2)
             if on_vector:
                 nc.vector.tensor_copy(out=dest, in_=src)
             else:
                 nc.scalar.copy(out=dest, in_=src)
-            return grouped
 
         def quantise_now(n, grouped):
-            pair, c, codes, scales, col0 = stream[n]
-            nc.vector.quantize_mx(
-                out=codes[:, c, col0 : col0 + PAIR].bitcast(FP8X4),
-                scales=scales[:, c, col0 : col0 + PAIR],
-                in_=grouped[:],
-            )
+            units, codes, scales = stream[n]
+            nc.vector.quantize_mx(out=codes.bitcast(FP8X4), scales=scales, in_=grouped[:])
 
         def quantise(n, grouped):
             if n >= LATER:
                 deferred.append((n, grouped))
             else:
                 quantise_now(n, grouped)
+
+        def bring(n, ring="in"):
+            grouped = new_grouped(n)
+            for j, unit in enumerate(stream[n][0]):
+                group_words(grouped, j, transpose_unit(unit, ring))
+            quantise(n, grouped)
 
         def quantise_deferred(count):
             for n, grouped in deferred[:count]:
@@ -280,8 +286,8 @@ def tile_nodeupdatenetwork_pb_kernel(
                 nc.sync.dma_start(out=vec_rows1[8:16, :], in_=beta1.rearrange("(a w) -> a w", w=P))
 
             def load_stage(stage):
-                w0_codes = staged.tile([P, GROUP_PASSES, GROUP_OUT], U32, align_bytes=64)
-                w0_scales = staged.tile([P, GROUP_PASSES, GROUP_OUT], U8, align_bytes=64)
+                w0_codes = staged.tile([P, 2, GROUP_PASSES, PAIR], U32, align_bytes=64)
+                w0_scales = staged.tile([P, 2, GROUP_PASSES, PAIR], U8, align_bytes=64)
                 x_codes = staged.tile([P, GROUP_PASSES, ROWS], U32, align_bytes=64)
                 x_scales = staged.tile([P, GROUP_PASSES, ROWS], U8, align_bytes=64)
                 stage_tiles.append((w0_codes, w0_scales, x_codes, x_scales))
@@ -296,13 +302,22 @@ def tile_nodeupdatenetwork_pb_kernel(
                             out=w0_pair[:, :, ks],
                             in_=w0[first_row : first_row + PAIR, ks].rearrange("(p e) k -> p e k", e=2),
                         )
-                    stream.extend([(w0_pair, c, w0_codes, w0_scales, PAIR * a) for c in range(GROUP_PASSES)])
+                    cuts = [(0, 1), (1, 2), (2, 3)] if stage == 0 and a == 0 else [(0, 2), (2, 3)]
+                    for c0, c1 in cuts:
+                        stream.append(
+                            (
+                                [(w0_pair, c) for c in range(c0, c1)],
+                                w0_codes[:, a, c0:c1, :].rearrange("p c n -> p (c n)"),
+                                w0_scales[:, a, c0:c1, :].rearrange("p c n -> p (c n)"),
+                            )
+                        )
 
                 load_w0(0)
                 if stage == 0:
                     load_vectors()
                 k0 = GROUP_K * stage
                 from_node = max(0, min(NODE_K - k0, GROUP_K))
+                x_pairs = []
                 for r in range(ROWS // PAIR):
                     rows = slice(PAIR * r, PAIR * (r + 1))
                     x_pair = raw.tile([P, 2, GROUP_K], BF16, tag="pair")
@@ -318,7 +333,13 @@ def tile_nodeupdatenetwork_pb_kernel(
                                 "(i p) k -> p i k", p=P
                             ),
                         )
-                    stream.extend([(x_pair, c, x_codes, x_scales, PAIR * r) for c in range(GROUP_PASSES)])
+                    x_pairs.append(x_pair)
+                run = 1 if stage == 0 else 2
+                for r in range(0, ROWS // PAIR, run):
+                    cols = slice(PAIR * r, PAIR * (r + run))
+                    for c in range(GROUP_PASSES):
+                        units = [(x_pair, c) for x_pair in x_pairs[r : r + run]]
+                        stream.append((units, x_codes[:, c, cols], x_scales[:, c, cols]))
                 load_w0(1)
 
             load_stage(0)
@@ -329,7 +350,14 @@ def tile_nodeupdatenetwork_pb_kernel(
                 nc.sync.dma_start(
                     out=w1_pair[:], in_=w1[PAIR * a : PAIR * (a + 1), :].rearrange("(i p) k -> p i k", p=P)
                 )
-                stream.extend([(w1_pair, c, w1_codes, w1_scales, PAIR * a) for c in range(HIDDEN_PASSES)])
+                for c in range(0, HIDDEN_PASSES, 2):
+                    stream.append(
+                        (
+                            [(w1_pair, c), (w1_pair, c + 1)],
+                            w1_codes[:, a, c : c + 2, :].rearrange("p c n -> p (c n)"),
+                            w1_scales[:, a, c : c + 2, :].rearrange("p c n -> p (c n)"),
+                        )
+                    )
             for m in range(HIDDEN_TILES // 2):
                 v = normed.tile([P, 2, ROWS], F32)
                 normed_pairs.append(v)
@@ -355,14 +383,15 @@ def tile_nodeupdatenetwork_pb_kernel(
                     out=minus_gain[:], in0=gain_mean[:, :, 0], scalar1=-1.0, scalar2=None, op0=ALU.mult
                 )
 
-            done_units = 0
             for n in range(HEAD_UNITS):
-                bank = transpose_in(n)
+                grouped = new_grouped(n)
+                bank = transpose_unit(stream[n][0][0])
                 if n == HEAD_MM:
                     matmul_half(0, 0)
                 if n == HEAD_MM + HEAD_D:
                     matmul_half(1, 0)
-                quantise(n, group_words(n, bank, n in HEAD_VECTOR))
+                group_words(grouped, 0, bank)
+                quantise(n, grouped)
                 if n == HEAD_ST:
                     half_statistics(0, 0)
                 if n == HEAD_ST + HEAD_D:
@@ -371,56 +400,63 @@ def tile_nodeupdatenetwork_pb_kernel(
                     nc.vector.tensor_copy(out=vec_words1[:], in_=vec_rows1[:])
                 if n == 7:
                     spread_vectors()
-            done_units = HEAD_UNITS
             pending = []
+            carry = []
+            following = HEAD_UNITS
             for r in range(HIDDEN_TILES):
-                n_units = UNITS[r]
-                ns = list(range(done_units, done_units + n_units))
-                done_units += n_units
-                k = FIRST_UNITS
-                on_vector = VECTOR_COPIES.get(r, [])
+                items = list(range(following, following + ITEMS[r]))
+                following += ITEMS[r]
                 todo = PIECES.get(r, [])
-                banks = [transpose_in(n) for n in ns[:k]]
+                units = [(n, j, unit) for n in items for j, unit in enumerate(stream[n][0])]
+                grouped = {}
+                for n in items:
+                    g = new_grouped(n)
+                    grouped[n] = g
                 for m, half in LEAKY.get(r, []):
                     leaky_half(m, half)
-                groups = []
-                for j, n in enumerate(ns[:k]):
-                    groups.append(group_words(n, banks[j], j in on_vector))
-                    if j == ARS_AFTER:
+                for n, g in carry:
+                    quantise(n, g)
+                banks = [transpose_unit(unit) for n, j, unit in units]
+                for i, (n, j, unit) in enumerate(units[:COPIES_FIRST]):
+                    group_words(grouped[n], j, banks[i], i in VECTOR_COPIES.get(r, []))
+                    if i == ARS_AFTER:
                         for tile in pending:
                             inverse_deviation(tile)
-                for j, n in enumerate(ns[:k]):
-                    if j == STT_AFTER:
-                        for tile in pending:
-                            scale_and_bias(tile)
-                    quantise(n, groups[j])
-                banks += [transpose_in(n) for n in ns[k:]]
+                if not units:
+                    for tile in pending:
+                        inverse_deviation(tile)
+                for tile in pending:
+                    scale_and_bias(tile)
+                for n in items[:1]:
+                    quantise(n, grouped[n])
                 if r >= 2:
                     matmul_half(r, 0)
                 matmul_half(r, 1)
-                for j in range(k, n_units):
-                    groups.append(group_words(ns[j], banks[j], j in on_vector))
+                for i, (n, j, unit) in list(enumerate(units))[COPIES_FIRST:]:
+                    group_words(grouped[n], j, banks[i], i in VECTOR_COPIES.get(r, []))
                 for p in todo:
                     regroup_piece(p, p in SCALAR_PIECES)
                 if r >= 2:
                     half_statistics(r, 0)
-                for j in range(k, n_units - 1):
-                    quantise(ns[j], groups[j])
+                if todo:
+                    for n in items[1:-1]:
+                        quantise(n, grouped[n])
                 for tile in pending:
                     normalise_hidden(tile, 0)
                     normalise_hidden(tile, 1)
-                if r < 15:
-                    for p in todo:
-                        quantise_piece(p)
                 half_statistics(r, 1)
-                if r == 15:
-                    quantise_piece(10)
-                if n_units > k:
-                    quantise(ns[-1], groups[-1])
+                if not todo:
+                    for n in items[1:-1]:
+                        quantise(n, grouped[n])
+                for p in todo[:1]:
+                    quantise_piece(p)
+                carry = [(n, grouped[n]) for n in items[1:][-1:]]
                 pending = [r]
                 mean_and_variance(r)
+            for n, g in carry:
+                quantise(n, g)
 
-            rest = list(range(done_units, len(stream)))
+            rest = list(range(following, len(stream)))
 
             inverse_deviation(15)
             quantise_piece(11)
@@ -432,7 +468,8 @@ def tile_nodeupdatenetwork_pb_kernel(
             normalise_hidden(15, 0)
             normalise_hidden(15, 1)
             leaky_half(6, 1)
-            banks = [transpose_in(n, "late") for n in rest[:2]]
+            late = new_grouped(rest[0])
+            banks = [transpose_unit(unit, "late") for unit in stream[rest[0]][0]]
 
         with ExitStack() as second:
             work = second.enter_context(tc.tile_pool(name="work", bufs=3))
@@ -491,9 +528,10 @@ def tile_nodeupdatenetwork_pb_kernel(
             for r in range(4):
                 leaky_pair(7, slice(PAIR * r, PAIR * (r + 1)))
                 regroup_piece(12 + r, True)
-                if r == 1:
-                    for j, n in enumerate(rest[:2]):
-                        quantise(n, group_words(n, banks[j]))
+                if r == 3:
+                    for j, bank in enumerate(banks):
+                        group_words(late, j, bank)
+                    quantise(rest[0], late)
             for r in range(3):
                 quantise_piece(12 + r)
             for q in range(3):
@@ -502,9 +540,7 @@ def tile_nodeupdatenetwork_pb_kernel(
             half_statistics(T1, 0)
             for q in range(3):
                 second_half(q, 1, 3, 4)
-            banks = [transpose_in(n, "late") for n in rest[2:4]]
-            for j, n in enumerate(rest[2:4]):
-                quantise(n, group_words(n, banks[j]))
+            bring(rest[1], "late")
             half_statistics(T1 + 1, 0)
             half_statistics(T1, 1)
             half_statistics(T1 + 1, 1)
@@ -518,18 +554,20 @@ def tile_nodeupdatenetwork_pb_kernel(
             for q in range(2):
                 normalise_out(q, 0)
                 normalise_out(q, 1)
-            banks = [transpose_in(n, "late") for n in rest[4:6]]
+            late = new_grouped(rest[2])
+            banks = [transpose_unit(unit, "late") for unit in stream[rest[2]][0]]
             half_statistics(T1 + 2, 1)
             quantise_deferred(1)
-            for j, n in enumerate(rest[4:6]):
-                quantise(n, group_words(n, banks[j]))
+            for j, bank in enumerate(banks):
+                group_words(late, j, bank)
+            quantise(rest[2], late)
             for q in range(3, OUT_TILES):
                 mean_and_variance(T1 + q - 1)
                 inverse_deviation(T1 + q - 1)
                 leaky_out(*BACK[q][0])
                 second_half(q, 0, 0, 4)
                 if q == 3:
-                    quantise_deferred(3)
+                    quantise_deferred(1)
                 scale_and_bias(T1 + q - 1)
                 half_statistics(T1 + q, 0)
                 normalise_out(q - 1, 0)
@@ -537,7 +575,7 @@ def tile_nodeupdatenetwork_pb_kernel(
                 second_half(q, 1, 0, 4)
                 for piece in BACK[q][1:]:
                     leaky_out(*piece)
-                quantise_deferred({3: 1, 4: 1, 5: 3, 6: 0, 7: 0}[q])
+                quantise_deferred({3: 0, 4: 1, 5: 1, 6: 0, 7: 0}[q])
                 half_statistics(T1 + q, 1)
                 for piece in BACK[q]:
                     transpose_back(*piece, "out")
@@ -548,8 +586,8 @@ def tile_nodeupdatenetwork_pb_kernel(
                     inverse_deviation(T1 + 7)
                 store(*BACK[q][-1])
                 if q == 4:
-                    for n in rest[6:]:
-                        quantise(n, group_words(n, transpose_in(n, "out")))
+                    for n in rest[3:]:
+                        bring(n, "out")
             leaky_out(6, 0)
             scale_and_bias(T1 + 7)
             leaky_out(6, 1)

@@ -45,9 +45,10 @@ HEAD_UNITS = 15
 LATER = 51
 DEF0 = 4
 LATE_Q = [0, 0, 0, 1, 1, 2, 0, 0, 0]
-RINGS = {"in": [0, 1, 2, 3], "late": [2, 3], "out": [2, 3, 0, 1], "tail": [6, 7, 2, 3, 0, 1]}
+RINGS = {"in": [0, 1, 2, 3], "late": [2, 3], "out": [0, 1, 2, 3], "tail": [6, 7, 0, 1, 2, 3]}
 OUT_BANKS = [4, 0, 6, 4, 6, 4, 6, 4]
-BACK = {3: [(0, 0), (0, 1)], 4: [(1, 0), (1, 1)], 5: [(2, 0), (2, 1), (3, 0)], 6: [(3, 1), (4, 0), (4, 1)], 7: [(5, 0), (5, 1)], 8: [(6, 0), (6, 1), (7, 0), (7, 1)]}
+BACK = {3: [(0, 1), (1, 0)], 4: [(1, 1), (2, 0)], 5: [(2, 1), (3, 0), (3, 1)], 6: [(4, 0), (4, 1)], 7: [(5, 0), (5, 1)]}
+TB = {3: [(0, 0), (0, 1)], 4: [(1, 0), (1, 1)], 5: [(2, 0), (2, 1), (3, 0)], 6: [(3, 1), (4, 0)], 7: [(4, 1), (5, 0), (5, 1)], 8: [(6, 0), (6, 1)]}
 ITEMS = [3, 3, 2, 2, 3, 3, 2, 2, 3, 3, 2, 2, 3, 2, 1, 1]
 COPIES_FIRST = 3
 VECTOR_COPIES = {0: [2], 1: [2], 2: [2]}
@@ -295,7 +296,7 @@ def tile_nodeupdatenetwork_pb_kernel(
                 def load_w0(a):
                     first_row = GROUP_OUT * stage + PAIR * a
                     w0_pair = raw.tile([P, 2, GROUP_K], BF16, tag="pair")
-                    cuts = GROUP_PASSES if (stage == 0 and a == 0) else 1
+                    cuts = 1
                     for j in range(cuts):
                         ks = slice(GROUP_K // cuts * j, GROUP_K // cuts * (j + 1))
                         nc.sync.dma_start(
@@ -313,8 +314,6 @@ def tile_nodeupdatenetwork_pb_kernel(
                         )
 
                 load_w0(0)
-                if stage == 0:
-                    load_vectors()
                 k0 = GROUP_K * stage
                 from_node = max(0, min(NODE_K - k0, GROUP_K))
                 x_pairs = []
@@ -334,6 +333,8 @@ def tile_nodeupdatenetwork_pb_kernel(
                             ),
                         )
                     x_pairs.append(x_pair)
+                    if stage == 0 and r == 1:
+                        load_vectors()
                 run = 1 if stage == 0 else 2
                 for r in range(0, ROWS // PAIR, run):
                     cols = slice(PAIR * r, PAIR * (r + run))
@@ -396,9 +397,9 @@ def tile_nodeupdatenetwork_pb_kernel(
                     half_statistics(0, 0)
                 if n == HEAD_ST + HEAD_D:
                     half_statistics(1, 0)
-                if n == 3:
+                if n == 8:
                     nc.vector.tensor_copy(out=vec_words1[:], in_=vec_rows1[:])
-                if n == 7:
+                if n == 11:
                     spread_vectors()
             pending = []
             carry = []
@@ -558,48 +559,57 @@ def tile_nodeupdatenetwork_pb_kernel(
             banks = [transpose_unit(unit, "late") for unit in stream[rest[2]][0]]
             half_statistics(T1 + 2, 1)
             quantise_deferred(1)
+            mean_and_variance(T1 + 2)
+            inverse_deviation(T1 + 2)
+            leaky_out(0, 0)
+            scale_and_bias(T1 + 2)
+            normalise_out(2, 0)
+            normalise_out(2, 1)
             for j, bank in enumerate(banks):
                 group_words(late, j, bank)
             quantise(rest[2], late)
             for q in range(3, OUT_TILES):
-                mean_and_variance(T1 + q - 1)
-                inverse_deviation(T1 + q - 1)
+                if q > 3:
+                    mean_and_variance(T1 + q - 1)
+                    inverse_deviation(T1 + q - 1)
                 leaky_out(*BACK[q][0])
                 second_half(q, 0, 0, 4)
                 if q == 3:
                     quantise_deferred(1)
-                scale_and_bias(T1 + q - 1)
+                if q > 3:
+                    scale_and_bias(T1 + q - 1)
                 half_statistics(T1 + q, 0)
-                normalise_out(q - 1, 0)
-                normalise_out(q - 1, 1)
+                if q > 3:
+                    normalise_out(q - 1, 0)
+                    normalise_out(q - 1, 1)
                 second_half(q, 1, 0, 4)
                 for piece in BACK[q][1:]:
                     leaky_out(*piece)
                 quantise_deferred({3: 0, 4: 1, 5: 1, 6: 0, 7: 0}[q])
                 half_statistics(T1 + q, 1)
-                for piece in BACK[q]:
+                for piece in TB[q]:
                     transpose_back(*piece, "out")
-                for piece in BACK[q][:-1]:
+                for piece in TB[q][:-1]:
                     store(*piece)
                 if q == 7:
                     mean_and_variance(T1 + 7)
                     inverse_deviation(T1 + 7)
-                store(*BACK[q][-1])
+                store(*TB[q][-1])
                 if q == 4:
                     for n in rest[3:]:
                         bring(n, "out")
             leaky_out(6, 0)
             scale_and_bias(T1 + 7)
             leaky_out(6, 1)
-            transpose_back(6, 0, "tail")
-            transpose_back(6, 1, "tail")
+            for piece in TB[8]:
+                transpose_back(*piece, "tail")
             normalise_out(7, 0)
             normalise_out(7, 1, True)
             leaky_out(7, 0)
             transpose_back(7, 0, "tail")
             leaky_out(7, 1)
             transpose_back(7, 1, "tail")
-            store(6, 0)
-            store(6, 1)
+            for piece in TB[8]:
+                store(*piece)
             store(7, 0)
             store(7, 1, True)

@@ -475,10 +475,11 @@ def tile_nodeupdatenetwork_pb_kernel(
         with ExitStack() as second:
             work = second.enter_context(tc.tile_pool(name="work", bufs=3))
             done = second.enter_context(tc.tile_pool(name="done", bufs=4))
-            stores = second.enter_context(tc.tile_pool(name="stores", bufs=10))
+            stores = second.enter_context(tc.tile_pool(name="stores", bufs=6))
             v1s = {}
             o1s = {}
             back = {}
+            rows_outs = {}
 
             def leaky_out(q, half):
                 if half == 0:
@@ -499,15 +500,22 @@ def tile_nodeupdatenetwork_pb_kernel(
                 back[q, half] = bank
 
             def store(q, half, on_vector=False):
-                rows_out = stores.tile([P, BANK], F32)
+                if q % 2 == 0:
+                    rows_out = stores.tile([P, BANK // P, 2 * P], F32)
+                    rows_outs[half] = rows_out
+                dest = rows_outs[half][:, :, P * (q % 2) : P * (q % 2 + 1)]
+                src = back[q, half][:].rearrange("p (i c) -> p i c", c=P)
                 if on_vector:
-                    nc.vector.tensor_copy(out=rows_out[:], in_=back[q, half][:])
+                    nc.vector.tensor_copy(out=dest, in_=src)
                 else:
-                    nc.scalar.copy(out=rows_out[:], in_=back[q, half][:])
-                nc.sync.dma_start(
-                    out=out_rows[BANK * half : BANK * (half + 1), P * q : P * (q + 1)].rearrange("(i p) c -> p i c", p=P),
-                    in_=rows_out[:].rearrange("p (i c) -> p i c", c=P),
-                )
+                    nc.scalar.copy(out=dest, in_=src)
+                if q % 2 == 1:
+                    nc.sync.dma_start(
+                        out=out_rows[BANK * half : BANK * (half + 1), P * (q - 1) : P * (q + 1)].rearrange(
+                            "(i p) c -> p i c", p=P
+                        ),
+                        in_=rows_outs[half][:],
+                    )
 
             def normalise_out(q, half, on_vector=False):
                 if half == 0:

@@ -36,6 +36,7 @@ HEAD_MM = 11
 HEAD_ST = 12
 HEAD_D = 2
 HEAD_VECTOR = []
+SPLIT = 4
 SCALAR_PIECES = [0, 1, 3, 4, 6, 7, 8, 9, 10, 11]
 LAGB = 3
 ARS_AFTER = 1
@@ -417,7 +418,10 @@ def tile_nodeupdatenetwork_pb_kernel(
                     leaky_half(m, half)
                 for n, g in carry:
                     quantise(n, g)
-                banks = [transpose_unit(unit) for n, j, unit in units]
+                banks = [transpose_unit(unit) for n, j, unit in units[:SPLIT]]
+                if r >= 2:
+                    matmul_half(r, 0)
+                banks += [transpose_unit(unit) for n, j, unit in units[SPLIT:]]
                 for i, (n, j, unit) in enumerate(units[:COPIES_FIRST]):
                     group_words(grouped[n], j, banks[i], i in VECTOR_COPIES.get(r, []))
                     if i == ARS_AFTER:
@@ -430,8 +434,6 @@ def tile_nodeupdatenetwork_pb_kernel(
                     scale_and_bias(tile)
                 for n in items[:1]:
                     quantise(n, grouped[n])
-                if r >= 2:
-                    matmul_half(r, 0)
                 matmul_half(r, 1)
                 for i, (n, j, unit) in list(enumerate(units))[COPIES_FIRST:]:
                     group_words(grouped[n], j, banks[i], i in VECTOR_COPIES.get(r, []))

@@ -36,6 +36,9 @@ HEAD_MM = 11
 HEAD_ST = 12
 HEAD_D = 2
 HEAD_VECTOR = []
+WARM_FIRST = 7
+WARM = 2
+WARM_AFTER = [2, 5, 8]
 SPLIT = 4
 SCALAR_PIECES = [0, 1, 3, 4, 6, 7, 8, 9, 10, 11]
 LAGB = 3
@@ -81,6 +84,8 @@ def tile_nodeupdatenetwork_pb_kernel(
 
         ident = const.tile([P, P], F32)
         make_identity(nc, ident[:])
+        zeros = const.tile([P, BANK], BF16)
+        nc.vector.memset(zeros[:], 0.0)
         eps = const.tile([P, 1], F32)
         nc.vector.memset(eps[:], EPS_BN)
         warm = const.tile([P, 1], F32)
@@ -177,6 +182,10 @@ def tile_nodeupdatenetwork_pb_kernel(
         pieces = {}
         normed_pairs = []
         leaky_groups = []
+
+        def keep_warm(bank, count):
+            for i in range(count):
+                nc.tensor.matmul(bank[:], lhsT=zeros[:, 0:P], rhs=zeros[:], start=True, stop=True)
 
         def transpose_unit(unit, ring="in"):
             pair, c = unit
@@ -385,9 +394,13 @@ def tile_nodeupdatenetwork_pb_kernel(
                     out=minus_gain[:], in0=gain_mean[:, :, 0], scalar1=-1.0, scalar2=None, op0=ALU.mult
                 )
 
+            idle_bank = psum_bank(7)
+            keep_warm(idle_bank, WARM_FIRST)
             for n in range(HEAD_UNITS):
                 grouped = new_grouped(n)
                 bank = transpose_unit(stream[n][0][0])
+                if n in WARM_AFTER:
+                    keep_warm(idle_bank, WARM)
                 if n == HEAD_MM:
                     matmul_half(0, 0)
                 if n == HEAD_MM + HEAD_D:

@@ -575,15 +575,16 @@ def tile_nodeupdatenetwork_pb_kernel(
             half_statistics(T1 + 2, 0)
             scale_and_bias(T1)
             scale_and_bias(T1 + 1)
-            for q in range(2):
-                normalise_out(q, 0)
-                normalise_out(q, 1)
+            normalise_out(0, 0)
+            normalise_out(0, 1)
+            normalise_out(1, 0)
             late = new_grouped(rest[2])
             banks = [transpose_unit(unit, "late") for unit in stream[rest[2]][0]]
             half_statistics(T1 + 2, 1)
             quantise_deferred(1)
             mean_and_variance(T1 + 2)
             inverse_deviation(T1 + 2)
+            normalise_out(1, 1)
             leaky_out(0, 0)
             scale_and_bias(T1 + 2)
             normalise_out(2, 0)
@@ -606,10 +607,11 @@ def tile_nodeupdatenetwork_pb_kernel(
                     normalise_out(q - 1, 0)
                     normalise_out(q - 1, 1)
                 second_half(q, 1, 0, 4)
-                for piece in BACK[q][1:]:
-                    leaky_out(*piece)
-                quantise_deferred({3: 0, 4: 1, 5: 1, 6: 0, 7: 0}[q])
+                leaky_out(*BACK[q][1])
                 half_statistics(T1 + q, 1)
+                quantise_deferred({3: 0, 4: 1, 5: 1, 6: 0, 7: 0}[q])
+                for piece in BACK[q][2:]:
+                    leaky_out(*piece)
                 for piece in TB[q]:
                     transpose_back(*piece, "out")
                 for piece in TB[q][:-1]:

@@ -36,7 +36,7 @@ HEAD_MM = 11
 HEAD_ST = 12
 HEAD_D = 2
 HEAD_VECTOR = []
-WARM_FIRST = 7
+WARM_FIRST = 5
 WARM = 2
 WARM_AFTER = [2, 5, 8]
 SPLIT = 4
@@ -306,7 +306,7 @@ def tile_nodeupdatenetwork_pb_kernel(
                 def load_w0(a):
                     first_row = GROUP_OUT * stage + PAIR * a
                     w0_pair = raw.tile([P, 2, GROUP_K], BF16, tag="pair")
-                    cuts = 1
+                    cuts = GROUP_PASSES if (stage == 0 and a == 0) else 1
                     for j in range(cuts):
                         ks = slice(GROUP_K // cuts * j, GROUP_K // cuts * (j + 1))
                         nc.sync.dma_start(
@@ -593,9 +593,6 @@ def tile_nodeupdatenetwork_pb_kernel(
                 group_words(late, j, bank)
             quantise(rest[2], late)
             for q in range(3, OUT_TILES):
-                if q > 3:
-                    mean_and_variance(T1 + q - 1)
-                    inverse_deviation(T1 + q - 1)
                 leaky_out(*BACK[q][0])
                 second_half(q, 0, 0, 4)
                 if q == 3:
@@ -616,9 +613,8 @@ def tile_nodeupdatenetwork_pb_kernel(
                     transpose_back(*piece, "out")
                 for piece in TB[q][:-1]:
                     store(*piece)
-                if q == 7:
-                    mean_and_variance(T1 + 7)
-                    inverse_deviation(T1 + 7)
+                mean_and_variance(T1 + q)
+                inverse_deviation(T1 + q)
                 store(*TB[q][-1])
                 if q == 4:
                     for n in rest[3:]:

from contextlib import ExitStack

import concourse.mybir as mybir
from concourse.masks import make_identity

F32 = mybir.dt.float32
BF16 = mybir.dt.bfloat16
U32 = mybir.dt.uint32
U8 = mybir.dt.uint8
FP8X4 = mybir.dt.float8_e4m3fn_x4
ALU = mybir.AluOpType
ACT = mybir.ActivationFunctionType

P = 128
ROWS = 1024
NODE_K = 2048
GROUPS = 4
GROUP_K = 1536
GROUP_OUT = 512
GROUP_PASSES = 3
GROUP_TILES = 4
HIDDEN = 2048
HIDDEN_PASSES = 4
HIDDEN_TILES = 16
OUT_CH = 1024
OUT_TILES = 8
PASS_WORDS = 256
BANK = 512
PAIR = 256
STATS = 6
EPS_BN = 1e-5
SLOPE = 0.01

RG = 6
HEAD_MM = 11
HEAD_ST = 12
HEAD_D = 2
HEAD_VECTOR = []
WARM_FIRST = 5
WARM = 2
WARM_AFTER = [2, 5, 8]
SPLIT = 4
SCALAR_PIECES = [0, 1, 3, 4, 6, 7, 8, 9, 10, 11]
LAGB = 3
ARS_AFTER = 1
N_LAST = True
STT_AFTER = 0
HEAD_UNITS = 15
LATER = 51
DEF0 = 4
LATE_Q = [0, 0, 0, 1, 1, 2, 0, 0, 0]
RINGS = {"in": [0, 1, 2, 3], "late": [2, 3], "out": [0, 1, 2, 3], "tail": [6, 7, 0, 1, 2, 3]}
OUT_BANKS = [4, 0, 6, 4, 6, 4, 6, 4]
BACK = {3: [(0, 1), (1, 0)], 4: [(1, 1), (2, 0)], 5: [(2, 1), (3, 0), (3, 1)], 6: [(4, 0), (4, 1)], 7: [(5, 0), (5, 1)]}
TB = {3: [(0, 0), (0, 1)], 4: [(1, 0), (1, 1)], 5: [(2, 0), (2, 1), (3, 0)], 6: [(3, 1), (4, 0)], 7: [(4, 1), (5, 0), (5, 1)], 8: [(6, 0), (6, 1)]}
ITEMS = [3, 3, 2, 2, 3, 3, 2, 2, 3, 3, 2, 2, 3, 2, 1, 1]
COPIES_FIRST = 3
VECTOR_COPIES = {0: [2], 1: [2], 2: [2]}
LEAKY = {2 * m + 3 + half: [(m, half)] for m in range(7) for half in range(2)}
PIECES = {4 * g + 5 + r: [4 * g + r] for g in range(3) for r in range(4)}
PIECES[15] = [10, 11]

FLOPS = 2 * ROWS * GROUPS * GROUP_K * GROUP_OUT + 2 * ROWS * HIDDEN * OUT_CH


def tile_nodeupdatenetwork_pb_kernel(
    tc, node_feat, aggr, w0, gamma0, beta0, w1, gamma1, beta1, out
):
    nc = tc.nc
    node_rows = node_feat.flatten_outer_dims()
    aggr_rows = aggr.flatten_outer_dims()
    out_rows = out.flatten_outer_dims()

    with ExitStack() as whole:
        whole.enter_context(tc.manual_schedule())
        const = whole.enter_context(tc.tile_pool(name="const", bufs=1))
        small = whole.enter_context(tc.tile_pool(name="small", bufs=4))
        kept = whole.enter_context(tc.tile_pool(name="kept", bufs=1))
        psum = whole.enter_context(tc.psum_pool(name="psum", bufs=1))

        def psum_bank(k):
            bank = psum.tile([P, BANK], F32, tag="bank%d" % k)
            return bank

        ident = const.tile([P, P], F32)
        make_identity(nc, ident[:])
        zeros = const.tile([P, BANK], BF16)
        nc.vector.memset(zeros[:], 0.0)
        eps = const.tile([P, 1], F32)
        nc.vector.memset(eps[:], EPS_BN)
        warm = const.tile([P, 1], F32)
        nc.scalar.activation(out=warm[:], in_=eps[:], func=ACT.Abs_reciprocal_sqrt)
        vec_rows = const.tile([P, 2 * P], BF16)
        nc.vector.memset(vec_rows[:], 0.0)
        vec_rows1 = const.tile([P, P], BF16)
        nc.vector.memset(vec_rows1[:], 0.0)
        vec_words1 = const.tile([P, P], F32)
        n_tiles = HIDDEN_TILES + OUT_TILES
        vec_cols = const.tile([P, 2 * P], BF16)
        gain_mean = const.tile([P, n_tiles, 2], F32)
        minus_gain = const.tile([P, n_tiles], F32)
        zero_shift = const.tile([P, n_tiles, 2], F32)

        w1_codes = kept.tile([P, OUT_TILES // 2, HIDDEN_PASSES, PAIR], U32, align_bytes=64)
        w1_scales = kept.tile([P, OUT_TILES // 2, HIDDEN_PASSES, PAIR], U8, align_bytes=64)
        h_codes = kept.tile([P, HIDDEN_PASSES, ROWS], U32, align_bytes=64)
        h_scales = kept.tile([P, HIDDEN_PASSES, ROWS], U8, align_bytes=64)

        state = {}

        def take_bank(ring):
            n = state.get(ring, 0)
            state[ring] = n + 1
            return psum_bank(RINGS[ring][n % len(RINGS[ring])])

        class_stats = {}
        mean_var_of = {}
        rstd_of = {}
        scale_bias_of = {}
        acc_of = {}

        def half_statistics(tile, half):
            if half == 0:
                stats = small.tile([P, 2, STATS], F32)
                class_stats[tile] = stats
            nc.vector.bn_stats(out=class_stats[tile][:, half, :], in_=acc_of[tile, half][:])

        def mean_and_variance(tile):
            mean_var = small.tile([P, 2], F32)
            nc.vector.bn_aggr(out=mean_var[:], in_=class_stats[tile][:].rearrange("p h s -> p (h s)"))
            mean_var_of[tile] = mean_var

        def inverse_deviation(tile):
            rstd = small.tile([P, 1], F32)
            nc.scalar.activation(
                out=rstd[:], in_=mean_var_of[tile][:, 1:2], func=ACT.Abs_reciprocal_sqrt, bias=eps[:, 0:1]
            )
            nc.scalar.activation(
                out=gain_mean[:, tile, 1:2], in_=mean_var_of[tile][:, 0:1], func=ACT.Identity,
                scale=minus_gain[:, tile : tile + 1],
            )
            rstd_of[tile] = rstd

        def scale_and_bias(tile):
            scale_bias = small.tile([P, 2], F32)
            nc.vector.scalar_tensor_tensor(
                out=scale_bias[:], in0=gain_mean[:, tile, :], scalar=rstd_of[tile][:, 0:1],
                in1=zero_shift[:, tile, :], op0=ALU.mult, op1=ALU.add,
            )
            scale_bias_of[tile] = scale_bias

        def normalise(tile, half, dest):
            nc.scalar.activation(
                out=dest, in_=acc_of[tile, half][:], func=ACT.Identity,
                scale=scale_bias_of[tile][:, 0:1], bias=scale_bias_of[tile][:, 1:2],
            )

        def multiply(acc, w_codes, w_scales, a_codes, a_scales, passes, first, last, w_tile, half):
            a = w_tile // 2
            w_cols = slice(P * (w_tile % 2), P * (w_tile % 2 + 1))
            r_cols = slice(BANK * half, BANK * (half + 1))
            for c in range(first, last):
                nc.tensor.matmul_mx(
                    out=acc[:],
                    lhsT=w_codes[:, a, c, w_cols].bitcast(FP8X4),
                    lhsT_scale=w_scales[:, a, c, w_cols],
                    rhs=a_codes[:, c, r_cols].bitcast(FP8X4),
                    rhs_scale=a_scales[:, c, r_cols],
                    start=(c == 0),
                    stop=(c == passes - 1),
                )

        regroup = whole.enter_context(tc.tile_pool(name="regroup", bufs=RG))
        h_pool = whole.enter_context(tc.tile_pool(name="h_pool", bufs=4))
        w1_raw = whole.enter_context(tc.tile_pool(name="w1_raw", bufs=3))
        w1_grouped = whole.enter_context(tc.tile_pool(name="w1_grouped", bufs=3))
        normed = whole.enter_context(tc.tile_pool(name="normed", bufs=2))
        leaky = whole.enter_context(tc.tile_pool(name="leaky", bufs=2))
        stream = []
        stage_tiles = []
        deferred = []
        pieces = {}
        normed_pairs = []
        leaky_groups = []

        def keep_warm(bank, count):
            for i in range(count):
                nc.tensor.matmul(bank[:], lhsT=zeros[:, 0:P], rhs=zeros[:], start=True, stop=True)

        def transpose_unit(unit, ring="in"):
            pair, c = unit
            bank = take_bank(ring)
            by_word = bank[:].rearrange("p (u n) -> p u n", u=2)
            for i in range(2):
                words = pair[:, i, :].bitcast(F32)
                for u in range(2):
                    first_word = PASS_WORDS * c + P * u
                    nc.tensor.transpose(
                        by_word[:, u, P * i : P * (i + 1)], words[:, first_word : first_word + P], ident[:]
                    )
            return bank

        def new_grouped(n):
            units = len(stream[n][0])
            if n >= LATER:
                grouped = w1_grouped.tile([P, 4 * PAIR * units], BF16, align_bytes=64, tag="later")
            else:
                grouped = regroup.tile([P, 4 * PAIR * units], BF16, align_bytes=64, tag="now%d" % units, bufs=2 + units)
            return grouped

        def group_words(grouped, j, bank, on_vector=False):
            dest = grouped[:, 4 * PAIR * j : 4 * PAIR * (j + 1)].bitcast(F32).rearrange("p (n u) -> p n u", u=2)
            src = bank[:].rearrange("p (u n) -> p n u", u=2)
            if on_vector:
                nc.vector.tensor_copy(out=dest, in_=src)
            else:
                nc.scalar.copy(out=dest, in_=src)

        def quantise_now(n, grouped):
            units, codes, scales = stream[n]
            nc.vector.quantize_mx(out=codes.bitcast(FP8X4), scales=scales, in_=grouped[:])

        def quantise(n, grouped):
            if n >= LATER:
                deferred.append((n, grouped))
            else:
                quantise_now(n, grouped)

        def bring(n, ring="in"):
            grouped = new_grouped(n)
            for j, unit in enumerate(stream[n][0]):
                group_words(grouped, j, transpose_unit(unit, ring))
            quantise(n, grouped)

        def quantise_deferred(count):
            for n, grouped in deferred[:count]:
                quantise_now(n, grouped)
            rest = deferred[count:]
            deferred.clear()
            deferred.extend(rest)

        def matmul_half(tile, half):
            g, t = divmod(tile, GROUP_TILES)
            w0_codes, w0_scales, x_codes, x_scales = stage_tiles[g]
            acc_of[tile, half] = psum_bank(4 + 2 * (tile % 2) + half)
            multiply(acc_of[tile, half], w0_codes, w0_scales, x_codes, x_scales, GROUP_PASSES, 0, GROUP_PASSES, t, half)

        def second_half(q, half, first, last):
            if first == 0:
                acc_of[HIDDEN_TILES + q, half] = psum_bank(OUT_BANKS[q] + half)
            multiply(
                acc_of[HIDDEN_TILES + q, half], w1_codes, w1_scales, h_codes, h_scales, HIDDEN_PASSES,
                first, last, q, half,
            )

        def normalise_hidden(tile, half):
            m, e = divmod(tile, 2)
            normalise(tile, half, normed_pairs[m][:, e, BANK * half : BANK * (half + 1)])

        def leaky_pair(m, rows):
            g, u = divmod(m, 2)
            v = normed_pairs[m][:, :, rows].rearrange("p t n -> p n t")
            nc.vector.scalar_tensor_tensor(
                out=leaky_groups[g][:, u, rows, :], in0=v, scalar=SLOPE, in1=v, op0=ALU.mult, op1=ALU.max,
            )

        def leaky_half(m, half):
            leaky_pair(m, slice(BANK * half, BANK * (half + 1)))

        def regroup_piece(piece, on_scalar=False):
            g, r = divmod(piece, ROWS // PAIR)
            h_grouped = h_pool.tile([P, 4 * PAIR], BF16, align_bytes=64)
            pairs = leaky_groups[g][:].rearrange("p u n e -> p u (n e)").bitcast(F32)
            dest = h_grouped[:].bitcast(F32).rearrange("p (n u) -> p n u", u=2)
            src = pairs[:, :, PAIR * r : PAIR * (r + 1)].rearrange("p u n -> p n u")
            if on_scalar:
                nc.scalar.copy(out=dest, in_=src)
            else:
                nc.vector.tensor_copy(out=dest, in_=src)
            pieces[piece] = h_grouped

        def quantise_piece(piece):
            g, r = divmod(piece, ROWS // PAIR)
            rows = slice(PAIR * r, PAIR * (r + 1))
            nc.vector.quantize_mx(
                out=h_codes[:, g, rows].bitcast(FP8X4), scales=h_scales[:, g, rows], in_=pieces[piece][:]
            )

        with ExitStack() as first:
            raw = first.enter_context(tc.tile_pool(name="raw", bufs=8))
            staged = first.enter_context(tc.tile_pool(name="staged", bufs=2))

            def load_vectors():
                nc.sync.dma_start(out=vec_rows[0:8, :], in_=gamma0.rearrange("(a w) -> a w", w=2 * P))
                nc.sync.dma_start(out=vec_rows[8:16, :], in_=beta0.rearrange("(a w) -> a w", w=2 * P))
                nc.sync.dma_start(out=vec_rows1[0:8, :], in_=gamma1.rearrange("(a w) -> a w", w=P))
                nc.sync.dma_start(out=vec_rows1[8:16, :], in_=beta1.rearrange("(a w) -> a w", w=P))

            def load_stage(stage):
                w0_codes = staged.tile([P, 2, GROUP_PASSES, PAIR], U32, align_bytes=64)
                w0_scales = staged.tile([P, 2, GROUP_PASSES, PAIR], U8, align_bytes=64)
                x_codes = staged.tile([P, GROUP_PASSES, ROWS], U32, align_bytes=64)
                x_scales = staged.tile([P, GROUP_PASSES, ROWS], U8, align_bytes=64)
                stage_tiles.append((w0_codes, w0_scales, x_codes, x_scales))

                def load_w0(a):
                    first_row = GROUP_OUT * stage + PAIR * a
                    w0_pair = raw.tile([P, 2, GROUP_K], BF16, tag="pair")
                    cuts = GROUP_PASSES if (stage == 0 and a == 0) else 1
                    for j in range(cuts):
                        ks = slice(GROUP_K // cuts * j, GROUP_K // cuts * (j + 1))
                        nc.sync.dma_start(
                            out=w0_pair[:, :, ks],
                            in_=w0[first_row : first_row + PAIR, ks].rearrange("(p e) k -> p e k", e=2),
                        )
                    cuts = [(0, 1), (1, 2), (2, 3)] if stage == 0 and a == 0 else [(0, 2), (2, 3)]
                    for c0, c1 in cuts:
                        stream.append(
                            (
                                [(w0_pair, c) for c in range(c0, c1)],
                                w0_codes[:, a, c0:c1, :].rearrange("p c n -> p (c n)"),
                                w0_scales[:, a, c0:c1, :].rearrange("p c n -> p (c n)"),
                            )
                        )

                load_w0(0)
                k0 = GROUP_K * stage
                from_node = max(0, min(NODE_K - k0, GROUP_K))
                x_pairs = []
                for r in range(ROWS // PAIR):
                    rows = slice(PAIR * r, PAIR * (r + 1))
                    x_pair = raw.tile([P, 2, GROUP_K], BF16, tag="pair")
                    if from_node > 0:
                        nc.sync.dma_start(
                            out=x_pair[:, :, 0:from_node],
                            in_=node_rows[rows, k0 : k0 + from_node].rearrange("(i p) k -> p i k", p=P),
                        )
                    if from_node < GROUP_K:
                        nc.sync.dma_start(
                            out=x_pair[:, :, from_node:GROUP_K],
                            in_=aggr_rows[rows, k0 + from_node - NODE_K : k0 + GROUP_K - NODE_K].rearrange(
                                "(i p) k -> p i k", p=P
                            ),
                        )
                    x_pairs.append(x_pair)
                    if stage == 0 and r == 1:
                        load_vectors()
                run = 1 if stage == 0 else 2
                for r in range(0, ROWS // PAIR, run):
                    cols = slice(PAIR * r, PAIR * (r + run))
                    for c in range(GROUP_PASSES):
                        units = [(x_pair, c) for x_pair in x_pairs[r : r + run]]
                        stream.append((units, x_codes[:, c, cols], x_scales[:, c, cols]))
                load_w0(1)

            load_stage(0)
            for stage in range(1, GROUPS):
                load_stage(stage)
            for a in range(OUT_TILES // 2):
                w1_pair = w1_raw.tile([P, 2, HIDDEN], BF16)
                nc.sync.dma_start(
                    out=w1_pair[:], in_=w1[PAIR * a : PAIR * (a + 1), :].rearrange("(i p) k -> p i k", p=P)
                )
                for c in range(0, HIDDEN_PASSES, 2):
                    stream.append(
                        (
                            [(w1_pair, c), (w1_pair, c + 1)],
                            w1_codes[:, a, c : c + 2, :].rearrange("p c n -> p (c n)"),
                            w1_scales[:, a, c : c + 2, :].rearrange("p c n -> p (c n)"),
                        )
                    )
            for m in range(HIDDEN_TILES // 2):
                v = normed.tile([P, 2, ROWS], F32)
                normed_pairs.append(v)
            for g in range(GROUPS):
                w = leaky.tile([P, 2, ROWS, 2], BF16, align_bytes=64)
                leaky_groups.append(w)

            def spread_vectors():
                vec_bank = take_bank("in")
                nc.tensor.transpose(vec_bank[:, 0:P], vec_rows[:].bitcast(F32), ident[:])
                nc.tensor.transpose(vec_bank[:, P : 2 * P], vec_words1[:], ident[:])
                nc.vector.tensor_copy(out=vec_cols[:].bitcast(F32), in_=vec_bank[:, 0:P])
                nc.vector.memset(zero_shift[:], 0.0)
                nc.vector.tensor_copy(out=gain_mean[:, HIDDEN_TILES:n_tiles, 0], in_=vec_bank[:, P : P + OUT_TILES])
                nc.vector.tensor_copy(
                    out=zero_shift[:, HIDDEN_TILES:n_tiles, 1], in_=vec_bank[:, P + OUT_TILES : P + 2 * OUT_TILES]
                )
                nc.vector.tensor_copy(out=gain_mean[:, 0:HIDDEN_TILES, 0], in_=vec_cols[:, 0:HIDDEN_TILES])
                nc.vector.tensor_copy(
                    out=zero_shift[:, 0:HIDDEN_TILES, 1], in_=vec_cols[:, HIDDEN_TILES : 2 * HIDDEN_TILES]
                )
                nc.vector.tensor_scalar(
                    out=minus_gain[:], in0=gain_mean[:, :, 0], scalar1=-1.0, scalar2=None, op0=ALU.mult
                )

            idle_bank = psum_bank(7)
            keep_warm(idle_bank, WARM_FIRST)
            for n in range(HEAD_UNITS):
                grouped = new_grouped(n)
                bank = transpose_unit(stream[n][0][0])
                if n in WARM_AFTER:
                    keep_warm(idle_bank, WARM)
                if n == HEAD_MM:
                    matmul_half(0, 0)
                if n == HEAD_MM + HEAD_D:
                    matmul_half(1, 0)
                group_words(grouped, 0, bank)
                quantise(n, grouped)
                if n == HEAD_ST:
                    half_statistics(0, 0)
                if n == HEAD_ST + HEAD_D:
                    half_statistics(1, 0)
                if n == 8:
                    nc.vector.tensor_copy(out=vec_words1[:], in_=vec_rows1[:])
                if n == 11:
                    spread_vectors()
            pending = []
            carry = []
            following = HEAD_UNITS
            for r in range(HIDDEN_TILES):
                items = list(range(following, following + ITEMS[r]))
                following += ITEMS[r]
                todo = PIECES.get(r, [])
                units = [(n, j, unit) for n in items for j, unit in enumerate(stream[n][0])]
                grouped = {}
                for n in items:
                    g = new_grouped(n)
                    grouped[n] = g
                for m, half in LEAKY.get(r, []):
                    leaky_half(m, half)
                for n, g in carry:
                    quantise(n, g)
                banks = [transpose_unit(unit) for n, j, unit in units[:SPLIT]]
                if r >= 2:
                    matmul_half(r, 0)
                banks += [transpose_unit(unit) for n, j, unit in units[SPLIT:]]
                for i, (n, j, unit) in enumerate(units[:COPIES_FIRST]):
                    group_words(grouped[n], j, banks[i], i in VECTOR_COPIES.get(r, []))
                    if i == ARS_AFTER:
                        for tile in pending:
                            inverse_deviation(tile)
                if not units:
                    for tile in pending:
                        inverse_deviation(tile)
                for tile in pending:
                    scale_and_bias(tile)
                for n in items[:1]:
                    quantise(n, grouped[n])
                matmul_half(r, 1)
                for i, (n, j, unit) in list(enumerate(units))[COPIES_FIRST:]:
                    group_words(grouped[n], j, banks[i], i in VECTOR_COPIES.get(r, []))
                for p in todo:
                    regroup_piece(p, p in SCALAR_PIECES)
                if r >= 2:
                    half_statistics(r, 0)
                if todo:
                    for n in items[1:-1]:
                        quantise(n, grouped[n])
                for tile in pending:
                    normalise_hidden(tile, 0)
                    normalise_hidden(tile, 1)
                half_statistics(r, 1)
                if not todo:
                    for n in items[1:-1]:
                        quantise(n, grouped[n])
                for p in todo[:1]:
                    quantise_piece(p)
                carry = [(n, grouped[n]) for n in items[1:][-1:]]
                pending = [r]
                mean_and_variance(r)
            for n, g in carry:
                quantise(n, g)

            rest = list(range(following, len(stream)))

            inverse_deviation(15)
            quantise_piece(11)
            scale_and_bias(15)
            second_half(1, 0, 0, 3)
            second_half(0, 0, 0, 3)
            second_half(1, 1, 0, 3)
            second_half(0, 1, 0, 3)
            normalise_hidden(15, 0)
            normalise_hidden(15, 1)
            leaky_half(6, 1)
            late = new_grouped(rest[0])
            banks = [transpose_unit(unit, "late") for unit in stream[rest[0]][0]]

        with ExitStack() as second:
            work = second.enter_context(tc.tile_pool(name="work", bufs=3))
            done = second.enter_context(tc.tile_pool(name="done", bufs=4))
            stores = second.enter_context(tc.tile_pool(name="stores", bufs=6))
            v1s = {}
            o1s = {}
            back = {}
            rows_outs = {}

            def leaky_out(q, half):
                if half == 0:
                    o1 = done.tile([P, ROWS], F32)
                    o1s[q] = o1
                r_cols = slice(BANK * half, BANK * (half + 1))
                nc.vector.scalar_tensor_tensor(
                    out=o1s[q][:, r_cols], in0=v1s[q][:, r_cols], scalar=SLOPE, in1=v1s[q][:, r_cols],
                    op0=ALU.mult, op1=ALU.max,
                )

            def transpose_back(q, half, ring):
                bank = take_bank(ring)
                view = bank[:].rearrange("p (i c) -> p i c", c=P)
                for i in range(BANK // P):
                    first_row = BANK * half + P * i
                    nc.tensor.transpose(view[:, i, :], o1s[q][:, first_row : first_row + P], ident[:])
                back[q, half] = bank

            def store(q, half, on_vector=False):
                if q % 2 == 0:
                    rows_out = stores.tile([P, BANK // P, 2 * P], F32)
                    rows_outs[half] = rows_out
                dest = rows_outs[half][:, :, P * (q % 2) : P * (q % 2 + 1)]
                src = back[q, half][:].rearrange("p (i c) -> p i c", c=P)
                if on_vector:
                    nc.vector.tensor_copy(out=dest, in_=src)
                else:
                    nc.scalar.copy(out=dest, in_=src)
                if q % 2 == 1:
                    nc.sync.dma_start(
                        out=out_rows[BANK * half : BANK * (half + 1), P * (q - 1) : P * (q + 1)].rearrange(
                            "(i p) c -> p i c", p=P
                        ),
                        in_=rows_outs[half][:],
                    )

            def normalise_out(q, half, on_vector=False):
                if half == 0:
                    v1 = work.tile([P, ROWS], F32)
                    v1s[q] = v1
                dest = v1s[q][:, BANK * half : BANK * (half + 1)]
                if on_vector:
                    scale_bias = scale_bias_of[HIDDEN_TILES + q]
                    nc.vector.tensor_scalar(
                        out=dest, in0=acc_of[HIDDEN_TILES + q, half][:], scalar1=scale_bias[:, 0:1],
                        scalar2=scale_bias[:, 1:2], op0=ALU.mult, op1=ALU.add,
                    )
                else:
                    normalise(HIDDEN_TILES + q, half, dest)

            T1 = HIDDEN_TILES
            second_half(2, 0, 0, 3)
            second_half(2, 1, 0, 3)
            for r in range(4):
                leaky_pair(7, slice(PAIR * r, PAIR * (r + 1)))
                regroup_piece(12 + r, True)
                if r == 3:
                    for j, bank in enumerate(banks):
                        group_words(late, j, bank)
                    quantise(rest[0], late)
            for r in range(3):
                quantise_piece(12 + r)
            for q in range(3):
                second_half(q, 0, 3, 4)
            quantise_piece(15)
            half_statistics(T1, 0)
            for q in range(3):
                second_half(q, 1, 3, 4)
            bring(rest[1], "late")
            half_statistics(T1 + 1, 0)
            half_statistics(T1, 1)
            half_statistics(T1 + 1, 1)
            mean_and_variance(T1)
            mean_and_variance(T1 + 1)
            inverse_deviation(T1)
            inverse_deviation(T1 + 1)
            half_statistics(T1 + 2, 0)
            scale_and_bias(T1)
            scale_and_bias(T1 + 1)
            normalise_out(0, 0)
            normalise_out(0, 1)
            normalise_out(1, 0)
            late = new_grouped(rest[2])
            banks = [transpose_unit(unit, "late") for unit in stream[rest[2]][0]]
            half_statistics(T1 + 2, 1)
            quantise_deferred(1)
            mean_and_variance(T1 + 2)
            inverse_deviation(T1 + 2)
            normalise_out(1, 1)
            leaky_out(0, 0)
            scale_and_bias(T1 + 2)
            normalise_out(2, 0)
            normalise_out(2, 1)
            for j, bank in enumerate(banks):
                group_words(late, j, bank)
            quantise(rest[2], late)
            for q in range(3, OUT_TILES):
                leaky_out(*BACK[q][0])
                second_half(q, 0, 0, 4)
                if q == 3:
                    quantise_deferred(1)
                if q > 3:
                    scale_and_bias(T1 + q - 1)
                half_statistics(T1 + q, 0)
                if q > 3:
                    normalise_out(q - 1, 0)
                    normalise_out(q - 1, 1)
                second_half(q, 1, 0, 4)
                leaky_out(*BACK[q][1])
                half_statistics(T1 + q, 1)
                quantise_deferred({3: 0, 4: 1, 5: 1, 6: 0, 7: 0}[q])
                for piece in BACK[q][2:]:
                    leaky_out(*piece)
                for piece in TB[q]:
                    transpose_back(*piece, "out")
                for piece in TB[q][:-1]:
                    store(*piece)
                mean_and_variance(T1 + q)
                inverse_deviation(T1 + q)
                store(*TB[q][-1])
                if q == 4:
                    for n in rest[3:]:
                        bring(n, "out")
            leaky_out(6, 0)
            scale_and_bias(T1 + 7)
            leaky_out(6, 1)
            for piece in TB[8]:
                transpose_back(*piece, "tail")
            normalise_out(7, 0)
            normalise_out(7, 1, True)
            leaky_out(7, 0)
            transpose_back(7, 0, "tail")
            leaky_out(7, 1)
            transpose_back(7, 1, "tail")
            for piece in TB[8]:
                store(*piece)
            store(7, 0)
            store(7, 1, True)
